import numpy as np
import ml_dtypes


def mxq(x, axis, fmt="e4m3"):
    dtype, down = {"e4m3": (ml_dtypes.float8_e4m3fn, 7), "e5m2": (ml_dtypes.float8_e5m2, 14)}[fmt]
    v = np.moveaxis(np.asarray(x, np.float32).astype(ml_dtypes.bfloat16).astype(np.float64), axis, -1)
    blocks = v.reshape(v.shape[:-1] + (-1, 32))
    amax = np.abs(blocks).max(-1, keepdims=True)
    byte = np.maximum(np.where(amax > 0, np.frexp(amax)[1] - 1 + 127, 0) - down, 1)
    scale = np.exp2(byte - 127.0)
    codes = (blocks / scale).astype(np.float32).astype(dtype).astype(np.float64)
    return np.moveaxis((codes * scale).reshape(v.shape), -1, axis)


WIDE = False


def mx_kscale(k):
    if not WIDE:
        return np.ones(k)
    levels = np.array([20, -20, 10, -10, 0])
    a = np.random.permutation(np.resize(levels, k // 512 * 4)).reshape(k // 512, 4)
    idx = np.arange(k)
    return np.exp2(a[idx // 512, idx % 128 // 32])


BF16 = ml_dtypes.bfloat16


def bf(x):
    return np.asarray(x, np.float32).astype(BF16)


def f64(x):
    return np.asarray(x).astype(np.float64)


B, K, N, T = 1024, 1024, 1024, 8
EPS = 1e-7
MAX_NORM = 1.0 - 1e-5


def _sum(x):
    return np.sum(x, axis=-1, keepdims=True)


def _n(x):
    return np.maximum(np.sqrt(_sum(x * x)), EPS)


def _artanh(x):
    c = np.clip(x, -1.0 + 1e-5, 1.0 - 1e-5)
    return 0.5 * np.log((1.0 + c) / (1.0 - c))


def _radial(a, k):
    r = _n(a)
    return np.tanh(k * r) * a / r


def _radial_bwd(a, k, g):
    r = _n(a)
    h = np.tanh(k * r)
    free = np.sqrt(_sum(a * a)) > EPS
    coef = np.where(free, (k * (1.0 - h * h) * r - h) / r ** 3, 0.0)
    return h / r * g + coef * _sum(g * a) * a


def _project(x):
    n = _n(x)
    return x * np.where(n > MAX_NORM, MAX_NORM / n, 1.0)


def _project_bwd(a, g):
    r = _n(a)
    on = r > MAX_NORM
    return g * np.where(on, MAX_NORM / r, 1.0) - np.where(on, MAX_NORM * _sum(g * a) / r ** 3, 0.0) * a


def _mobius_add(x, y):
    x2 = _sum(x * x)
    y2 = _sum(y * y)
    xy = _sum(x * y)
    num = (1.0 + 2.0 * xy + y2) * x + (1.0 - x2) * y
    den = np.maximum(1.0 + 2.0 * xy + x2 * y2, EPS)
    return num / den


def _mobius_add_bwd(x, y, g, wrt):
    x2 = _sum(x * x)
    y2 = _sum(y * y)
    xy = _sum(x * y)
    den0 = 1.0 + 2.0 * xy + x2 * y2
    den = np.maximum(den0, EPS)
    o = ((1.0 + 2.0 * xy + y2) * x + (1.0 - x2) * y) / den
    gn = g / den
    dA = _sum(gn * x)
    dB = _sum(gn * y)
    dD = np.where(den0 > EPS, -_sum(gn * o), 0.0)
    if wrt == 'x':
        return (1.0 + 2.0 * xy + y2) * gn + 2.0 * (dA + dD) * y + 2.0 * (dD * y2 - dB) * x
    return (1.0 - x2) * gn + 2.0 * (dA + dD) * x + 2.0 * (dA + dD * x2) * y


def setup_inputs():
    s = mx_kscale(B)
    m = np.random.standard_normal(K)
    w0 = np.random.standard_normal((N, K)) * 1.5 / np.sqrt(N)
    u = w0 @ m
    u = u / _n(u)
    v = np.random.standard_normal((B, K)) + m
    vi0 = bf(0.7 * v / (1.0 + _n(v)))
    z0 = np.random.standard_normal((B, N)) + np.random.standard_normal((B, 1)) * np.sqrt(N) * u
    z0 = bf(0.5 * z0 / (1.0 + _n(z0)))
    b = bf(0.45 * (0.7 * u + 0.7 * np.random.standard_normal(N) / np.sqrt(N)))
    step_sizes = bf(np.log(2.0 / T) + 0.1 * np.random.standard_normal(1))
    W = bf(w0)
    g = np.random.standard_normal((B, T, N)) + np.random.standard_normal((B, T, 1)) * np.sqrt(N) * u
    g = g * np.exp2(np.random.randint(-12, 1, (B, 1, 1))) * 4.0 / s[:, None, None]
    mv = f64(vi0) @ f64(W).T
    vn = _n(f64(vi0))
    return {'z_0': z0, 'v_init': bf(f64(vi0) * s[:, None]), 'W': W, 'b': b, 'step_sizes': step_sizes,
            'mv': np.asarray(mv, np.float32), 'vn': np.asarray(vn, np.float32), 'grad_out': bf(g)}


def reference(z_0, v_init, W, b, step_sizes, mv, vn, grad_out):
    z_0, b, step_sizes, mv, vn, g = f64(z_0), f64(b), f64(step_sizes), f64(mv), f64(vn), f64(grad_out)
    step = 1.0 / (1.0 + np.exp(-step_sizes))
    k1 = _artanh(vn) / vn
    res = _radial(mv, k1)
    b_pt = _radial(b, 1.0)
    p = _mobius_add(res, b_pt)
    v0 = _project(p)
    c = (step * np.arange(1.0, T + 1.0))[None, :, None]
    v_t = c * v0[:, None, :]
    x = z_0[:, None, :]
    k2 = 1.0 / np.maximum(1.0 - _sum(x * x), EPS)
    sec = _radial(v_t, k2)
    q = _mobius_add(x, sec)
    dq = _project_bwd(q, g)
    ds = _mobius_add_bwd(x, sec, dq, 'y')
    dv_t = _radial_bwd(v_t, k2, ds)
    dv0 = np.sum(c * dv_t, axis=1)
    dp = _project_bwd(p, dv0)
    dres = _mobius_add_bwd(res, b_pt, dp, 'x')
    dmv = _radial_bwd(mv, k1, dres)
    return mxq(dmv, 0, 'e5m2').T @ mxq(f64(v_init), 0, 'e4m3')

@@ -1,0 +1,509 @@
+from contextlib import ExitStack
+
+import concourse.masks as masks
+import concourse.mybir as mybir
+
+F32 = mybir.dt.float32
+BF16 = mybir.dt.bfloat16
+U32 = mybir.dt.uint32
+U8 = mybir.dt.uint8
+E4M3_X4 = mybir.dt.float8_e4m3fn_x4
+E5M2_X4 = mybir.dt.float8_e5m2_x4
+ACT = mybir.ActivationFunctionType
+MUL = mybir.AluOpType.mult
+ADD = mybir.AluOpType.add
+SUB = mybir.AluOpType.subtract
+
+P = 128
+ROWS = 1024
+N = 1024
+K = 1024
+T = 8
+PACK = 4
+PASSES = ROWS // (P * PACK)
+TILES = PASSES * PACK
+BANK = 512
+HALVES = N // BANK
+BLOCKS = N // P
+BLOCKS_PER_BANK = BANK // P
+
+EPS = 1e-7
+EPS_SQ = EPS * EPS
+TINY = 1e-30
+MAX_NORM = 1.0 - 1e-5
+CLIP = 1.0 - 1e-5
+
+FLOPS = 2 * ROWS * N * K
+BYTES = 2 * (2 * ROWS * N + ROWS * T * N + N + 1) + 4 * (ROWS * N + ROWS) + 4 * N * K
+
+
+def tile_paralleldirectpoincaredynamics_v_kernel(
+    tc, z_0, v_init, W, b, step_sizes, mv, vn, grad_out, out
+):
+    nc = tc.nc
+    with ExitStack() as ctx:
+        keep = ctx.enter_context(tc.tile_pool(name="keep", bufs=1))
+        grads = ctx.enter_context(tc.tile_pool(name="grads", bufs=3))
+        unread = ctx.enter_context(tc.tile_pool(name="unread", bufs=4))
+        stage = ctx.enter_context(tc.tile_pool(name="stage", bufs=2))
+        psum = ctx.enter_context(tc.psum_pool(name="psum", bufs=8))
+
+        x_all = keep.tile([P, TILES, N], BF16, name="x_all")
+        v0_all = keep.tile([P, TILES, N], F32, name="v0_all")
+        b_all = keep.tile([P, N], BF16, name="b_all")
+        vn_row = keep.tile([P, TILES], F32, name="vn_row")
+        logit = keep.tile([P, 1], BF16, name="logit")
+        z_view = z_0.rearrange("(c p j) n -> c p (j n)", c=PASSES, p=P, j=PACK)
+        mv_view = mv.rearrange("(c p j) n -> c p (j n)", c=PASSES, p=P, j=PACK)
+        v_view = v_init.rearrange("(c p j) k -> c p (j k)", c=PASSES, p=P, j=PACK)
+        g_view = grad_out.rearrange("(c p j) t n -> c j p (t n)", c=PASSES, p=P, j=PACK)
+
+        nc.sync.dma_start(out=b_all[:], in_=b.partition_broadcast(P))
+        for c in range(PASSES):
+            of_pass = slice(c * PACK, (c + 1) * PACK)
+            nc.sync.dma_start(
+                out=v0_all[:, of_pass, :].rearrange("p j n -> p (j n)"), in_=mv_view[c]
+            )
+            nc.sync.dma_start(
+                out=x_all[:, of_pass, :].rearrange("p j n -> p (j n)"), in_=z_view[c]
+            )
+        with nc.allow_non_contiguous_dma(reason="one float32 a row: runs of 4 values"):
+            nc.sync.dma_start(
+                out=vn_row[:].rearrange("p (c j) -> p c j", c=PASSES),
+                in_=vn.rearrange("(c p j) o -> p c (j o)", c=PASSES, p=P, j=PACK),
+            )
+            nc.sync.dma_start(out=logit[:], in_=step_sizes.partition_broadcast(P))
+
+        identity = keep.tile([P, P], F32, name="identity")
+        masks.make_identity(nc, identity[:])
+        horizon = keep.tile([P, T], F32, name="horizon")
+        for t in range(T):
+            nc.vector.memset(horizon[:, t : t + 1], float(t + 1))
+
+        def mul(dst, a, b_):
+            nc.vector.tensor_tensor(out=dst, in0=a, in1=b_, op=MUL)
+            return dst
+
+        def add(dst, a, b_):
+            nc.vector.tensor_tensor(out=dst, in0=a, in1=b_, op=ADD)
+            return dst
+
+        def sub(dst, a, b_):
+            nc.vector.tensor_tensor(out=dst, in0=a, in1=b_, op=SUB)
+            return dst
+
+        def fused(dst, a, scalar, b_, op0, op1):
+            nc.vector.scalar_tensor_tensor(out=dst, in0=a, scalar=scalar, in1=b_, op0=op0, op1=op1)
+            return dst
+
+        def scale(dst, a, s):
+            nc.vector.tensor_scalar(out=dst, in0=a, scalar1=s, scalar2=None, op0=MUL)
+            return dst
+
+        def shift(dst, a, s):
+            nc.vector.tensor_scalar(out=dst, in0=a, scalar1=s, scalar2=None, op0=ADD)
+            return dst
+
+        def affine(dst, a, s, offset):
+            nc.vector.tensor_scalar(out=dst, in0=a, scalar1=s, scalar2=offset, op0=MUL, op1=ADD)
+            return dst
+
+        def at_least(dst, a, low):
+            nc.vector.tensor_scalar(
+                out=dst, in0=a, scalar1=low, scalar2=None, op0=mybir.AluOpType.max
+            )
+            return dst
+
+        def above(dst, a, bound):
+            nc.vector.tensor_scalar(
+                out=dst, in0=a, scalar1=bound, scalar2=None, op0=mybir.AluOpType.is_gt
+            )
+            return dst
+
+        def inverse(dst, a):
+            nc.vector.reciprocal(out=dst, in_=a)
+            return dst
+
+        def table(dst, a, func, s=1.0):
+            nc.scalar.activation(out=dst, in_=a, func=func, scale=s)
+            return dst
+
+        def dot(acc, a, b_, width):
+            products = unread.tile([P, N], F32, name="products")
+            nc.vector.scalar_tensor_tensor(
+                out=products[:, :width], in0=a, scalar=1.0, in1=b_, op0=MUL, op1=MUL, accum_out=acc
+            )
+
+        def square_sum(acc, a):
+            squares = unread.tile([P, N], BF16, name="squares")
+            nc.scalar.activation(out=squares[:], in_=a, func=ACT.Square, accum_out=acc)
+
+        def quantise_pass(rows, codes, scales, packed_dtype):
+            grouped = stage.tile([P, N, PACK], BF16, name="grouped", align_bytes=64)
+            nc.scalar.copy(out=grouped[:], in_=rows.rearrange("p j n -> p n j"))
+            nc.vector.quantize_mx(
+                out=codes.bitcast(packed_dtype),
+                scales=scales,
+                in_=grouped[:].rearrange("p n j -> p (n j)"),
+            )
+
+        v_codes = keep.tile([P, PASSES, K], U32, name="v_codes", align_bytes=64)
+        v_scales = keep.tile([P, PASSES, K], U8, name="v_scales", align_bytes=64)
+        d_codes = keep.tile([P, PASSES, N], U32, name="d_codes", align_bytes=64)
+        d_scales = keep.tile([P, PASSES, N], U8, name="d_scales", align_bytes=64)
+
+        a_scaled = keep.tile([P, TILES, T], F32, name="a_scaled")
+        from_dots = keep.tile([P, 3, 2, TILES, T], F32, name="from_dots")
+        to_kappa = keep.tile([P, TILES, 3, 5], F32, name="to_kappa")
+        dots = keep.tile([P, TILES, 2, T], F32, name="dots")
+        inputs = keep.tile([P, TILES, 5], F32, name="inputs")
+        kappa = keep.tile([P, TILES, 3], F32, name="kappa")
+
+        with tc.tile_pool(name="chain", bufs=1) as chain:
+
+            def col(name):
+                return chain.tile([P, 1], F32, name=name)
+
+            def row(name):
+                return chain.tile([P, TILES], F32, name=name)
+
+            def row2(name):
+                return chain.tile([P, 2, TILES], F32, name=name)
+
+            def grid(name):
+                return chain.tile([P, TILES, T], F32, name=name)
+
+            def grid2(name):
+                return chain.tile([P, 2, TILES, T], F32, name=name)
+
+            def pair(r):
+                return r.unsqueeze(1).to_broadcast([P, 2, TILES])
+
+            def over_t(r):
+                return r.unsqueeze(2).to_broadcast([P, TILES, T])
+
+            def over_tiles(h):
+                return h.unsqueeze(1).to_broadcast([P, TILES, T])
+
+            def both(g):
+                return g.unsqueeze(1).to_broadcast([P, 2, TILES, T])
+
+            def both_over_t(r):
+                return r.unsqueeze(1).unsqueeze(3).to_broadcast([P, 2, TILES, T])
+
+            def projection(make, tag, norm_sq):
+                r = table(make(tag + "_r"), at_least(make(tag + "_c"), norm_sq, EPS_SQ), ACT.Sqrt)
+                on = above(make(tag + "_on"), r, MAX_NORM)
+                ir = inverse(make(tag + "_ir"), r)
+                excess = mul(make(tag + "_ex"), affine(make(tag + "_sc"), ir, MAX_NORM, -1.0), on)
+                pi = affine(make(tag + "_pi"), excess, 1.0, 1.0)
+                ir3 = mul(make(tag + "_ir3"), mul(make(tag + "_ir2"), ir, ir), ir)
+                phi = fused(make(tag + "_phi"), ir3, MAX_NORM, on, MUL, MUL)
+                return pi, phi
+
+            def radial_coefficient(make, tag, h, kr, ir, free):
+                slope = affine(make(tag + "_sl"), mul(make(tag + "_h2"), h, h), -1.0, 1.0)
+                top = sub(make(tag + "_top"), mul(make(tag + "_skr"), slope, kr), h)
+                ir3 = mul(make(tag + "_jr3"), mul(make(tag + "_jr2"), ir, ir), ir)
+                return mul(make(tag + "_cf"), mul(make(tag + "_q"), top, ir3), free)
+
+            bb = col("bb")
+            m2, mb, x2, xb = row("m2"), row("mb"), row("x2"), row("xb")
+            square_sum(bb[:], b_all[:])
+            for i in range(TILES):
+                square_sum(m2[:, i : i + 1], v0_all[:, i, :])
+                square_sum(x2[:, i : i + 1], x_all[:, i, :])
+                dot(mb[:, i : i + 1], v0_all[:, i, :], b_all[:], N)
+                dot(xb[:, i : i + 1], x_all[:, i, :], b_all[:], N)
+
+            rb = table(col("rb"), at_least(col("bb_c"), bb, EPS_SQ), ACT.Sqrt)
+            beta = mul(col("beta"), table(col("hb"), rb, ACT.Tanh), inverse(col("irb"), rb))
+            beta2 = scale(col("beta2"), beta, 2.0)
+            y2 = mul(col("y2"), mul(col("beta_bb"), beta, bb), beta)
+
+            clipped = row("clipped")
+            nc.vector.tensor_scalar(
+                out=clipped,
+                in0=vn_row,
+                scalar1=-CLIP,
+                scalar2=CLIP,
+                op0=mybir.AluOpType.max,
+                op1=mybir.AluOpType.min,
+            )
+            ratio = mul(
+                row("ratio"),
+                affine(row("one_plus"), clipped, 1.0, 1.0),
+                inverse(row("inv_one_minus"), affine(row("one_minus"), clipped, -1.0, 1.0)),
+            )
+            k1 = fused(
+                row("k1"), table(row("ln_ratio"), ratio, ACT.Ln), 0.5, inverse(row("ivn"), vn_row), MUL, MUL
+            )
+
+            rm = table(row("rm"), at_least(row("m2_c"), m2, EPS_SQ), ACT.Sqrt)
+            k1_rm = mul(row("k1_rm"), k1, rm)
+            hm = table(row("hm"), k1_rm, ACT.Tanh)
+            irm = inverse(row("irm"), rm)
+            alpha = mul(row("alpha"), hm, irm)
+            alpha_m2 = mul(row("alpha_m2"), alpha, m2)
+            res2 = mul(row("res2"), alpha_m2, alpha)
+            res_b = scale(row("res_b"), mul(row("alpha_mb"), alpha, mb), beta)
+
+            base = affine(row("base"), res_b, 2.0, 1.0)
+            den0 = fused(row("den0"), res2, y2, base, MUL, ADD)
+            iden = inverse(row("iden"), at_least(row("den"), den0, EPS))
+            p1 = mul(row("p1"), shift(row("a1"), base, y2), iden)
+            p2 = mul(row("p2"), affine(row("a2"), res2, -1.0, 1.0), iden)
+            p_dir = row2("p_dir")
+            pa = mul(p_dir[:, 0, :], p1, alpha)
+            pb = scale(p_dir[:, 1, :], p2, beta)
+            p_mv = add(row("p_mv"), mul(row("pa_m2"), pa, m2), mul(row("pb_mb"), pb, mb))
+            p_b = fused(row("p_b"), pb, bb, mul(row("pa_mb"), pa, mb), MUL, ADD)
+            pp = add(row("pp"), mul(row("pa_pmv"), pa, p_mv), mul(row("pb_pb"), pb, p_b))
+            pi, phi = projection(row, "p", pp)
+
+            mu = mul(row("mu"), pi, pa)
+            nu = mul(row("nu"), pi, pb)
+            vv, xv = row("vv"), row("xv")
+            for i in range(TILES):
+                v0 = v0_all[:, i, :]
+                nc.scalar.activation(out=v0, in_=v0, func=ACT.Copy, scale=mu[:, i : i + 1])
+                fused(v0, b_all[:], nu[:, i : i + 1], v0, MUL, ADD)
+                square_sum(vv[:, i : i + 1], v0)
+                dot(xv[:, i : i + 1], x_all[:, i, :], v0, N)
+            vb = add(row("vb"), mul(row("mu_mb"), mu, mb), scale(row("nu_bb"), nu, bb))
+
+            dp_mv = mul(row2("dp_mv"), p_dir, pair(fused(row("n_phi_pmv"), phi, -1.0, p_mv, MUL, MUL)))
+            add(dp_mv[:, 0, :], dp_mv[:, 0, :], pi)
+            dp_b = mul(row2("dp_b"), p_dir, pair(fused(row("n_phi_pb"), phi, -1.0, p_b, MUL, MUL)))
+            add(dp_b[:, 1, :], dp_b[:, 1, :], pi)
+            dp_p = mul(row2("dp_p"), p_dir, pair(sub(row("pi_phi_pp"), pi, mul(row("phi_pp"), phi, pp))))
+            d_a = mul(row2("d_a"), dp_mv, pair(mul(row("iden_alpha"), iden, alpha)))
+            d_b = mul(row2("d_b"), dp_b, pair(scale(row("iden_beta"), iden, beta)))
+            live = fused(row("n_live_iden"), above(row("live"), den0, EPS), -1.0, iden, MUL, MUL)
+            d_d = mul(row2("d_d"), dp_p, pair(live))
+            to_b = add(row2("to_b"), d_a, d_d)
+            to_res = fused(row2("to_res"), d_d, y2, d_b, MUL, SUB)
+            dres_mv = add(
+                row2("dres_mv"),
+                add(
+                    row2("dres_mv2"),
+                    mul(row2("dres_mv_a"), dp_mv, pair(p1)),
+                    mul(row2("dres_mv_b"), to_b, pair(scale(row("beta2_mb"), mb, beta2))),
+                ),
+                mul(row2("dres_mv_c"), to_res, pair(scale(row("alpha_m2_2"), alpha_m2, 2.0))),
+            )
+            coef_m = radial_coefficient(row, "m", hm, k1_rm, irm, above(row("free_m"), m2, EPS_SQ))
+            lost = mul(row("lost"), pa, phi)
+            on_both = chain.tile([P, 2, 2, TILES], F32, name="on_both")
+            sub(
+                on_both[:, 0],
+                add(
+                    row2("on_mv2"),
+                    mul(row2("on_mv_a"), to_res, pair(fused(row("alpha_sq2"), alpha, 2.0, alpha, MUL, MUL))),
+                    mul(row2("on_mv_b"), dres_mv, pair(coef_m)),
+                ),
+                mul(row2("on_mv_c"), p_dir, pair(mul(row("lost_pa"), lost, pa))),
+            )
+            sub(
+                on_both[:, 1],
+                mul(row2("on_b_a"), to_b, pair(scale(row("alpha_beta2"), alpha, beta2))),
+                mul(row2("on_b_c"), p_dir, pair(mul(row("lost_pb"), lost, pb))),
+            )
+            imu = inverse(row("imu"), mu)
+            in_v0_b = chain.tile([P, 2, 2, TILES], F32, name="in_v0_b")
+            mul(in_v0_b[:, :, 0, :], on_both[:, :, 0, :], pair(imu))
+            sub(in_v0_b[:, :, 1, :], on_both[:, :, 1, :], mul(row2("nu_first"), in_v0_b[:, :, 0, :], pair(nu)))
+            weights = chain.tile([P, 2, 2, TILES], F32, name="weights")
+            mul(weights[:, 0], in_v0_b[:, 0], pair(imu))
+            sub(weights[:, 1], in_v0_b[:, 1], mul(row2("nu_on_v0"), weights[:, 0], pair(nu)))
+            nc.vector.memset(to_kappa[:], 0.0)
+            nc.vector.tensor_copy(out=to_kappa[:, :, 0, 0], in_=mu)
+
+            def kappa_column(m):
+                return to_kappa[:, :, 1:3, m].rearrange("p i k -> p k i")
+
+            w_v0, w_b = weights[:, :, 0, :], weights[:, :, 1, :]
+            add(kappa_column(0), mul(row2("kx_a"), w_v0, pair(xv)), mul(row2("kx_b"), w_b, pair(xb)))
+            add(kappa_column(1), mul(row2("kv_a"), w_v0, pair(vv)), mul(row2("kv_b"), w_b, pair(vb)))
+            add(to_kappa[:, :, 1, 1], to_kappa[:, :, 1, 1], mu)
+            nc.vector.tensor_copy(out=kappa_column(2), in_=w_v0)
+            mul(kappa_column(3), w_b, pair(imu))
+            mul(kappa_column(4), w_b, pair(imu))
+
+            step = affine(col("step"), table(col("half_tanh"), logit, ACT.Tanh, 0.5), 0.5, 0.5)
+            ct = scale(chain.tile([P, T], F32, name="ct"), horizon, step)
+            ct3 = mul(chain.tile([P, T], F32, name="ct3"), mul(chain.tile([P, T], F32, name="ct2"), ct, ct), ct)
+            gap = affine(row("gap"), x2, -1.0, 1.0)
+            k2 = inverse(row("k2"), at_least(row("gap_c"), gap, EPS))
+            r0 = table(row("r0"), at_least(row("vv_c"), vv, TINY), ACT.Sqrt)
+            c_r0 = mul(grid("c_r0"), over_t(r0), over_tiles(ct))
+            rt = at_least(grid("rt"), c_r0, EPS)
+            k2_rt = mul(grid("k2_rt"), rt, over_t(k2))
+            ht = table(grid("ht"), k2_rt, ACT.Tanh)
+            irt = inverse(grid("irt"), rt)
+            s = mul(grid("s"), mul(grid("sigma"), ht, irt), over_tiles(ct))
+            x_sec = mul(grid("x_sec"), s, over_t(xv))
+            sec2 = mul(grid("sec2"), mul(grid("s_vv"), s, over_t(vv)), s)
+            base_t = affine(grid("base_t"), x_sec, 2.0, 1.0)
+            den0_t = add(grid("den0_t"), mul(grid("x2_sec2"), sec2, over_t(x2)), base_t)
+            iden_t = inverse(grid("iden_t"), at_least(grid("den_t"), den0_t, EPS))
+            q_dir = grid2("q_dir")
+            q1 = mul(q_dir[:, 0], add(grid("b1"), base_t, sec2), iden_t)
+            q2 = mul(grid("q2"), iden_t, over_t(gap))
+            q2s = mul(q_dir[:, 1], q2, s)
+            q_x = add(grid("q_x"), mul(grid("q1_x2"), q1, over_t(x2)), mul(grid("q2_xsec"), q2, x_sec))
+            q_v = add(grid("q_v"), mul(grid("q1_xv"), q1, over_t(xv)), mul(grid("q2s_vv"), q2s, over_t(vv)))
+            qq = add(grid("qq"), mul(grid("q1_qx"), q1, q_x), mul(grid("q2s_qv"), q2s, q_v))
+            pi_q, phi_q = projection(grid, "q", qq)
+
+            dq_x = mul(grid2("dq_x"), q_dir, both(fused(grid("n_phi_qx"), phi_q, -1.0, q_x, MUL, MUL)))
+            add(dq_x[:, 0], dq_x[:, 0], pi_q)
+            dq_v = mul(grid2("dq_v"), q_dir, both(fused(grid("n_phi_qv"), phi_q, -1.0, q_v, MUL, MUL)))
+            add(dq_v[:, 1], dq_v[:, 1], pi_q)
+            dq_q = mul(grid2("dq_q"), q_dir, both(sub(grid("pi_phi_qq"), pi_q, mul(grid("phi_qq"), phi_q, qq))))
+            e_a = mul(grid2("e_a"), dq_x, both(iden_t))
+            live_t = fused(grid("n_live_t"), above(grid("live_t"), den0_t, EPS), -1.0, iden_t, MUL, MUL)
+            e_d = mul(grid2("e_d"), dq_q, both(live_t))
+            to_x = add(grid2("to_x"), e_a, e_d)
+            to_v = mul(
+                grid2("to_v"), add(grid2("to_sec"), mul(grid2("e_d_x2"), e_d, both_over_t(x2)), e_a), both(s)
+            )
+            ds_v = fused(
+                grid2("ds_v"),
+                add(
+                    grid2("ds_v_half"),
+                    mul(grid2("to_x_xv"), to_x, both_over_t(xv)),
+                    mul(grid2("to_v_vv"), to_v, both_over_t(vv)),
+                ),
+                2.0,
+                mul(grid2("q2_dqv"), dq_v, both(q2)),
+                MUL,
+                ADD,
+            )
+            coef_t = radial_coefficient(grid, "t", ht, k2_rt, irt, above(grid("free_t"), c_r0, EPS))
+            coef_c3 = mul(grid("coef_c3"), coef_t, over_tiles(ct3))
+            nc.vector.memset(from_dots[:, 2, 0], 0.0)
+            a_t = mul(from_dots[:, 2, 1], q2s, pi_q)
+            mul(a_scaled[:], a_t, over_t(mu))
+            q2_phi = mul(grid("q2_phi"), q2, phi_q)
+            mul(
+                from_dots[:, 0],
+                fused(
+                    grid2("x_part"),
+                    to_x,
+                    2.0,
+                    mul(grid2("x_lost"), q_dir, both(mul(grid("q2_phi_q1"), q2_phi, q1))),
+                    MUL,
+                    SUB,
+                ),
+                both(s),
+            )
+            add(
+                from_dots[:, 1],
+                mul(
+                    grid2("v_part_s"),
+                    fused(
+                        grid2("v_part"),
+                        to_v,
+                        2.0,
+                        mul(grid2("v_lost"), q_dir, both(mul(grid("q2_phi_q2s"), q2_phi, q2s))),
+                        MUL,
+                        SUB,
+                    ),
+                    both(s),
+                ),
+                mul(grid2("v_radial"), ds_v, both(coef_c3)),
+            )
+
+        for c in range(PASSES):
+            v_rows = stage.tile([P, PACK, K], BF16, name="rows")
+            nc.sync.dma_start(out=v_rows[:].rearrange("p j k -> p (j k)"), in_=v_view[c])
+            quantise_pass(v_rows[:], v_codes[:, c, :], v_scales[:, c, :], E4M3_X4)
+
+        with tc.tile_pool(name="work", bufs=2) as work:
+            for c in range(PASSES):
+                d_rows = stage.tile([P, PACK, N], BF16, name="rows")
+                for j in range(PACK):
+                    i = c * PACK + j
+                    g = grads.tile([P, T, N], BF16, name="g")
+                    nc.sync.dma_start(out=g[:].rearrange("p t n -> p (t n)"), in_=g_view[c, j])
+
+                    turned_sum = [psum.tile([P, BANK], F32, name="bank") for h in range(HALVES)]
+                    for t in range(T):
+                        weighted = work.tile([P, N], F32, name="weighted", bufs=4)
+                        nc.scalar.activation(
+                            out=weighted[:], in_=g[:, t, :], func=ACT.Copy, scale=a_scaled[:, i, t : t + 1]
+                        )
+                        for k in range(BLOCKS):
+                            h, q = divmod(k, BLOCKS_PER_BANK)
+                            nc.tensor.matmul(
+                                out=turned_sum[h][:, q * P : (q + 1) * P],
+                                lhsT=weighted[:, k * P : (k + 1) * P],
+                                rhs=identity[:],
+                                is_transpose=True,
+                                start=(t == 0 and q == 0),
+                                stop=(t == T - 1 and q == BLOCKS_PER_BANK - 1),
+                            )
+
+                    for t in range(T):
+                        dot(dots[:, i, 0, t : t + 1], g[:, t, :], x_all[:, i, :], N)
+                    for t in range(T):
+                        dot(dots[:, i, 1, t : t + 1], g[:, t, :], v0_all[:, i, :], N)
+
+                    turned = work.tile([P, N], F32, name="turned")
+                    for h in range(HALVES):
+                        nc.scalar.copy(out=turned[:, h * BANK : (h + 1) * BANK], in_=turned_sum[h][:])
+                    mu_s = [psum.tile([P, BANK], F32, name="bank") for h in range(HALVES)]
+                    for k in range(BLOCKS):
+                        h, q = divmod(k, BLOCKS_PER_BANK)
+                        nc.tensor.transpose(
+                            out=mu_s[h][:, q * P : (q + 1) * P],
+                            in_=turned[:, k * P : (k + 1) * P],
+                            identity=identity[:],
+                        )
+                    for h in range(HALVES):
+                        dot(inputs[:, i, 3 + h : 4 + h], b_all[:, h * BANK : (h + 1) * BANK], mu_s[h][:], BANK)
+
+                    terms = work.tile([P, 3, 2, T], F32, name="terms")
+                    mul(terms[:], from_dots[:, :, :, i, :], dots[:, i].unsqueeze(1).to_broadcast([P, 3, 2, T]))
+                    nc.vector.tensor_reduce(
+                        out=inputs[:, i, 0:3], in_=terms[:], axis=mybir.AxisListType.XY, op=ADD
+                    )
+                    kappa_terms = work.tile([P, 3, 5], F32, name="kappa_terms")
+                    mul(kappa_terms[:], to_kappa[:, i], inputs[:, i].unsqueeze(1).to_broadcast([P, 3, 5]))
+                    nc.vector.tensor_reduce(
+                        out=kappa[:, i, :], in_=kappa_terms[:], axis=mybir.AxisListType.X, op=ADD
+                    )
+
+                    mix = work.tile([P, N], F32, name="mix")
+                    nc.scalar.activation(
+                        out=mix[:], in_=x_all[:, i, :], func=ACT.Copy, scale=kappa[:, i, 0:1]
+                    )
+                    fused(mix[:], v0_all[:, i, :], kappa[:, i, 1:2], mix[:], MUL, ADD)
+                    fused(mix[:], b_all[:], kappa[:, i, 2:3], mix[:], MUL, ADD)
+                    for h in range(HALVES):
+                        half = slice(h * BANK, (h + 1) * BANK)
+                        add(d_rows[:, j, half], mix[:, half], mu_s[h][:])
+                quantise_pass(d_rows[:], d_codes[:, c, :], d_scales[:, c, :], E5M2_X4)
+
+            for m in range(BLOCKS):
+                of_block = slice(m * P, (m + 1) * P)
+                result = work.tile([P, K], F32, name="result")
+                for h in range(K // BANK):
+                    half = slice(h * BANK, (h + 1) * BANK)
+                    acc = psum.tile([P, BANK], F32, name="bank")
+                    for c in range(PASSES):
+                        nc.tensor.matmul_mx(
+                            out=acc[:],
+                            lhsT=d_codes[:, c, of_block].bitcast(E5M2_X4),
+                            lhsT_scale=d_scales[:, c, of_block],
+                            rhs=v_codes[:, c, half].bitcast(E4M3_X4),
+                            rhs_scale=v_scales[:, c, half],
+                            start=(c == 0),
+                            stop=(c == PASSES - 1),
+                        )
+                    if h % 2 == 0:
+                        nc.scalar.copy(out=result[:, half], in_=acc[:])
+                    else:
+                        nc.vector.tensor_copy(out=result[:, half], in_=acc[:])
+                nc.sync.dma_start(out=out[of_block, :], in_=result[:])

@@ -26,6 +26,8 @@ BANK = 512
 HALVES = N // BANK
 BLOCKS = N // P
 BLOCKS_PER_BANK = BANK // P
+B_COPIES = 32
+V_INIT_AT = 5
 
 EPS = 1e-7
 EPS_SQ = EPS * EPS
@@ -44,25 +46,27 @@ def tile_paralleldirectpoincaredynamics_v_kernel(
     with ExitStack() as ctx:
         keep = ctx.enter_context(tc.tile_pool(name="keep", bufs=1))
         grads = ctx.enter_context(tc.tile_pool(name="grads", bufs=3))
-        unread = ctx.enter_context(tc.tile_pool(name="unread", bufs=4))
+        unread = ctx.enter_context(tc.tile_pool(name="unread", bufs=3))
         stage = ctx.enter_context(tc.tile_pool(name="stage", bufs=2))
+        chain = ctx.enter_context(tc.tile_pool(name="chain", bufs=1))
+        work = ctx.enter_context(tc.tile_pool(name="work", bufs=2))
         psum = ctx.enter_context(tc.psum_pool(name="psum", bufs=8))
 
         x_all = keep.tile([P, TILES, N], BF16, name="x_all")
-        v0_all = keep.tile([P, TILES, N], F32, name="v0_all")
+        mv_all = keep.tile([P, TILES, N], F32, name="mv_all")
         b_all = keep.tile([P, N], BF16, name="b_all")
         vn_row = keep.tile([P, TILES], F32, name="vn_row")
         logit = keep.tile([P, 1], BF16, name="logit")
         z_view = z_0.rearrange("(c p j) n -> c p (j n)", c=PASSES, p=P, j=PACK)
         mv_view = mv.rearrange("(c p j) n -> c p (j n)", c=PASSES, p=P, j=PACK)
-        v_view = v_init.rearrange("(c p j) k -> c p (j k)", c=PASSES, p=P, j=PACK)
+        v_view = v_init.rearrange("(c p j) k -> p c (j k)", c=PASSES, p=P, j=PACK)
         g_view = grad_out.rearrange("(c p j) t n -> c j p (t n)", c=PASSES, p=P, j=PACK)
 
         nc.sync.dma_start(out=b_all[:], in_=b.partition_broadcast(P))
         for c in range(PASSES):
             of_pass = slice(c * PACK, (c + 1) * PACK)
             nc.sync.dma_start(
-                out=v0_all[:, of_pass, :].rearrange("p j n -> p (j n)"), in_=mv_view[c]
+                out=mv_all[:, of_pass, :].rearrange("p j n -> p (j n)"), in_=mv_view[c]
             )
             nc.sync.dma_start(
                 out=x_all[:, of_pass, :].rearrange("p j n -> p (j n)"), in_=z_view[c]
@@ -126,6 +130,8 @@ def tile_paralleldirectpoincaredynamics_v_kernel(
 
         def table(dst, a, func, s=1.0):
             nc.scalar.activation(out=dst, in_=a, func=func, scale=s)
+            for spare in range(2):
+                next_x_dot()
             return dst
 
         def dot(acc, a, b_, width):
@@ -138,14 +144,38 @@ def tile_paralleldirectpoincaredynamics_v_kernel(
             squares = unread.tile([P, N], BF16, name="squares")
             nc.scalar.activation(out=squares[:], in_=a, func=ACT.Square, accum_out=acc)
 
-        def quantise_pass(rows, codes, scales, packed_dtype):
-            grouped = stage.tile([P, N, PACK], BF16, name="grouped", align_bytes=64)
-            nc.scalar.copy(out=grouped[:], in_=rows.rearrange("p j n -> p n j"))
-            nc.vector.quantize_mx(
-                out=codes.bitcast(packed_dtype),
-                scales=scales,
-                in_=grouped[:].rearrange("p n j -> p (n j)"),
-            )
+        def regroup_pass(rows, copy):
+            halves = []
+            for h in range(HALVES):
+                grouped = stage.tile([P, BANK, PACK], BF16, name="grouped", align_bytes=64)
+                copy(
+                    out=grouped[:].rearrange("p (c r) j -> p c j r", r=4),
+                    in_=rows[:, :, h * BANK : (h + 1) * BANK].rearrange("p j (c r) -> p c j r", r=4),
+                )
+                halves.append(grouped)
+            return halves
+
+        def quantise_pass(halves, codes, scales, packed_dtype):
+            for h in range(HALVES):
+                half = slice(h * BANK, (h + 1) * BANK)
+                nc.vector.quantize_mx(
+                    out=codes[:, half].bitcast(packed_dtype),
+                    scales=scales[:, half],
+                    in_=halves[h][:].rearrange("p n j -> p (n j)"),
+                )
+
+        g_tiles = {}
+        x_dots_issued = [0]
+
+        def next_x_dot():
+            i, t = divmod(x_dots_issued[0], T)
+            x_dots_issued[0] += 1
+            if t == 0:
+                g_tiles[i] = grads.tile([P, T, N], BF16, name="g")
+                nc.sync.dma_start(
+                    out=g_tiles[i][:].rearrange("p t n -> p (t n)"), in_=g_view[i // PACK, i % PACK]
+                )
+            dot(dots[:, i, 0, t : t + 1], g_tiles[i][:, t, :], x_all[:, i, :], N)
 
         v_codes = keep.tile([P, PASSES, K], U32, name="v_codes", align_bytes=64)
         v_scales = keep.tile([P, PASSES, K], U8, name="v_scales", align_bytes=64)
@@ -154,356 +184,392 @@ def tile_paralleldirectpoincaredynamics_v_kernel(
 
         a_scaled = keep.tile([P, TILES, T], F32, name="a_scaled")
         from_dots = keep.tile([P, 3, 2, TILES, T], F32, name="from_dots")
-        to_kappa = keep.tile([P, TILES, 3, 5], F32, name="to_kappa")
+        to_kappa = keep.tile([P, TILES, 3, 4], F32, name="to_kappa")
+        mu = keep.tile([P, TILES], F32, name="mu")
+        nu = keep.tile([P, TILES], F32, name="nu")
         dots = keep.tile([P, TILES, 2, T], F32, name="dots")
-        inputs = keep.tile([P, TILES, 5], F32, name="inputs")
+        inputs = keep.tile([P, TILES, 4], F32, name="inputs")
         kappa = keep.tile([P, TILES, 3], F32, name="kappa")
+        b_cols = keep.tile([P, BLOCKS, B_COPIES], F32, name="b_cols")
 
-        with tc.tile_pool(name="chain", bufs=1) as chain:
 
-            def col(name):
-                return chain.tile([P, 1], F32, name=name)
+        def banks():
+            return [psum.tile([P, BANK], F32, name="bank") for h in range(HALVES)]
 
-            def row(name):
-                return chain.tile([P, TILES], F32, name=name)
+        def add_turned(total, term, first, last):
+            for k in range(BLOCKS):
+                h, q = divmod(k, BLOCKS_PER_BANK)
+                nc.tensor.matmul(
+                    out=total[h][:, q * P : (q + 1) * P],
+                    lhsT=term[:, k * P : (k + 1) * P],
+                    rhs=identity[:],
+                    is_transpose=True,
+                    start=(first and q == 0),
+                    stop=(last and q == BLOCKS_PER_BANK - 1),
+                )
 
-            def row2(name):
-                return chain.tile([P, 2, TILES], F32, name=name)
+        def out_of_psum(dst, total):
+            for h in range(HALVES):
+                nc.scalar.copy(out=dst[:, h * BANK : (h + 1) * BANK], in_=total[h][:])
 
-            def grid(name):
-                return chain.tile([P, TILES, T], F32, name=name)
+        def times_row_factor(src, factor):
+            scaled = work.tile([P, N], F32, name="scaled", bufs=4)
+            nc.scalar.activation(out=scaled[:], in_=src, func=ACT.Copy, scale=factor)
+            return scaled
 
-            def grid2(name):
-                return chain.tile([P, 2, TILES, T], F32, name=name)
-
-            def pair(r):
-                return r.unsqueeze(1).to_broadcast([P, 2, TILES])
-
-            def over_t(r):
-                return r.unsqueeze(2).to_broadcast([P, TILES, T])
-
-            def over_tiles(h):
-                return h.unsqueeze(1).to_broadcast([P, TILES, T])
-
-            def both(g):
-                return g.unsqueeze(1).to_broadcast([P, 2, TILES, T])
-
-            def both_over_t(r):
-                return r.unsqueeze(1).unsqueeze(3).to_broadcast([P, 2, TILES, T])
-
-            def projection(make, tag, norm_sq):
-                r = table(make(tag + "_r"), at_least(make(tag + "_c"), norm_sq, EPS_SQ), ACT.Sqrt)
-                on = above(make(tag + "_on"), r, MAX_NORM)
-                ir = inverse(make(tag + "_ir"), r)
-                excess = mul(make(tag + "_ex"), affine(make(tag + "_sc"), ir, MAX_NORM, -1.0), on)
-                pi = affine(make(tag + "_pi"), excess, 1.0, 1.0)
-                ir3 = mul(make(tag + "_ir3"), mul(make(tag + "_ir2"), ir, ir), ir)
-                phi = fused(make(tag + "_phi"), ir3, MAX_NORM, on, MUL, MUL)
-                return pi, phi
-
-            def radial_coefficient(make, tag, h, kr, ir, free):
-                slope = affine(make(tag + "_sl"), mul(make(tag + "_h2"), h, h), -1.0, 1.0)
-                top = sub(make(tag + "_top"), mul(make(tag + "_skr"), slope, kr), h)
-                ir3 = mul(make(tag + "_jr3"), mul(make(tag + "_jr2"), ir, ir), ir)
-                return mul(make(tag + "_cf"), mul(make(tag + "_q"), top, ir3), free)
-
-            bb = col("bb")
-            m2, mb, x2, xb = row("m2"), row("mb"), row("x2"), row("xb")
-            square_sum(bb[:], b_all[:])
-            for i in range(TILES):
-                square_sum(m2[:, i : i + 1], v0_all[:, i, :])
-                square_sum(x2[:, i : i + 1], x_all[:, i, :])
-                dot(mb[:, i : i + 1], v0_all[:, i, :], b_all[:], N)
-                dot(xb[:, i : i + 1], x_all[:, i, :], b_all[:], N)
-
-            rb = table(col("rb"), at_least(col("bb_c"), bb, EPS_SQ), ACT.Sqrt)
-            beta = mul(col("beta"), table(col("hb"), rb, ACT.Tanh), inverse(col("irb"), rb))
-            beta2 = scale(col("beta2"), beta, 2.0)
-            y2 = mul(col("y2"), mul(col("beta_bb"), beta, bb), beta)
-
-            clipped = row("clipped")
-            nc.vector.tensor_scalar(
-                out=clipped,
-                in0=vn_row,
-                scalar1=-CLIP,
-                scalar2=CLIP,
-                op0=mybir.AluOpType.max,
-                op1=mybir.AluOpType.min,
-            )
-            ratio = mul(
-                row("ratio"),
-                affine(row("one_plus"), clipped, 1.0, 1.0),
-                inverse(row("inv_one_minus"), affine(row("one_minus"), clipped, -1.0, 1.0)),
-            )
-            k1 = fused(
-                row("k1"), table(row("ln_ratio"), ratio, ACT.Ln), 0.5, inverse(row("ivn"), vn_row), MUL, MUL
+        b_f32 = work.tile([P, N], F32, name="scaled", bufs=4)
+        nc.vector.tensor_copy(out=b_f32[:], in_=b_all[:])
+        b_turned = banks()
+        add_turned(b_turned, b_f32, True, True)
+        for h in range(HALVES):
+            nc.scalar.copy(
+                out=b_cols[:, h * BLOCKS_PER_BANK : (h + 1) * BLOCKS_PER_BANK, :],
+                in_=b_turned[h][:].rearrange("p (q r) -> p q r", r=P)[:, :, :B_COPIES],
             )
 
-            rm = table(row("rm"), at_least(row("m2_c"), m2, EPS_SQ), ACT.Sqrt)
-            k1_rm = mul(row("k1_rm"), k1, rm)
-            hm = table(row("hm"), k1_rm, ACT.Tanh)
-            irm = inverse(row("irm"), rm)
-            alpha = mul(row("alpha"), hm, irm)
-            alpha_m2 = mul(row("alpha_m2"), alpha, m2)
-            res2 = mul(row("res2"), alpha_m2, alpha)
-            res_b = scale(row("res_b"), mul(row("alpha_mb"), alpha, mb), beta)
+        def col(name):
+            return chain.tile([P, 1], F32, name=name)
 
-            base = affine(row("base"), res_b, 2.0, 1.0)
-            den0 = fused(row("den0"), res2, y2, base, MUL, ADD)
-            iden = inverse(row("iden"), at_least(row("den"), den0, EPS))
-            p1 = mul(row("p1"), shift(row("a1"), base, y2), iden)
-            p2 = mul(row("p2"), affine(row("a2"), res2, -1.0, 1.0), iden)
-            p_dir = row2("p_dir")
-            pa = mul(p_dir[:, 0, :], p1, alpha)
-            pb = scale(p_dir[:, 1, :], p2, beta)
-            p_mv = add(row("p_mv"), mul(row("pa_m2"), pa, m2), mul(row("pb_mb"), pb, mb))
-            p_b = fused(row("p_b"), pb, bb, mul(row("pa_mb"), pa, mb), MUL, ADD)
-            pp = add(row("pp"), mul(row("pa_pmv"), pa, p_mv), mul(row("pb_pb"), pb, p_b))
-            pi, phi = projection(row, "p", pp)
+        def row(name):
+            return chain.tile([P, TILES], F32, name=name)
 
-            mu = mul(row("mu"), pi, pa)
-            nu = mul(row("nu"), pi, pb)
-            vv, xv = row("vv"), row("xv")
-            for i in range(TILES):
-                v0 = v0_all[:, i, :]
-                nc.scalar.activation(out=v0, in_=v0, func=ACT.Copy, scale=mu[:, i : i + 1])
-                fused(v0, b_all[:], nu[:, i : i + 1], v0, MUL, ADD)
-                square_sum(vv[:, i : i + 1], v0)
-                dot(xv[:, i : i + 1], x_all[:, i, :], v0, N)
-            vb = add(row("vb"), mul(row("mu_mb"), mu, mb), scale(row("nu_bb"), nu, bb))
+        def row2(name):
+            return chain.tile([P, 2, TILES], F32, name=name)
 
-            dp_mv = mul(row2("dp_mv"), p_dir, pair(fused(row("n_phi_pmv"), phi, -1.0, p_mv, MUL, MUL)))
-            add(dp_mv[:, 0, :], dp_mv[:, 0, :], pi)
-            dp_b = mul(row2("dp_b"), p_dir, pair(fused(row("n_phi_pb"), phi, -1.0, p_b, MUL, MUL)))
-            add(dp_b[:, 1, :], dp_b[:, 1, :], pi)
-            dp_p = mul(row2("dp_p"), p_dir, pair(sub(row("pi_phi_pp"), pi, mul(row("phi_pp"), phi, pp))))
-            d_a = mul(row2("d_a"), dp_mv, pair(mul(row("iden_alpha"), iden, alpha)))
-            d_b = mul(row2("d_b"), dp_b, pair(scale(row("iden_beta"), iden, beta)))
-            live = fused(row("n_live_iden"), above(row("live"), den0, EPS), -1.0, iden, MUL, MUL)
-            d_d = mul(row2("d_d"), dp_p, pair(live))
-            to_b = add(row2("to_b"), d_a, d_d)
-            to_res = fused(row2("to_res"), d_d, y2, d_b, MUL, SUB)
-            dres_mv = add(
-                row2("dres_mv"),
-                add(
-                    row2("dres_mv2"),
-                    mul(row2("dres_mv_a"), dp_mv, pair(p1)),
-                    mul(row2("dres_mv_b"), to_b, pair(scale(row("beta2_mb"), mb, beta2))),
-                ),
-                mul(row2("dres_mv_c"), to_res, pair(scale(row("alpha_m2_2"), alpha_m2, 2.0))),
-            )
-            coef_m = radial_coefficient(row, "m", hm, k1_rm, irm, above(row("free_m"), m2, EPS_SQ))
-            lost = mul(row("lost"), pa, phi)
-            on_both = chain.tile([P, 2, 2, TILES], F32, name="on_both")
-            sub(
-                on_both[:, 0],
-                add(
-                    row2("on_mv2"),
-                    mul(row2("on_mv_a"), to_res, pair(fused(row("alpha_sq2"), alpha, 2.0, alpha, MUL, MUL))),
-                    mul(row2("on_mv_b"), dres_mv, pair(coef_m)),
-                ),
-                mul(row2("on_mv_c"), p_dir, pair(mul(row("lost_pa"), lost, pa))),
-            )
-            sub(
-                on_both[:, 1],
-                mul(row2("on_b_a"), to_b, pair(scale(row("alpha_beta2"), alpha, beta2))),
-                mul(row2("on_b_c"), p_dir, pair(mul(row("lost_pb"), lost, pb))),
-            )
-            imu = inverse(row("imu"), mu)
-            in_v0_b = chain.tile([P, 2, 2, TILES], F32, name="in_v0_b")
-            mul(in_v0_b[:, :, 0, :], on_both[:, :, 0, :], pair(imu))
-            sub(in_v0_b[:, :, 1, :], on_both[:, :, 1, :], mul(row2("nu_first"), in_v0_b[:, :, 0, :], pair(nu)))
-            weights = chain.tile([P, 2, 2, TILES], F32, name="weights")
-            mul(weights[:, 0], in_v0_b[:, 0], pair(imu))
-            sub(weights[:, 1], in_v0_b[:, 1], mul(row2("nu_on_v0"), weights[:, 0], pair(nu)))
-            nc.vector.memset(to_kappa[:], 0.0)
-            nc.vector.tensor_copy(out=to_kappa[:, :, 0, 0], in_=mu)
+        def grid(name):
+            return chain.tile([P, TILES, T], F32, name=name)
 
-            def kappa_column(m):
-                return to_kappa[:, :, 1:3, m].rearrange("p i k -> p k i")
+        def grid2(name):
+            return chain.tile([P, 2, TILES, T], F32, name=name)
 
-            w_v0, w_b = weights[:, :, 0, :], weights[:, :, 1, :]
-            add(kappa_column(0), mul(row2("kx_a"), w_v0, pair(xv)), mul(row2("kx_b"), w_b, pair(xb)))
-            add(kappa_column(1), mul(row2("kv_a"), w_v0, pair(vv)), mul(row2("kv_b"), w_b, pair(vb)))
-            add(to_kappa[:, :, 1, 1], to_kappa[:, :, 1, 1], mu)
-            nc.vector.tensor_copy(out=kappa_column(2), in_=w_v0)
-            mul(kappa_column(3), w_b, pair(imu))
-            mul(kappa_column(4), w_b, pair(imu))
+        def pair(r):
+            return r.unsqueeze(1).to_broadcast([P, 2, TILES])
 
-            step = affine(col("step"), table(col("half_tanh"), logit, ACT.Tanh, 0.5), 0.5, 0.5)
-            ct = scale(chain.tile([P, T], F32, name="ct"), horizon, step)
-            ct3 = mul(chain.tile([P, T], F32, name="ct3"), mul(chain.tile([P, T], F32, name="ct2"), ct, ct), ct)
-            gap = affine(row("gap"), x2, -1.0, 1.0)
-            k2 = inverse(row("k2"), at_least(row("gap_c"), gap, EPS))
-            r0 = table(row("r0"), at_least(row("vv_c"), vv, TINY), ACT.Sqrt)
-            c_r0 = mul(grid("c_r0"), over_t(r0), over_tiles(ct))
-            rt = at_least(grid("rt"), c_r0, EPS)
-            k2_rt = mul(grid("k2_rt"), rt, over_t(k2))
-            ht = table(grid("ht"), k2_rt, ACT.Tanh)
-            irt = inverse(grid("irt"), rt)
-            s = mul(grid("s"), mul(grid("sigma"), ht, irt), over_tiles(ct))
-            x_sec = mul(grid("x_sec"), s, over_t(xv))
-            sec2 = mul(grid("sec2"), mul(grid("s_vv"), s, over_t(vv)), s)
-            base_t = affine(grid("base_t"), x_sec, 2.0, 1.0)
-            den0_t = add(grid("den0_t"), mul(grid("x2_sec2"), sec2, over_t(x2)), base_t)
-            iden_t = inverse(grid("iden_t"), at_least(grid("den_t"), den0_t, EPS))
-            q_dir = grid2("q_dir")
-            q1 = mul(q_dir[:, 0], add(grid("b1"), base_t, sec2), iden_t)
-            q2 = mul(grid("q2"), iden_t, over_t(gap))
-            q2s = mul(q_dir[:, 1], q2, s)
-            q_x = add(grid("q_x"), mul(grid("q1_x2"), q1, over_t(x2)), mul(grid("q2_xsec"), q2, x_sec))
-            q_v = add(grid("q_v"), mul(grid("q1_xv"), q1, over_t(xv)), mul(grid("q2s_vv"), q2s, over_t(vv)))
-            qq = add(grid("qq"), mul(grid("q1_qx"), q1, q_x), mul(grid("q2s_qv"), q2s, q_v))
-            pi_q, phi_q = projection(grid, "q", qq)
+        def over_t(r):
+            return r.unsqueeze(2).to_broadcast([P, TILES, T])
 
-            dq_x = mul(grid2("dq_x"), q_dir, both(fused(grid("n_phi_qx"), phi_q, -1.0, q_x, MUL, MUL)))
-            add(dq_x[:, 0], dq_x[:, 0], pi_q)
-            dq_v = mul(grid2("dq_v"), q_dir, both(fused(grid("n_phi_qv"), phi_q, -1.0, q_v, MUL, MUL)))
-            add(dq_v[:, 1], dq_v[:, 1], pi_q)
-            dq_q = mul(grid2("dq_q"), q_dir, both(sub(grid("pi_phi_qq"), pi_q, mul(grid("phi_qq"), phi_q, qq))))
-            e_a = mul(grid2("e_a"), dq_x, both(iden_t))
-            live_t = fused(grid("n_live_t"), above(grid("live_t"), den0_t, EPS), -1.0, iden_t, MUL, MUL)
-            e_d = mul(grid2("e_d"), dq_q, both(live_t))
-            to_x = add(grid2("to_x"), e_a, e_d)
-            to_v = mul(
-                grid2("to_v"), add(grid2("to_sec"), mul(grid2("e_d_x2"), e_d, both_over_t(x2)), e_a), both(s)
-            )
-            ds_v = fused(
-                grid2("ds_v"),
-                add(
-                    grid2("ds_v_half"),
-                    mul(grid2("to_x_xv"), to_x, both_over_t(xv)),
-                    mul(grid2("to_v_vv"), to_v, both_over_t(vv)),
-                ),
+        def over_tiles(h):
+            return h.unsqueeze(1).to_broadcast([P, TILES, T])
+
+        def both(g):
+            return g.unsqueeze(1).to_broadcast([P, 2, TILES, T])
+
+        def both_over_t(r):
+            return r.unsqueeze(1).unsqueeze(3).to_broadcast([P, 2, TILES, T])
+
+        def projection(make, tag, norm_sq):
+            r = table(make(tag + "_r"), at_least(make(tag + "_c"), norm_sq, EPS_SQ), ACT.Sqrt)
+            on = above(make(tag + "_on"), r, MAX_NORM)
+            ir = inverse(make(tag + "_ir"), r)
+            excess = mul(make(tag + "_ex"), affine(make(tag + "_sc"), ir, MAX_NORM, -1.0), on)
+            pi = affine(make(tag + "_pi"), excess, 1.0, 1.0)
+            ir3 = mul(make(tag + "_ir3"), mul(make(tag + "_ir2"), ir, ir), ir)
+            phi = fused(make(tag + "_phi"), ir3, MAX_NORM, on, MUL, MUL)
+            return pi, phi
+
+        def radial_coefficient(make, tag, h, kr, ir, free):
+            slope = affine(make(tag + "_sl"), mul(make(tag + "_h2"), h, h), -1.0, 1.0)
+            top = sub(make(tag + "_top"), mul(make(tag + "_skr"), slope, kr), h)
+            ir3 = mul(make(tag + "_jr3"), mul(make(tag + "_jr2"), ir, ir), ir)
+            return mul(make(tag + "_cf"), mul(make(tag + "_q"), top, ir3), free)
+
+        bb = col("bb")
+        m2, mb, x2, xb, xm = row("m2"), row("mb"), row("x2"), row("xb"), row("xm")
+        square_sum(bb[:], b_all[:])
+        for i in range(TILES):
+            square_sum(m2[:, i : i + 1], mv_all[:, i, :])
+            square_sum(x2[:, i : i + 1], x_all[:, i, :])
+            dot(mb[:, i : i + 1], mv_all[:, i, :], b_all[:], N)
+            dot(xb[:, i : i + 1], x_all[:, i, :], b_all[:], N)
+            dot(xm[:, i : i + 1], x_all[:, i, :], mv_all[:, i, :], N)
+
+        rb = table(col("rb"), at_least(col("bb_c"), bb, EPS_SQ), ACT.Sqrt)
+        beta = mul(col("beta"), table(col("hb"), rb, ACT.Tanh), inverse(col("irb"), rb))
+        beta2 = scale(col("beta2"), beta, 2.0)
+        y2 = mul(col("y2"), mul(col("beta_bb"), beta, bb), beta)
+
+        clipped = row("clipped")
+        nc.vector.tensor_scalar(
+            out=clipped,
+            in0=vn_row,
+            scalar1=-CLIP,
+            scalar2=CLIP,
+            op0=mybir.AluOpType.max,
+            op1=mybir.AluOpType.min,
+        )
+        ratio = mul(
+            row("ratio"),
+            affine(row("one_plus"), clipped, 1.0, 1.0),
+            inverse(row("inv_one_minus"), affine(row("one_minus"), clipped, -1.0, 1.0)),
+        )
+        k1 = fused(
+            row("k1"), table(row("ln_ratio"), ratio, ACT.Ln), 0.5, inverse(row("ivn"), vn_row), MUL, MUL
+        )
+
+        rm = table(row("rm"), at_least(row("m2_c"), m2, EPS_SQ), ACT.Sqrt)
+        k1_rm = mul(row("k1_rm"), k1, rm)
+        hm = table(row("hm"), k1_rm, ACT.Tanh)
+        irm = inverse(row("irm"), rm)
+        alpha = mul(row("alpha"), hm, irm)
+        alpha_m2 = mul(row("alpha_m2"), alpha, m2)
+        res2 = mul(row("res2"), alpha_m2, alpha)
+        res_b = scale(row("res_b"), mul(row("alpha_mb"), alpha, mb), beta)
+
+        base = affine(row("base"), res_b, 2.0, 1.0)
+        den0 = fused(row("den0"), res2, y2, base, MUL, ADD)
+        iden = inverse(row("iden"), at_least(row("den"), den0, EPS))
+        p1 = mul(row("p1"), shift(row("a1"), base, y2), iden)
+        p2 = mul(row("p2"), affine(row("a2"), res2, -1.0, 1.0), iden)
+        p_dir = row2("p_dir")
+        pa = mul(p_dir[:, 0, :], p1, alpha)
+        pb = scale(p_dir[:, 1, :], p2, beta)
+        p_mv = add(row("p_mv"), mul(row("pa_m2"), pa, m2), mul(row("pb_mb"), pb, mb))
+        p_b = fused(row("p_b"), pb, bb, mul(row("pa_mb"), pa, mb), MUL, ADD)
+        pp = add(row("pp"), mul(row("pa_pmv"), pa, p_mv), mul(row("pb_pb"), pb, p_b))
+        pi, phi = projection(row, "p", pp)
+
+        mul(mu, pi, pa)
+        mul(nu, pi, pb)
+        vv = mul(row("vv"), mul(row("pi_sq"), pi, pi), pp)
+        xv = add(row("xv"), mul(row("mu_xm"), mu, xm), mul(row("nu_xb"), nu, xb))
+        vb = add(row("vb"), mul(row("mu_mb"), mu, mb), scale(row("nu_bb"), nu, bb))
+
+        step = affine(col("step"), table(col("half_tanh"), logit, ACT.Tanh, 0.5), 0.5, 0.5)
+        ct = scale(chain.tile([P, T], F32, name="ct"), horizon, step)
+        ct3 = mul(chain.tile([P, T], F32, name="ct3"), mul(chain.tile([P, T], F32, name="ct2"), ct, ct), ct)
+        gap = affine(row("gap"), x2, -1.0, 1.0)
+        k2 = inverse(row("k2"), at_least(row("gap_c"), gap, EPS))
+        r0 = table(row("r0"), at_least(row("vv_c"), vv, TINY), ACT.Sqrt)
+        c_r0 = mul(grid("c_r0"), over_t(r0), over_tiles(ct))
+        rt = at_least(grid("rt"), c_r0, EPS)
+        k2_rt = mul(grid("k2_rt"), rt, over_t(k2))
+        ht = table(grid("ht"), k2_rt, ACT.Tanh)
+        irt = inverse(grid("irt"), rt)
+        s = mul(grid("s"), mul(grid("sigma"), ht, irt), over_tiles(ct))
+        x_sec = mul(grid("x_sec"), s, over_t(xv))
+        sec2 = mul(grid("sec2"), mul(grid("s_vv"), s, over_t(vv)), s)
+        base_t = affine(grid("base_t"), x_sec, 2.0, 1.0)
+        den0_t = add(grid("den0_t"), mul(grid("x2_sec2"), sec2, over_t(x2)), base_t)
+        iden_t = inverse(grid("iden_t"), at_least(grid("den_t"), den0_t, EPS))
+        q_dir = grid2("q_dir")
+        q1 = mul(q_dir[:, 0], add(grid("b1"), base_t, sec2), iden_t)
+        q2 = mul(grid("q2"), iden_t, over_t(gap))
+        q2s = mul(q_dir[:, 1], q2, s)
+        q_x = add(grid("q_x"), mul(grid("q1_x2"), q1, over_t(x2)), mul(grid("q2_xsec"), q2, x_sec))
+        q_v = add(grid("q_v"), mul(grid("q1_xv"), q1, over_t(xv)), mul(grid("q2s_vv"), q2s, over_t(vv)))
+        qq = add(grid("qq"), mul(grid("q1_qx"), q1, q_x), mul(grid("q2s_qv"), q2s, q_v))
+        pi_q, phi_q = projection(grid, "q", qq)
+
+        a_t = mul(from_dots[:, 2, 1], q2s, pi_q)
+        mul(a_scaled[:], a_t, over_t(mu))
+        nc.vector.memset(from_dots[:, 2, 0], 0.0)
+
+        dp_mv = mul(row2("dp_mv"), p_dir, pair(fused(row("n_phi_pmv"), phi, -1.0, p_mv, MUL, MUL)))
+        add(dp_mv[:, 0, :], dp_mv[:, 0, :], pi)
+        dp_b = mul(row2("dp_b"), p_dir, pair(fused(row("n_phi_pb"), phi, -1.0, p_b, MUL, MUL)))
+        add(dp_b[:, 1, :], dp_b[:, 1, :], pi)
+        dp_p = mul(row2("dp_p"), p_dir, pair(sub(row("pi_phi_pp"), pi, mul(row("phi_pp"), phi, pp))))
+        d_a = mul(row2("d_a"), dp_mv, pair(mul(row("iden_alpha"), iden, alpha)))
+        d_b = mul(row2("d_b"), dp_b, pair(scale(row("iden_beta"), iden, beta)))
+        live = fused(row("n_live_iden"), above(row("live"), den0, EPS), -1.0, iden, MUL, MUL)
+        d_d = mul(row2("d_d"), dp_p, pair(live))
+        to_b = add(row2("to_b"), d_a, d_d)
+        to_res = fused(row2("to_res"), d_d, y2, d_b, MUL, SUB)
+        dres_mv = add(
+            row2("dres_mv"),
+            add(
+                row2("dres_mv2"),
+                mul(row2("dres_mv_a"), dp_mv, pair(p1)),
+                mul(row2("dres_mv_b"), to_b, pair(scale(row("beta2_mb"), mb, beta2))),
+            ),
+            mul(row2("dres_mv_c"), to_res, pair(scale(row("alpha_m2_2"), alpha_m2, 2.0))),
+        )
+        coef_m = radial_coefficient(row, "m", hm, k1_rm, irm, above(row("free_m"), m2, EPS_SQ))
+        lost = mul(row("lost"), pa, phi)
+        on_both = chain.tile([P, 2, 2, TILES], F32, name="on_both")
+        sub(
+            on_both[:, 0],
+            add(
+                row2("on_mv2"),
+                mul(row2("on_mv_a"), to_res, pair(fused(row("alpha_sq2"), alpha, 2.0, alpha, MUL, MUL))),
+                mul(row2("on_mv_b"), dres_mv, pair(coef_m)),
+            ),
+            mul(row2("on_mv_c"), p_dir, pair(mul(row("lost_pa"), lost, pa))),
+        )
+        sub(
+            on_both[:, 1],
+            mul(row2("on_b_a"), to_b, pair(scale(row("alpha_beta2"), alpha, beta2))),
+            mul(row2("on_b_c"), p_dir, pair(mul(row("lost_pb"), lost, pb))),
+        )
+        imu = inverse(row("imu"), mu)
+        in_v0_b = chain.tile([P, 2, 2, TILES], F32, name="in_v0_b")
+        mul(in_v0_b[:, :, 0, :], on_both[:, :, 0, :], pair(imu))
+        sub(in_v0_b[:, :, 1, :], on_both[:, :, 1, :], mul(row2("nu_first"), in_v0_b[:, :, 0, :], pair(nu)))
+        weights = chain.tile([P, 2, 2, TILES], F32, name="weights")
+        mul(weights[:, 0], in_v0_b[:, 0], pair(imu))
+        sub(weights[:, 1], in_v0_b[:, 1], mul(row2("nu_on_v0"), weights[:, 0], pair(nu)))
+        nc.vector.memset(to_kappa[:], 0.0)
+        nc.vector.tensor_copy(out=to_kappa[:, :, 0, 0], in_=mu)
+
+        def kappa_column(m):
+            return to_kappa[:, :, 1:3, m].rearrange("p i k -> p k i")
+
+        w_v0, w_b = weights[:, :, 0, :], weights[:, :, 1, :]
+        add(kappa_column(0), mul(row2("kx_a"), w_v0, pair(xv)), mul(row2("kx_b"), w_b, pair(xb)))
+        add(kappa_column(1), mul(row2("kv_a"), w_v0, pair(vv)), mul(row2("kv_b"), w_b, pair(vb)))
+        add(to_kappa[:, :, 1, 1], to_kappa[:, :, 1, 1], mu)
+        nc.vector.tensor_copy(out=kappa_column(2), in_=w_v0)
+        mul(kappa_column(3), w_b, pair(imu))
+
+        dq_x = mul(grid2("dq_x"), q_dir, both(fused(grid("n_phi_qx"), phi_q, -1.0, q_x, MUL, MUL)))
+        add(dq_x[:, 0], dq_x[:, 0], pi_q)
+        dq_v = mul(grid2("dq_v"), q_dir, both(fused(grid("n_phi_qv"), phi_q, -1.0, q_v, MUL, MUL)))
+        add(dq_v[:, 1], dq_v[:, 1], pi_q)
+        dq_q = mul(grid2("dq_q"), q_dir, both(sub(grid("pi_phi_qq"), pi_q, mul(grid("phi_qq"), phi_q, qq))))
+        e_a = mul(grid2("e_a"), dq_x, both(iden_t))
+        live_t = fused(grid("n_live_t"), above(grid("live_t"), den0_t, EPS), -1.0, iden_t, MUL, MUL)
+        e_d = mul(grid2("e_d"), dq_q, both(live_t))
+        to_x = add(grid2("to_x"), e_a, e_d)
+        to_v = mul(
+            grid2("to_v"), add(grid2("to_sec"), mul(grid2("e_d_x2"), e_d, both_over_t(x2)), e_a), both(s)
+        )
+        ds_v = fused(
+            grid2("ds_v"),
+            add(
+                grid2("ds_v_half"),
+                mul(grid2("to_x_xv"), to_x, both_over_t(xv)),
+                mul(grid2("to_v_vv"), to_v, both_over_t(vv)),
+            ),
+            2.0,
+            mul(grid2("q2_dqv"), dq_v, both(q2)),
+            MUL,
+            ADD,
+        )
+        coef_t = radial_coefficient(grid, "t", ht, k2_rt, irt, above(grid("free_t"), c_r0, EPS))
+        coef_c3 = mul(grid("coef_c3"), coef_t, over_tiles(ct3))
+        q2_phi = mul(grid("q2_phi"), q2, phi_q)
+        mul(
+            from_dots[:, 0],
+            fused(
+                grid2("x_part"),
+                to_x,
                 2.0,
-                mul(grid2("q2_dqv"), dq_v, both(q2)),
+                mul(grid2("x_lost"), q_dir, both(mul(grid("q2_phi_q1"), q2_phi, q1))),
                 MUL,
-                ADD,
-            )
-            coef_t = radial_coefficient(grid, "t", ht, k2_rt, irt, above(grid("free_t"), c_r0, EPS))
-            coef_c3 = mul(grid("coef_c3"), coef_t, over_tiles(ct3))
-            nc.vector.memset(from_dots[:, 2, 0], 0.0)
-            a_t = mul(from_dots[:, 2, 1], q2s, pi_q)
-            mul(a_scaled[:], a_t, over_t(mu))
-            q2_phi = mul(grid("q2_phi"), q2, phi_q)
+                SUB,
+            ),
+            both(s),
+        )
+        add(
+            from_dots[:, 1],
             mul(
-                from_dots[:, 0],
+                grid2("v_part_s"),
                 fused(
-                    grid2("x_part"),
-                    to_x,
+                    grid2("v_part"),
+                    to_v,
                     2.0,
-                    mul(grid2("x_lost"), q_dir, both(mul(grid("q2_phi_q1"), q2_phi, q1))),
+                    mul(grid2("v_lost"), q_dir, both(mul(grid("q2_phi_q2s"), q2_phi, q2s))),
                     MUL,
                     SUB,
                 ),
                 both(s),
+            ),
+            mul(grid2("v_radial"), ds_v, both(coef_c3)),
+        )
+
+
+        turned_sums = {}
+        d_rows = {}
+
+        def weighted_sum(i):
+            v0 = mv_all[:, i, :]
+            nc.scalar.activation(out=v0, in_=v0, func=ACT.Copy, scale=mu[:, i : i + 1])
+            fused(v0, b_all[:], nu[:, i : i + 1], v0, MUL, ADD)
+            while x_dots_issued[0] < (i + 1) * T:
+                next_x_dot()
+            total = banks()
+            for t in range(T):
+                term = times_row_factor(g_tiles[i][:, t, :], a_scaled[:, i, t : t + 1])
+                add_turned(total, term, t == 0, t == T - 1)
+            return total
+
+        def inner_products(i, total):
+            for t in range(T):
+                dot(dots[:, i, 1, t : t + 1], g_tiles[i][:, t, :], mv_all[:, i, :], N)
+            turned_sums[i] = work.tile([P, N], F32, name="turned_sum", bufs=3)
+            out_of_psum(turned_sums[i], total)
+            s_b = psum.tile([P, BANK], F32, name="bank")
+            for k in range(BLOCKS):
+                nc.tensor.matmul(
+                    out=s_b[:, :B_COPIES],
+                    lhsT=turned_sums[i][:, k * P : (k + 1) * P],
+                    rhs=b_cols[:, k, :],
+                    start=(k == 0),
+                    stop=(k == BLOCKS - 1),
+                )
+            nc.vector.tensor_copy(out=inputs[:, i, 3:4], in_=s_b[:, 0:1])
+            terms = work.tile([P, 3, 2, T], F32, name="terms")
+            mul(terms[:], from_dots[:, :, :, i, :], dots[:, i].unsqueeze(1).to_broadcast([P, 3, 2, T]))
+            nc.vector.tensor_reduce(
+                out=inputs[:, i, 0:3], in_=terms[:], axis=mybir.AxisListType.XY, op=ADD
             )
-            add(
-                from_dots[:, 1],
-                mul(
-                    grid2("v_part_s"),
-                    fused(
-                        grid2("v_part"),
-                        to_v,
-                        2.0,
-                        mul(grid2("v_lost"), q_dir, both(mul(grid("q2_phi_q2s"), q2_phi, q2s))),
-                        MUL,
-                        SUB,
-                    ),
-                    both(s),
-                ),
-                mul(grid2("v_radial"), ds_v, both(coef_c3)),
+            kappa_terms = work.tile([P, 3, 4], F32, name="kappa_terms")
+            mul(kappa_terms[:], to_kappa[:, i], inputs[:, i].unsqueeze(1).to_broadcast([P, 3, 4]))
+            nc.vector.tensor_reduce(
+                out=kappa[:, i, :], in_=kappa_terms[:], axis=mybir.AxisListType.X, op=ADD
             )
 
-        for c in range(PASSES):
-            v_rows = stage.tile([P, PACK, K], BF16, name="rows")
-            nc.sync.dma_start(out=v_rows[:].rearrange("p j k -> p (j k)"), in_=v_view[c])
-            quantise_pass(v_rows[:], v_codes[:, c, :], v_scales[:, c, :], E4M3_X4)
+        def finish(i):
+            mix = banks()
+            for k, src in enumerate((x_all[:, i, :], mv_all[:, i, :], b_all[:])):
+                add_turned(mix, times_row_factor(src, kappa[:, i, k : k + 1]), k == 0, k == 2)
+            turned_mix = work.tile([P, N], F32, name="turned_mix")
+            out_of_psum(turned_mix, mix)
+            dmv = banks()
+            add_turned(dmv, turned_sums[i], True, False)
+            add_turned(dmv, turned_mix, False, True)
+            out_of_psum(d_rows[i // PACK][:, i % PACK, :], dmv)
 
-        with tc.tile_pool(name="work", bufs=2) as work:
-            for c in range(PASSES):
-                d_rows = stage.tile([P, PACK, N], BF16, name="rows")
-                for j in range(PACK):
-                    i = c * PACK + j
-                    g = grads.tile([P, T, N], BF16, name="g")
-                    nc.sync.dma_start(out=g[:].rearrange("p t n -> p (t n)"), in_=g_view[c, j])
+        for i in range(TILES + 1):
+            if i < TILES:
+                if i % PACK == 0:
+                    d_rows[i // PACK] = stage.tile([P, PACK, N], BF16, name="rows")
+                total = weighted_sum(i)
+            if i > 0:
+                finish(i - 1)
+            c = i - V_INIT_AT
+            if c == 0:
+                v_rows = grads.tile([P, PASSES, PACK, K], BF16, name="g")
+                nc.sync.dma_start(out=v_rows[:].rearrange("p c j k -> p c (j k)"), in_=v_view)
+            if 0 <= c < PASSES:
+                v_halves = regroup_pass(v_rows[:, c], nc.scalar.copy)
+            if i < TILES:
+                inner_products(i, total)
+            if 0 <= c < PASSES:
+                quantise_pass(v_halves, v_codes[:, c, :], v_scales[:, c, :], E4M3_X4)
+            if i > 0 and i % PACK == 0:
+                done = i // PACK - 1
+                d_halves = regroup_pass(d_rows[done][:], nc.vector.tensor_copy)
+                quantise_pass(d_halves, d_codes[:, done, :], d_scales[:, done, :], E5M2_X4)
 
-                    turned_sum = [psum.tile([P, BANK], F32, name="bank") for h in range(HALVES)]
-                    for t in range(T):
-                        weighted = work.tile([P, N], F32, name="weighted", bufs=4)
-                        nc.scalar.activation(
-                            out=weighted[:], in_=g[:, t, :], func=ACT.Copy, scale=a_scaled[:, i, t : t + 1]
-                        )
-                        for k in range(BLOCKS):
-                            h, q = divmod(k, BLOCKS_PER_BANK)
-                            nc.tensor.matmul(
-                                out=turned_sum[h][:, q * P : (q + 1) * P],
-                                lhsT=weighted[:, k * P : (k + 1) * P],
-                                rhs=identity[:],
-                                is_transpose=True,
-                                start=(t == 0 and q == 0),
-                                stop=(t == T - 1 and q == BLOCKS_PER_BANK - 1),
-                            )
-
-                    for t in range(T):
-                        dot(dots[:, i, 0, t : t + 1], g[:, t, :], x_all[:, i, :], N)
-                    for t in range(T):
-                        dot(dots[:, i, 1, t : t + 1], g[:, t, :], v0_all[:, i, :], N)
-
-                    turned = work.tile([P, N], F32, name="turned")
-                    for h in range(HALVES):
-                        nc.scalar.copy(out=turned[:, h * BANK : (h + 1) * BANK], in_=turned_sum[h][:])
-                    mu_s = [psum.tile([P, BANK], F32, name="bank") for h in range(HALVES)]
-                    for k in range(BLOCKS):
-                        h, q = divmod(k, BLOCKS_PER_BANK)
-                        nc.tensor.transpose(
-                            out=mu_s[h][:, q * P : (q + 1) * P],
-                            in_=turned[:, k * P : (k + 1) * P],
-                            identity=identity[:],
-                        )
-                    for h in range(HALVES):
-                        dot(inputs[:, i, 3 + h : 4 + h], b_all[:, h * BANK : (h + 1) * BANK], mu_s[h][:], BANK)
-
-                    terms = work.tile([P, 3, 2, T], F32, name="terms")
-                    mul(terms[:], from_dots[:, :, :, i, :], dots[:, i].unsqueeze(1).to_broadcast([P, 3, 2, T]))
-                    nc.vector.tensor_reduce(
-                        out=inputs[:, i, 0:3], in_=terms[:], axis=mybir.AxisListType.XY, op=ADD
+        for m in range(BLOCKS):
+            of_block = slice(m * P, (m + 1) * P)
+            result = work.tile([P, K], F32, name="scaled", bufs=4)
+            for h in range(K // BANK):
+                half = slice(h * BANK, (h + 1) * BANK)
+                acc = psum.tile([P, BANK], F32, name="bank")
+                for c in range(PASSES):
+                    nc.tensor.matmul_mx(
+                        out=acc[:],
+                        lhsT=d_codes[:, c, of_block].bitcast(E5M2_X4),
+                        lhsT_scale=d_scales[:, c, of_block],
+                        rhs=v_codes[:, c, half].bitcast(E4M3_X4),
+                        rhs_scale=v_scales[:, c, half],
+                        start=(c == 0),
+                        stop=(c == PASSES - 1),
                     )
-                    kappa_terms = work.tile([P, 3, 5], F32, name="kappa_terms")
-                    mul(kappa_terms[:], to_kappa[:, i], inputs[:, i].unsqueeze(1).to_broadcast([P, 3, 5]))
-                    nc.vector.tensor_reduce(
-                        out=kappa[:, i, :], in_=kappa_terms[:], axis=mybir.AxisListType.X, op=ADD
-                    )
-
-                    mix = work.tile([P, N], F32, name="mix")
-                    nc.scalar.activation(
-                        out=mix[:], in_=x_all[:, i, :], func=ACT.Copy, scale=kappa[:, i, 0:1]
-                    )
-                    fused(mix[:], v0_all[:, i, :], kappa[:, i, 1:2], mix[:], MUL, ADD)
-                    fused(mix[:], b_all[:], kappa[:, i, 2:3], mix[:], MUL, ADD)
-                    for h in range(HALVES):
-                        half = slice(h * BANK, (h + 1) * BANK)
-                        add(d_rows[:, j, half], mix[:, half], mu_s[h][:])
-                quantise_pass(d_rows[:], d_codes[:, c, :], d_scales[:, c, :], E5M2_X4)
-
-            for m in range(BLOCKS):
-                of_block = slice(m * P, (m + 1) * P)
-                result = work.tile([P, K], F32, name="result")
-                for h in range(K // BANK):
-                    half = slice(h * BANK, (h + 1) * BANK)
-                    acc = psum.tile([P, BANK], F32, name="bank")
-                    for c in range(PASSES):
-                        nc.tensor.matmul_mx(
-                            out=acc[:],
-                            lhsT=d_codes[:, c, of_block].bitcast(E5M2_X4),
-                            lhsT_scale=d_scales[:, c, of_block],
-                            rhs=v_codes[:, c, half].bitcast(E4M3_X4),
-                            rhs_scale=v_scales[:, c, half],
-                            start=(c == 0),
-                            stop=(c == PASSES - 1),
-                        )
-                    if h % 2 == 0:
-                        nc.scalar.copy(out=result[:, half], in_=acc[:])
-                    else:
-                        nc.vector.tensor_copy(out=result[:, half], in_=acc[:])
-                nc.sync.dma_start(out=out[of_block, :], in_=result[:])
+                if h % 2 == 0:
+                    nc.scalar.copy(out=result[:, half], in_=acc[:])
+                else:
+                    nc.vector.tensor_copy(out=result[:, half], in_=acc[:])
+            nc.sync.dma_start(out=out[of_block, :], in_=result[:])

@@ -62,21 +62,18 @@ def tile_paralleldirectpoincaredynamics_v_kernel(
         v_view = v_init.rearrange("(c p j) k -> p c (j k)", c=PASSES, p=P, j=PACK)
         g_view = grad_out.rearrange("(c p j) t n -> c j p (t n)", c=PASSES, p=P, j=PACK)
 
-        nc.sync.dma_start(out=b_all[:], in_=b.partition_broadcast(P))
-        for c in range(PASSES):
-            of_pass = slice(c * PACK, (c + 1) * PACK)
-            nc.sync.dma_start(
-                out=mv_all[:, of_pass, :].rearrange("p j n -> p (j n)"), in_=mv_view[c]
-            )
-            nc.sync.dma_start(
-                out=x_all[:, of_pass, :].rearrange("p j n -> p (j n)"), in_=z_view[c]
-            )
         with nc.allow_non_contiguous_dma(reason="one float32 a row: runs of 4 values"):
             nc.sync.dma_start(
                 out=vn_row[:].rearrange("p (c j) -> p c j", c=PASSES),
                 in_=vn.rearrange("(c p j) o -> p c (j o)", c=PASSES, p=P, j=PACK),
             )
             nc.sync.dma_start(out=logit[:], in_=step_sizes.partition_broadcast(P))
+        nc.sync.dma_start(out=b_all[:], in_=b.partition_broadcast(P))
+        for whole, view in ((mv_all, mv_view), (x_all, z_view)):
+            for c in range(PASSES):
+                nc.sync.dma_start(
+                    out=whole[:, c * PACK : (c + 1) * PACK, :].rearrange("p j n -> p (j n)"), in_=view[c]
+                )
 
         identity = keep.tile([P, P], F32, name="identity")
         masks.make_identity(nc, identity[:])
@@ -130,8 +127,6 @@ def tile_paralleldirectpoincaredynamics_v_kernel(
 
         def table(dst, a, func, s=1.0):
             nc.scalar.activation(out=dst, in_=a, func=func, scale=s)
-            for spare in range(2):
-                next_x_dot()
             return dst
 
         def dot(acc, a, b_, width):
@@ -165,17 +160,27 @@ def tile_paralleldirectpoincaredynamics_v_kernel(
                 )
 
         g_tiles = {}
-        x_dots_issued = [0]
+        xb = keep.tile([P, TILES], F32, name="xb")
+        xm = keep.tile([P, TILES], F32, name="xm")
+        ready_issued = [0]
 
-        def next_x_dot():
-            i, t = divmod(x_dots_issued[0], T)
-            x_dots_issued[0] += 1
-            if t == 0:
-                g_tiles[i] = grads.tile([P, T, N], BF16, name="g")
-                nc.sync.dma_start(
-                    out=g_tiles[i][:].rearrange("p t n -> p (t n)"), in_=g_view[i // PACK, i % PACK]
-                )
-            dot(dots[:, i, 0, t : t + 1], g_tiles[i][:, t, :], x_all[:, i, :], N)
+        def ready_dot():
+            n = ready_issued[0]
+            ready_issued[0] += 1
+            if n < 2 * TILES:
+                i = n // 2
+                if n % 2 == 0:
+                    dot(xb[:, i : i + 1], x_all[:, i, :], b_all[:], N)
+                else:
+                    dot(xm[:, i : i + 1], x_all[:, i, :], mv_all[:, i, :], N)
+            else:
+                i, t = divmod(n - 2 * TILES, T)
+                if t == 0:
+                    g_tiles[i] = grads.tile([P, T, N], BF16, name="g")
+                    nc.sync.dma_start(
+                        out=g_tiles[i][:].rearrange("p t n -> p (t n)"), in_=g_view[i // PACK, i % PACK]
+                    )
+                dot(dots[:, i, 0, t : t + 1], g_tiles[i][:, t, :], x_all[:, i, :], N)
 
         v_codes = keep.tile([P, PASSES, K], U32, name="v_codes", align_bytes=64)
         v_scales = keep.tile([P, PASSES, K], U8, name="v_scales", align_bytes=64)
@@ -239,9 +244,6 @@ def tile_paralleldirectpoincaredynamics_v_kernel(
         def grid(name):
             return chain.tile([P, TILES, T], F32, name=name)
 
-        def grid2(name):
-            return chain.tile([P, 2, TILES, T], F32, name=name)
-
         def pair(r):
             return r.unsqueeze(1).to_broadcast([P, 2, TILES])
 
@@ -251,42 +253,6 @@ def tile_paralleldirectpoincaredynamics_v_kernel(
         def over_tiles(h):
             return h.unsqueeze(1).to_broadcast([P, TILES, T])
 
-        def both(g):
-            return g.unsqueeze(1).to_broadcast([P, 2, TILES, T])
-
-        def both_over_t(r):
-            return r.unsqueeze(1).unsqueeze(3).to_broadcast([P, 2, TILES, T])
-
-        def projection(make, tag, norm_sq):
-            r = table(make(tag + "_r"), at_least(make(tag + "_c"), norm_sq, EPS_SQ), ACT.Sqrt)
-            on = above(make(tag + "_on"), r, MAX_NORM)
-            ir = inverse(make(tag + "_ir"), r)
-            excess = mul(make(tag + "_ex"), affine(make(tag + "_sc"), ir, MAX_NORM, -1.0), on)
-            pi = affine(make(tag + "_pi"), excess, 1.0, 1.0)
-            ir3 = mul(make(tag + "_ir3"), mul(make(tag + "_ir2"), ir, ir), ir)
-            phi = fused(make(tag + "_phi"), ir3, MAX_NORM, on, MUL, MUL)
-            return pi, phi
-
-        def radial_coefficient(make, tag, h, kr, ir, free):
-            slope = affine(make(tag + "_sl"), mul(make(tag + "_h2"), h, h), -1.0, 1.0)
-            top = sub(make(tag + "_top"), mul(make(tag + "_skr"), slope, kr), h)
-            ir3 = mul(make(tag + "_jr3"), mul(make(tag + "_jr2"), ir, ir), ir)
-            return mul(make(tag + "_cf"), mul(make(tag + "_q"), top, ir3), free)
-
-        bb = col("bb")
-        m2, mb, x2, xb, xm = row("m2"), row("mb"), row("x2"), row("xb"), row("xm")
-        square_sum(bb[:], b_all[:])
-        for i in range(TILES):
-            square_sum(m2[:, i : i + 1], mv_all[:, i, :])
-            square_sum(x2[:, i : i + 1], x_all[:, i, :])
-            dot(mb[:, i : i + 1], mv_all[:, i, :], b_all[:], N)
-            dot(xb[:, i : i + 1], x_all[:, i, :], b_all[:], N)
-            dot(xm[:, i : i + 1], x_all[:, i, :], mv_all[:, i, :], N)
-
-        rb = table(col("rb"), at_least(col("bb_c"), bb, EPS_SQ), ACT.Sqrt)
-        beta = mul(col("beta"), table(col("hb"), rb, ACT.Tanh), inverse(col("irb"), rb))
-        beta2 = scale(col("beta2"), beta, 2.0)
-        y2 = mul(col("y2"), mul(col("beta_bb"), beta, bb), beta)
 
         clipped = row("clipped")
         nc.vector.tensor_scalar(
@@ -297,186 +263,370 @@ def tile_paralleldirectpoincaredynamics_v_kernel(
             op0=mybir.AluOpType.max,
             op1=mybir.AluOpType.min,
         )
-        ratio = mul(
-            row("ratio"),
-            affine(row("one_plus"), clipped, 1.0, 1.0),
-            inverse(row("inv_one_minus"), affine(row("one_minus"), clipped, -1.0, 1.0)),
-        )
-        k1 = fused(
-            row("k1"), table(row("ln_ratio"), ratio, ACT.Ln), 0.5, inverse(row("ivn"), vn_row), MUL, MUL
-        )
+        ivn = inverse(row("ivn"), vn_row)
 
-        rm = table(row("rm"), at_least(row("m2_c"), m2, EPS_SQ), ACT.Sqrt)
+        one_minus = affine(row("one_minus"), clipped, -1.0, 1.0)
+
+        inv_one_minus = inverse(row("inv_one_minus"), one_minus)
+
+        ratio = fused(row("ratio"), clipped, 1.0, inv_one_minus, ADD, MUL)
+        ln_ratio = table(row("ln_ratio"), ratio, ACT.Ln)
+
+        bb = col("bb")
+        square_sum(bb, b_all[:])
+        bb_c = at_least(col("bb_c"), bb, EPS_SQ)
+        rb = table(col("rb"), bb_c, ACT.Sqrt)
+        hb = table(col("hb"), rb, ACT.Tanh)
+        half_tanh = table(col("half_tanh"), logit, ACT.Tanh, 0.5)
+
+        m2, mb, x2 = row("m2"), row("mb"), row("x2")
+        for i in range(TILES):
+            square_sum(m2[:, i : i + 1], mv_all[:, i, :])
+            dot(mb[:, i : i + 1], mv_all[:, i, :], b_all[:], N)
+        for spare in range(4):
+            ready_dot()
+
+        m2_c = at_least(row("m2_c"), m2, EPS_SQ)
+        free_m = above(row("free_m"), m2, EPS_SQ)
+        k1 = fused(row("k1"), ln_ratio, 0.5, ivn, MUL, MUL)
+        irb = inverse(col("irb"), rb)
+        step = affine(col("step"), half_tanh, 0.5, 0.5)
+        rm = table(row("rm"), m2_c, ACT.Sqrt)
+
+        beta = mul(col("beta"), hb, irb)
+        ct = scale(chain.tile([P, T], F32, name="ct"), horizon, step)
+        ready_dot()
+
+        beta2 = scale(col("beta2"), beta, 2.0)
+        beta_bb = mul(col("beta_bb"), beta, bb)
+        ct2 = mul(chain.tile([P, T], F32, name="ct2"), ct, ct)
+        ready_dot()
+
+        y2 = mul(col("y2"), beta_bb, beta)
+        ct3 = mul(chain.tile([P, T], F32, name="ct3"), ct2, ct)
+
         k1_rm = mul(row("k1_rm"), k1, rm)
-        hm = table(row("hm"), k1_rm, ACT.Tanh)
         irm = inverse(row("irm"), rm)
-        alpha = mul(row("alpha"), hm, irm)
-        alpha_m2 = mul(row("alpha_m2"), alpha, m2)
-        res2 = mul(row("res2"), alpha_m2, alpha)
-        res_b = scale(row("res_b"), mul(row("alpha_mb"), alpha, mb), beta)
+        hm = table(row("hm"), k1_rm, ACT.Tanh)
+        for i in range(TILES):
+            square_sum(x2[:, i : i + 1], x_all[:, i, :])
+        ready_dot()
+        ready_dot()
 
-        base = affine(row("base"), res_b, 2.0, 1.0)
+        alpha = mul(row("alpha"), hm, irm)
+        ready_dot()
+
+        alpha_m2 = mul(row("alpha_m2"), alpha, m2)
+        alpha_mb = mul(row("alpha_mb"), alpha, mb)
+        ready_dot()
+
+        res2 = mul(row("res2"), alpha_m2, alpha)
+        res_b2 = scale(row("res_b2"), alpha_mb, beta2)
+        ready_dot()
+
+        base = shift(row("base"), res_b2, 1.0)
+        a2 = affine(row("a2"), res2, -1.0, 1.0)
+        ready_dot()
+
         den0 = fused(row("den0"), res2, y2, base, MUL, ADD)
-        iden = inverse(row("iden"), at_least(row("den"), den0, EPS))
-        p1 = mul(row("p1"), shift(row("a1"), base, y2), iden)
-        p2 = mul(row("p2"), affine(row("a2"), res2, -1.0, 1.0), iden)
-        p_dir = row2("p_dir")
-        pa = mul(p_dir[:, 0, :], p1, alpha)
-        pb = scale(p_dir[:, 1, :], p2, beta)
-        p_mv = add(row("p_mv"), mul(row("pa_m2"), pa, m2), mul(row("pb_mb"), pb, mb))
-        p_b = fused(row("p_b"), pb, bb, mul(row("pa_mb"), pa, mb), MUL, ADD)
-        pp = add(row("pp"), mul(row("pa_pmv"), pa, p_mv), mul(row("pb_pb"), pb, p_b))
-        pi, phi = projection(row, "p", pp)
+        a1 = shift(row("a1"), base, y2)
+        ready_dot()
+
+        den = at_least(row("den"), den0, EPS)
+        live = above(row("live"), den0, EPS)
+        ready_dot()
+
+        iden = inverse(row("iden"), den)
+        ready_dot()
+
+        p1 = mul(row("p1"), a1, iden)
+        p2 = mul(row("p2"), a2, iden)
+        ready_dot()
+
+        pa = mul(row("pa"), p1, alpha)
+        pb = scale(row("pb"), p2, beta)
+        ready_dot()
+
+        pa_m2 = mul(row("pa_m2"), pa, m2)
+        pb_mb = mul(row("pb_mb"), pb, mb)
+        pa_mb = mul(row("pa_mb"), pa, mb)
+        ready_dot()
+
+        p_mv = add(row("p_mv"), pa_m2, pb_mb)
+        p_b = fused(row("p_b"), pb, bb, pa_mb, MUL, ADD)
+        ready_dot()
+
+        pa_pmv = mul(row("pa_pmv"), pa, p_mv)
+        pb_pb = mul(row("pb_pb"), pb, p_b)
+        gap = affine(row("gap"), x2, -1.0, 1.0)
+        ready_dot()
+
+        pp = add(row("pp"), pa_pmv, pb_pb)
+        gap_c = at_least(row("gap_c"), gap, EPS)
+        ready_dot()
+
+        pp_c = at_least(row("pp_c"), pp, TINY)
+        on_p = above(row("on_p"), pp, MAX_NORM * MAX_NORM)
+        k2 = inverse(row("k2"), gap_c)
+        rp_raw = table(row("rp_raw"), pp_c, ACT.Sqrt)
+        while ready_issued[0] < 2 * TILES:
+            ready_dot()
+
+        rp = at_least(row("rp"), rp_raw, EPS)
+
+        irp = inverse(row("irp"), rp)
+
+        shrink = fused(row("shrink"), irp, MAX_NORM, on_p, MUL, MUL)
+        irp2 = mul(row("irp2"), irp, irp)
+
+        pi = fused(row("pi"), shrink, 1.0, on_p, ADD, SUB)
+        phi = mul(row("phi"), shrink, irp2)
 
         mul(mu, pi, pa)
         mul(nu, pi, pb)
-        vv = mul(row("vv"), mul(row("pi_sq"), pi, pi), pp)
-        xv = add(row("xv"), mul(row("mu_xm"), mu, xm), mul(row("nu_xb"), nu, xb))
-        vb = add(row("vb"), mul(row("mu_mb"), mu, mb), scale(row("nu_bb"), nu, bb))
+        r0 = mul(row("r0"), pi, rp_raw)
+        pi_sq = mul(row("pi_sq"), pi, pi)
 
-        step = affine(col("step"), table(col("half_tanh"), logit, ACT.Tanh, 0.5), 0.5, 0.5)
-        ct = scale(chain.tile([P, T], F32, name="ct"), horizon, step)
-        ct3 = mul(chain.tile([P, T], F32, name="ct3"), mul(chain.tile([P, T], F32, name="ct2"), ct, ct), ct)
-        gap = affine(row("gap"), x2, -1.0, 1.0)
-        k2 = inverse(row("k2"), at_least(row("gap_c"), gap, EPS))
-        r0 = table(row("r0"), at_least(row("vv_c"), vv, TINY), ACT.Sqrt)
         c_r0 = mul(grid("c_r0"), over_t(r0), over_tiles(ct))
+        vv = mul(row("vv"), pi_sq, pp)
+        mu_xm = mul(row("mu_xm"), mu, xm)
+        nu_xb = mul(row("nu_xb"), nu, xb)
+
         rt = at_least(grid("rt"), c_r0, EPS)
+        free_t = above(grid("free_t"), c_r0, EPS)
+        xv = add(row("xv"), mu_xm, nu_xb)
+
         k2_rt = mul(grid("k2_rt"), rt, over_t(k2))
-        ht = table(grid("ht"), k2_rt, ACT.Tanh)
         irt = inverse(grid("irt"), rt)
-        s = mul(grid("s"), mul(grid("sigma"), ht, irt), over_tiles(ct))
+        ht = table(grid("ht"), k2_rt, ACT.Tanh)
+        ready_dot()
+        ready_dot()
+
+        sigma = mul(grid("sigma"), ht, irt)
+
+        s = mul(grid("s"), sigma, over_tiles(ct))
+
         x_sec = mul(grid("x_sec"), s, over_t(xv))
-        sec2 = mul(grid("sec2"), mul(grid("s_vv"), s, over_t(vv)), s)
+        s_vv = mul(grid("s_vv"), s, over_t(vv))
+
         base_t = affine(grid("base_t"), x_sec, 2.0, 1.0)
-        den0_t = add(grid("den0_t"), mul(grid("x2_sec2"), sec2, over_t(x2)), base_t)
-        iden_t = inverse(grid("iden_t"), at_least(grid("den_t"), den0_t, EPS))
-        q_dir = grid2("q_dir")
-        q1 = mul(q_dir[:, 0], add(grid("b1"), base_t, sec2), iden_t)
+        sec2 = mul(grid("sec2"), s_vv, s)
+
+        x2_sec2 = mul(grid("x2_sec2"), sec2, over_t(x2))
+        b1 = add(grid("b1"), base_t, sec2)
+
+        den0_t = add(grid("den0_t"), x2_sec2, base_t)
+
+        den_t = at_least(grid("den_t"), den0_t, EPS)
+        live_t = above(grid("live_t"), den0_t, EPS)
+
+        iden_t = inverse(grid("iden_t"), den_t)
+
+        q1 = mul(grid("q1"), b1, iden_t)
         q2 = mul(grid("q2"), iden_t, over_t(gap))
-        q2s = mul(q_dir[:, 1], q2, s)
-        q_x = add(grid("q_x"), mul(grid("q1_x2"), q1, over_t(x2)), mul(grid("q2_xsec"), q2, x_sec))
-        q_v = add(grid("q_v"), mul(grid("q1_xv"), q1, over_t(xv)), mul(grid("q2s_vv"), q2s, over_t(vv)))
-        qq = add(grid("qq"), mul(grid("q1_qx"), q1, q_x), mul(grid("q2s_qv"), q2s, q_v))
-        pi_q, phi_q = projection(grid, "q", qq)
+
+        q2s = mul(grid("q2s"), q2, s)
+        q1_x2 = mul(grid("q1_x2"), q1, over_t(x2))
+        q2_xsec = mul(grid("q2_xsec"), q2, x_sec)
+        q1_xv = mul(grid("q1_xv"), q1, over_t(xv))
+
+        q_x = add(grid("q_x"), q1_x2, q2_xsec)
+        q2s_vv = mul(grid("q2s_vv"), q2s, over_t(vv))
+
+        q_v = add(grid("q_v"), q1_xv, q2s_vv)
+        q1_qx = mul(grid("q1_qx"), q1, q_x)
+
+        q2s_qv = mul(grid("q2s_qv"), q2s, q_v)
+
+        qq = add(grid("qq"), q1_qx, q2s_qv)
+
+        qq_c = at_least(grid("qq_c"), qq, EPS_SQ)
+        on_q = above(grid("on_q"), qq, MAX_NORM * MAX_NORM)
+        rq = table(grid("rq"), qq_c, ACT.Sqrt)
+        ready_dot()
+        ready_dot()
+
+        irq = inverse(grid("irq"), rq)
+
+        shrink_q = fused(grid("shrink_q"), irq, MAX_NORM, on_q, MUL, MUL)
+        irq2 = mul(grid("irq2"), irq, irq)
+
+        pi_q = fused(grid("pi_q"), shrink_q, 1.0, on_q, ADD, SUB)
+        phi_q = mul(grid("phi_q"), shrink_q, irq2)
 
         a_t = mul(from_dots[:, 2, 1], q2s, pi_q)
-        mul(a_scaled[:], a_t, over_t(mu))
         nc.vector.memset(from_dots[:, 2, 0], 0.0)
 
-        dp_mv = mul(row2("dp_mv"), p_dir, pair(fused(row("n_phi_pmv"), phi, -1.0, p_mv, MUL, MUL)))
-        add(dp_mv[:, 0, :], dp_mv[:, 0, :], pi)
-        dp_b = mul(row2("dp_b"), p_dir, pair(fused(row("n_phi_pb"), phi, -1.0, p_b, MUL, MUL)))
-        add(dp_b[:, 1, :], dp_b[:, 1, :], pi)
-        dp_p = mul(row2("dp_p"), p_dir, pair(sub(row("pi_phi_pp"), pi, mul(row("phi_pp"), phi, pp))))
-        d_a = mul(row2("d_a"), dp_mv, pair(mul(row("iden_alpha"), iden, alpha)))
-        d_b = mul(row2("d_b"), dp_b, pair(scale(row("iden_beta"), iden, beta)))
-        live = fused(row("n_live_iden"), above(row("live"), den0, EPS), -1.0, iden, MUL, MUL)
-        d_d = mul(row2("d_d"), dp_p, pair(live))
-        to_b = add(row2("to_b"), d_a, d_d)
-        to_res = fused(row2("to_res"), d_d, y2, d_b, MUL, SUB)
-        dres_mv = add(
-            row2("dres_mv"),
-            add(
-                row2("dres_mv2"),
-                mul(row2("dres_mv_a"), dp_mv, pair(p1)),
-                mul(row2("dres_mv_b"), to_b, pair(scale(row("beta2_mb"), mb, beta2))),
-            ),
-            mul(row2("dres_mv_c"), to_res, pair(scale(row("alpha_m2_2"), alpha_m2, 2.0))),
-        )
-        coef_m = radial_coefficient(row, "m", hm, k1_rm, irm, above(row("free_m"), m2, EPS_SQ))
+        mul(a_scaled[:], a_t, over_t(mu))
+
+        phi_qq = mul(grid("phi_qq"), phi_q, qq)
+        phi_qx = mul(grid("phi_qx"), phi_q, q_x)
+        q2_phi = mul(grid("q2_phi"), q2, phi_q)
+        iden_pi = mul(grid("iden_pi"), iden_t, pi_q)
+        ht2 = mul(grid("ht2"), ht, ht)
+        irt2 = mul(grid("irt2"), irt, irt)
+        xv_svv = add(grid("xv_svv"), s_vv, over_t(xv))
+        q2_pi = mul(grid("q2_pi"), q2, pi_q)
+
+        keep_q = sub(grid("keep_q"), pi_q, phi_qq)
+        lost_x = mul(grid("lost_x"), q2_phi, q1)
+        lost_v = mul(grid("lost_v"), q2_phi, q2s)
+        lost_qv = mul(grid("lost_qv"), q2_phi, q_v)
+        s_iden_pi = mul(grid("s_iden_pi"), s, iden_pi)
+        slope_t = affine(grid("slope_t"), ht2, -1.0, 1.0)
+        irt3 = mul(grid("irt3"), irt2, irt)
+
+        live_keep = mul(grid("live_keep"), live_t, keep_q)
+        slope_kr = mul(grid("slope_kr"), slope_t, k2_rt)
+        free_irt3 = mul(grid("free_irt3"), irt3, free_t)
+        iden_pi_sum = mul(grid("iden_pi_sum"), iden_pi, xv_svv)
+        ss_iden_pi = mul(grid("ss_iden_pi"), s, s_iden_pi)
+
+        on_x_sum = add(grid("on_x_sum"), phi_qx, live_keep)
+        x2_live_keep = mul(grid("x2_live_keep"), live_keep, over_t(x2))
+        top_t = sub(grid("top_t"), slope_kr, ht)
+        free_c3 = mul(grid("free_c3"), free_irt3, over_tiles(ct3))
+
+        on_x = mul(grid("on_x"), iden_t, on_x_sum)
+        on_sec_sum = add(grid("on_sec_sum"), phi_qx, x2_live_keep)
+        coef_c3 = mul(grid("coef_c3"), top_t, free_c3)
+
+        on_sec = mul(grid("on_sec"), iden_t, on_sec_sum)
+        x_c_half = fused(grid("x_c_half"), on_x, 2.0, lost_x, MUL, ADD)
+        on_x_xv = mul(grid("on_x_xv"), on_x, over_t(xv))
+        v_b = mul(grid("v_b"), coef_c3, q2_pi)
+        coef_a = mul(grid("coef_a"), coef_c3, iden_pi_sum)
+
+        s_on_sec = mul(grid("s_on_sec"), s, on_sec)
+        x_c = fused(grid("x_c"), x_c_half, -1.0, s, MUL, MUL)
+        v_a_half = add(grid("v_a_half"), ss_iden_pi, coef_a)
+
+        v_c_first = fused(grid("v_c_first"), s_on_sec, 2.0, lost_v, MUL, ADD)
+        s_on_sec_vv = mul(grid("s_on_sec_vv"), s_on_sec, over_t(vv))
+        x_c_q1 = mul(grid("x_c_q1"), x_c, q1)
+        mul(from_dots[:, 0, 1], x_c, q2s)
+
+        s_v_c_first = mul(grid("s_v_c_first"), s, v_c_first)
+        ds_v_c_half = add(grid("ds_v_c_half"), on_x_xv, s_on_sec_vv)
+        fused(from_dots[:, 0, 0], s_iden_pi, 2.0, x_c_q1, MUL, ADD)
+
+        ds_v_c = fused(grid("ds_v_c"), ds_v_c_half, 2.0, lost_qv, MUL, ADD)
+
+        phi_pp = mul(row("phi_pp"), phi, pp)
+        iden_alpha = mul(row("iden_alpha"), iden, alpha)
+        iden_beta = scale(row("iden_beta"), iden, beta)
+        phi_pmv = mul(row("phi_pmv"), phi, p_mv)
+        phi_pb = mul(row("phi_pb"), phi, p_b)
+
+        coef_ds_v_c = mul(grid("coef_ds_v_c"), coef_c3, ds_v_c)
+        beta2_mb = scale(row("beta2_mb"), mb, beta2)
+        alpha2_m2 = scale(row("alpha2_m2"), alpha_m2, 2.0)
+        hm2 = mul(row("hm2"), hm, hm)
+        irm2 = mul(row("irm2"), irm, irm)
+
+        v_c = fused(grid("v_c"), s_v_c_first, -1.0, coef_ds_v_c, MUL, SUB)
         lost = mul(row("lost"), pa, phi)
-        on_both = chain.tile([P, 2, 2, TILES], F32, name="on_both")
-        sub(
-            on_both[:, 0],
-            add(
-                row2("on_mv2"),
-                mul(row2("on_mv_a"), to_res, pair(fused(row("alpha_sq2"), alpha, 2.0, alpha, MUL, MUL))),
-                mul(row2("on_mv_b"), dres_mv, pair(coef_m)),
-            ),
-            mul(row2("on_mv_c"), p_dir, pair(mul(row("lost_pa"), lost, pa))),
-        )
-        sub(
-            on_both[:, 1],
-            mul(row2("on_b_a"), to_b, pair(scale(row("alpha_beta2"), alpha, beta2))),
-            mul(row2("on_b_c"), p_dir, pair(mul(row("lost_pb"), lost, pb))),
-        )
+        alpha_sq2 = fused(row("alpha_sq2"), alpha, 2.0, alpha, MUL, MUL)
+        alpha_beta2 = scale(row("alpha_beta2"), alpha, beta2)
         imu = inverse(row("imu"), mu)
+
+        v_c_q1 = mul(grid("v_c_q1"), v_c, q1)
+        v_c_q2s = mul(grid("v_c_q2s"), v_c, q2s)
+        keep_p = sub(row("keep_p"), pi, phi_pp)
+        a_first = mul(row("a_first"), iden_alpha, pi)
+        b_first = mul(row("b_first"), iden_beta, pi)
+
+        fused(from_dots[:, 1, 0], v_a_half, 2.0, v_c_q1, MUL, ADD)
+        add(from_dots[:, 1, 1], v_c_q2s, v_b)
+        alpha_phi_pmv = mul(row("alpha_phi_pmv"), alpha, phi_pmv)
+        beta_phi_pb = scale(row("beta_phi_pb"), phi_pb, beta)
+        slope_m = affine(row("slope_m"), hm2, -1.0, 1.0)
+        irm3 = mul(row("irm3"), irm2, irm)
+
+        live_keep_p = mul(row("live_keep_p"), live, keep_p)
+        lost_pa = mul(row("lost_pa"), lost, pa)
+        lost_pb = mul(row("lost_pb"), lost, pb)
+        p1_phi_pmv = mul(row("p1_phi_pmv"), p1, phi_pmv)
+        p1_pi = mul(row("p1_pi"), p1, pi)
+
+        to_b_sum = add(row("to_b_sum"), alpha_phi_pmv, live_keep_p)
+        y2_live_keep_p = scale(row("y2_live_keep_p"), live_keep_p, y2)
+        slope_km = mul(row("slope_km"), slope_m, k1_rm)
+        free_irm3 = mul(row("free_irm3"), irm3, free_m)
+        mb_a_first = mul(row("mb_a_first"), beta2_mb, a_first)
+        m2_b_first = mul(row("m2_b_first"), alpha2_m2, b_first)
+
+        to_b_c = mul(row("to_b_c"), iden, to_b_sum)
+        to_res_sum = sub(row("to_res_sum"), y2_live_keep_p, beta_phi_pb)
+        top_m = sub(row("top_m"), slope_km, hm)
+        on_b_a = mul(row("on_b_a"), alpha_beta2, a_first)
+        sq_b_first = mul(row("sq_b_first"), alpha_sq2, b_first)
+        dres_a = add(row("dres_a"), p1_pi, mb_a_first)
+
+        to_res_c = mul(row("to_res_c"), iden, to_res_sum)
+        coef_m = mul(row("coef_m"), top_m, free_irm3)
+        mb_to_b_c = mul(row("mb_to_b_c"), beta2_mb, to_b_c)
+        ab_to_b_c = mul(row("ab_to_b_c"), alpha_beta2, to_b_c)
+
+        m2_to_res_c = mul(row("m2_to_res_c"), alpha2_m2, to_res_c)
+        sq_to_res_c = mul(row("sq_to_res_c"), alpha_sq2, to_res_c)
+        dres_c_part = add(row("dres_c_part"), p1_phi_pmv, mb_to_b_c)
+        on_b_c = add(row("on_b_c"), ab_to_b_c, lost_pb)
+        on_mv_a = mul(row("on_mv_a"), coef_m, dres_a)
+        coef_dres_b = mul(row("coef_dres_b"), coef_m, m2_b_first)
+
+        dres_c = add(row("dres_c"), dres_c_part, m2_to_res_c)
+        on_mv_c_part = add(row("on_mv_c_part"), sq_to_res_c, lost_pa)
+        on_mv_b = add(row("on_mv_b"), coef_dres_b, sq_b_first)
+        on_b_c_pa = mul(row("on_b_c_pa"), on_b_c, pa)
+
+        coef_dres_c = mul(row("coef_dres_c"), coef_m, dres_c)
+        on_both = chain.tile([P, 2, 2, TILES], F32, name="on_both")
+        sub(on_both[:, 1, 0, :], on_b_a, on_b_c_pa)
+        fused(on_both[:, 1, 1, :], on_b_c, -1.0, pb, MUL, MUL)
+        mu_mb = mul(row("mu_mb"), mu, mb)
+        nu_bb = scale(row("nu_bb"), nu, bb)
+
+        on_mv_c = add(row("on_mv_c"), coef_dres_c, on_mv_c_part)
+        vb = add(row("vb"), mu_mb, nu_bb)
+        nc.vector.memset(to_kappa[:], 0.0)
+
+        on_mv_c_pa = mul(row("on_mv_c_pa"), on_mv_c, pa)
+        on_mv_c_pb = mul(row("on_mv_c_pb"), on_mv_c, pb)
+        nc.vector.tensor_copy(out=to_kappa[:, :, 0, 0], in_=mu)
+
+        sub(on_both[:, 0, 0, :], on_mv_a, on_mv_c_pa)
+        fused(on_both[:, 0, 1, :], on_mv_c_pb, -1.0, on_mv_b, MUL, SUB)
+
         in_v0_b = chain.tile([P, 2, 2, TILES], F32, name="in_v0_b")
         mul(in_v0_b[:, :, 0, :], on_both[:, :, 0, :], pair(imu))
-        sub(in_v0_b[:, :, 1, :], on_both[:, :, 1, :], mul(row2("nu_first"), in_v0_b[:, :, 0, :], pair(nu)))
+
+        nu_first = mul(row2("nu_first"), in_v0_b[:, :, 0, :], pair(nu))
+
+        sub(in_v0_b[:, :, 1, :], on_both[:, :, 1, :], nu_first)
+
         weights = chain.tile([P, 2, 2, TILES], F32, name="weights")
         mul(weights[:, 0], in_v0_b[:, 0], pair(imu))
-        sub(weights[:, 1], in_v0_b[:, 1], mul(row2("nu_on_v0"), weights[:, 0], pair(nu)))
-        nc.vector.memset(to_kappa[:], 0.0)
-        nc.vector.tensor_copy(out=to_kappa[:, :, 0, 0], in_=mu)
+
+        nu_on_v0 = mul(row2("nu_on_v0"), weights[:, 0], pair(nu))
+
+        sub(weights[:, 1], in_v0_b[:, 1], nu_on_v0)
 
         def kappa_column(m):
             return to_kappa[:, :, 1:3, m].rearrange("p i k -> p k i")
 
         w_v0, w_b = weights[:, :, 0, :], weights[:, :, 1, :]
-        add(kappa_column(0), mul(row2("kx_a"), w_v0, pair(xv)), mul(row2("kx_b"), w_b, pair(xb)))
-        add(kappa_column(1), mul(row2("kv_a"), w_v0, pair(vv)), mul(row2("kv_b"), w_b, pair(vb)))
-        add(to_kappa[:, :, 1, 1], to_kappa[:, :, 1, 1], mu)
+        kx_a = mul(row2("kx_a"), w_v0, pair(xv))
+        kx_b = mul(row2("kx_b"), w_b, pair(xb))
+        kv_a = mul(row2("kv_a"), w_v0, pair(vv))
+        kv_b = mul(row2("kv_b"), w_b, pair(vb))
         nc.vector.tensor_copy(out=kappa_column(2), in_=w_v0)
         mul(kappa_column(3), w_b, pair(imu))
 
-        dq_x = mul(grid2("dq_x"), q_dir, both(fused(grid("n_phi_qx"), phi_q, -1.0, q_x, MUL, MUL)))
-        add(dq_x[:, 0], dq_x[:, 0], pi_q)
-        dq_v = mul(grid2("dq_v"), q_dir, both(fused(grid("n_phi_qv"), phi_q, -1.0, q_v, MUL, MUL)))
-        add(dq_v[:, 1], dq_v[:, 1], pi_q)
-        dq_q = mul(grid2("dq_q"), q_dir, both(sub(grid("pi_phi_qq"), pi_q, mul(grid("phi_qq"), phi_q, qq))))
-        e_a = mul(grid2("e_a"), dq_x, both(iden_t))
-        live_t = fused(grid("n_live_t"), above(grid("live_t"), den0_t, EPS), -1.0, iden_t, MUL, MUL)
-        e_d = mul(grid2("e_d"), dq_q, both(live_t))
-        to_x = add(grid2("to_x"), e_a, e_d)
-        to_v = mul(
-            grid2("to_v"), add(grid2("to_sec"), mul(grid2("e_d_x2"), e_d, both_over_t(x2)), e_a), both(s)
-        )
-        ds_v = fused(
-            grid2("ds_v"),
-            add(
-                grid2("ds_v_half"),
-                mul(grid2("to_x_xv"), to_x, both_over_t(xv)),
-                mul(grid2("to_v_vv"), to_v, both_over_t(vv)),
-            ),
-            2.0,
-            mul(grid2("q2_dqv"), dq_v, both(q2)),
-            MUL,
-            ADD,
-        )
-        coef_t = radial_coefficient(grid, "t", ht, k2_rt, irt, above(grid("free_t"), c_r0, EPS))
-        coef_c3 = mul(grid("coef_c3"), coef_t, over_tiles(ct3))
-        q2_phi = mul(grid("q2_phi"), q2, phi_q)
-        mul(
-            from_dots[:, 0],
-            fused(
-                grid2("x_part"),
-                to_x,
-                2.0,
-                mul(grid2("x_lost"), q_dir, both(mul(grid("q2_phi_q1"), q2_phi, q1))),
-                MUL,
-                SUB,
-            ),
-            both(s),
-        )
-        add(
-            from_dots[:, 1],
-            mul(
-                grid2("v_part_s"),
-                fused(
-                    grid2("v_part"),
-                    to_v,
-                    2.0,
-                    mul(grid2("v_lost"), q_dir, both(mul(grid("q2_phi_q2s"), q2_phi, q2s))),
-                    MUL,
-                    SUB,
-                ),
-                both(s),
-            ),
-            mul(grid2("v_radial"), ds_v, both(coef_c3)),
-        )
+        add(kappa_column(0), kx_a, kx_b)
+        add(kappa_column(1), kv_a, kv_b)
 
+        add(to_kappa[:, :, 1, 1], to_kappa[:, :, 1, 1], mu)
 
         turned_sums = {}
         d_rows = {}
@@ -485,8 +635,8 @@ def tile_paralleldirectpoincaredynamics_v_kernel(
             v0 = mv_all[:, i, :]
             nc.scalar.activation(out=v0, in_=v0, func=ACT.Copy, scale=mu[:, i : i + 1])
             fused(v0, b_all[:], nu[:, i : i + 1], v0, MUL, ADD)
-            while x_dots_issued[0] < (i + 1) * T:
-                next_x_dot()
+            while ready_issued[0] < 2 * TILES + (i + 1) * T:
+                ready_dot()
             total = banks()
             for t in range(T):
                 term = times_row_factor(g_tiles[i][:, t, :], a_scaled[:, i, t : t + 1])

@@ -63,17 +63,18 @@ def tile_paralleldirectpoincaredynamics_v_kernel(
         g_view = grad_out.rearrange("(c p j) t n -> c j p (t n)", c=PASSES, p=P, j=PACK)
 
         with nc.allow_non_contiguous_dma(reason="one float32 a row: runs of 4 values"):
-            nc.sync.dma_start(
+            nc.scalar.dma_start(
                 out=vn_row[:].rearrange("p (c j) -> p c j", c=PASSES),
                 in_=vn.rearrange("(c p j) o -> p c (j o)", c=PASSES, p=P, j=PACK),
             )
-            nc.sync.dma_start(out=logit[:], in_=step_sizes.partition_broadcast(P))
-        nc.sync.dma_start(out=b_all[:], in_=b.partition_broadcast(P))
-        for whole, view in ((mv_all, mv_view), (x_all, z_view)):
-            for c in range(PASSES):
-                nc.sync.dma_start(
-                    out=whole[:, c * PACK : (c + 1) * PACK, :].rearrange("p j n -> p (j n)"), in_=view[c]
-                )
+            nc.scalar.dma_start(out=logit[:], in_=step_sizes.partition_broadcast(P))
+        nc.scalar.dma_start(out=b_all[:], in_=b.partition_broadcast(P))
+        for j in range(PACK):
+            nc.sync.dma_start(out=mv_all[:, j, :], in_=mv_view[0][:, j * N : (j + 1) * N])
+        for whole, view, c in ((mv_all, mv_view, 1), (x_all, z_view, 0), (x_all, z_view, 1)):
+            nc.sync.dma_start(
+                out=whole[:, c * PACK : (c + 1) * PACK, :].rearrange("p j n -> p (j n)"), in_=view[c]
+            )
 
         identity = keep.tile([P, P], F32, name="identity")
         masks.make_identity(nc, identity[:])
@@ -173,7 +174,7 @@ def tile_paralleldirectpoincaredynamics_v_kernel(
                     dot(xb[:, i : i + 1], x_all[:, i, :], b_all[:], N)
                 else:
                     dot(xm[:, i : i + 1], x_all[:, i, :], mv_all[:, i, :], N)
-            else:
+            elif n < 2 * TILES + TILES * T:
                 i, t = divmod(n - 2 * TILES, T)
                 if t == 0:
                     g_tiles[i] = grads.tile([P, T, N], BF16, name="g")
@@ -201,17 +202,19 @@ def tile_paralleldirectpoincaredynamics_v_kernel(
         def banks():
             return [psum.tile([P, BANK], F32, name="bank") for h in range(HALVES)]
 
-        def add_turned(total, term, first, last):
-            for k in range(BLOCKS):
-                h, q = divmod(k, BLOCKS_PER_BANK)
-                nc.tensor.matmul(
-                    out=total[h][:, q * P : (q + 1) * P],
-                    lhsT=term[:, k * P : (k + 1) * P],
-                    rhs=identity[:],
-                    is_transpose=True,
-                    start=(first and q == 0),
-                    stop=(last and q == BLOCKS_PER_BANK - 1),
-                )
+        def add_turned(total, terms, first, last):
+            for h in range(HALVES):
+                for m, term in enumerate(terms):
+                    for q in range(BLOCKS_PER_BANK):
+                        k = h * BLOCKS_PER_BANK + q
+                        nc.tensor.matmul(
+                            out=total[h][:, q * P : (q + 1) * P],
+                            lhsT=term[:, k * P : (k + 1) * P],
+                            rhs=identity[:],
+                            is_transpose=True,
+                            start=(first and m == 0 and q == 0),
+                            stop=(last and m == len(terms) - 1 and q == BLOCKS_PER_BANK - 1),
+                        )
 
         def out_of_psum(dst, total):
             for h in range(HALVES):
@@ -225,7 +228,7 @@ def tile_paralleldirectpoincaredynamics_v_kernel(
         b_f32 = work.tile([P, N], F32, name="scaled", bufs=4)
         nc.vector.tensor_copy(out=b_f32[:], in_=b_all[:])
         b_turned = banks()
-        add_turned(b_turned, b_f32, True, True)
+        add_turned(b_turned, [b_f32], True, True)
         for h in range(HALVES):
             nc.scalar.copy(
                 out=b_cols[:, h * BLOCKS_PER_BANK : (h + 1) * BLOCKS_PER_BANK, :],
@@ -273,59 +276,55 @@ def tile_paralleldirectpoincaredynamics_v_kernel(
         ln_ratio = table(row("ln_ratio"), ratio, ACT.Ln)
 
         bb = col("bb")
-        square_sum(bb, b_all[:])
-        bb_c = at_least(col("bb_c"), bb, EPS_SQ)
-        rb = table(col("rb"), bb_c, ACT.Sqrt)
-        hb = table(col("hb"), rb, ACT.Tanh)
-        half_tanh = table(col("half_tanh"), logit, ACT.Tanh, 0.5)
-
         m2, mb, x2 = row("m2"), row("mb"), row("x2")
+        square_sum(bb, b_all[:])
         for i in range(TILES):
             square_sum(m2[:, i : i + 1], mv_all[:, i, :])
             dot(mb[:, i : i + 1], mv_all[:, i, :], b_all[:], N)
-        for spare in range(4):
+        for spare in range(2):
             ready_dot()
 
         m2_c = at_least(row("m2_c"), m2, EPS_SQ)
+        bb_c = at_least(col("bb_c"), bb, EPS_SQ)
         free_m = above(row("free_m"), m2, EPS_SQ)
         k1 = fused(row("k1"), ln_ratio, 0.5, ivn, MUL, MUL)
-        irb = inverse(col("irb"), rb)
-        step = affine(col("step"), half_tanh, 0.5, 0.5)
         rm = table(row("rm"), m2_c, ACT.Sqrt)
-
-        beta = mul(col("beta"), hb, irb)
-        ct = scale(chain.tile([P, T], F32, name="ct"), horizon, step)
+        rb = table(col("rb"), bb_c, ACT.Sqrt)
         ready_dot()
-
-        beta2 = scale(col("beta2"), beta, 2.0)
-        beta_bb = mul(col("beta_bb"), beta, bb)
-        ct2 = mul(chain.tile([P, T], F32, name="ct2"), ct, ct)
         ready_dot()
-
-        y2 = mul(col("y2"), beta_bb, beta)
-        ct3 = mul(chain.tile([P, T], F32, name="ct3"), ct2, ct)
 
         k1_rm = mul(row("k1_rm"), k1, rm)
         irm = inverse(row("irm"), rm)
+        irb = inverse(col("irb"), rb)
         hm = table(row("hm"), k1_rm, ACT.Tanh)
+        hb = table(col("hb"), rb, ACT.Tanh)
+        half_tanh = table(col("half_tanh"), logit, ACT.Tanh, 0.5)
         for i in range(TILES):
             square_sum(x2[:, i : i + 1], x_all[:, i, :])
         ready_dot()
         ready_dot()
 
         alpha = mul(row("alpha"), hm, irm)
+        beta = mul(col("beta"), hb, irb)
+        step = affine(col("step"), half_tanh, 0.5, 0.5)
         ready_dot()
 
         alpha_m2 = mul(row("alpha_m2"), alpha, m2)
         alpha_mb = mul(row("alpha_mb"), alpha, mb)
+        beta2 = scale(col("beta2"), beta, 2.0)
+        beta_bb = mul(col("beta_bb"), beta, bb)
+        ct = scale(chain.tile([P, T], F32, name="ct"), horizon, step)
         ready_dot()
 
         res2 = mul(row("res2"), alpha_m2, alpha)
         res_b2 = scale(row("res_b2"), alpha_mb, beta2)
+        y2 = mul(col("y2"), beta_bb, beta)
+        ct2 = mul(chain.tile([P, T], F32, name="ct2"), ct, ct)
         ready_dot()
 
         base = shift(row("base"), res_b2, 1.0)
         a2 = affine(row("a2"), res2, -1.0, 1.0)
+        ct3 = mul(chain.tile([P, T], F32, name="ct3"), ct2, ct)
         ready_dot()
 
         den0 = fused(row("den0"), res2, y2, base, MUL, ADD)
@@ -640,7 +639,7 @@ def tile_paralleldirectpoincaredynamics_v_kernel(
             total = banks()
             for t in range(T):
                 term = times_row_factor(g_tiles[i][:, t, :], a_scaled[:, i, t : t + 1])
-                add_turned(total, term, t == 0, t == T - 1)
+                add_turned(total, [term], t == 0, t == T - 1)
             return total
 
         def inner_products(i, total):
@@ -657,14 +656,18 @@ def tile_paralleldirectpoincaredynamics_v_kernel(
                     start=(k == 0),
                     stop=(k == BLOCKS - 1),
                 )
+            ready_dot()
             nc.vector.tensor_copy(out=inputs[:, i, 3:4], in_=s_b[:, 0:1])
             terms = work.tile([P, 3, 2, T], F32, name="terms")
             mul(terms[:], from_dots[:, :, :, i, :], dots[:, i].unsqueeze(1).to_broadcast([P, 3, 2, T]))
+            ready_dot()
             nc.vector.tensor_reduce(
                 out=inputs[:, i, 0:3], in_=terms[:], axis=mybir.AxisListType.XY, op=ADD
             )
+            ready_dot()
             kappa_terms = work.tile([P, 3, 4], F32, name="kappa_terms")
             mul(kappa_terms[:], to_kappa[:, i], inputs[:, i].unsqueeze(1).to_broadcast([P, 3, 4]))
+            ready_dot()
             nc.vector.tensor_reduce(
                 out=kappa[:, i, :], in_=kappa_terms[:], axis=mybir.AxisListType.X, op=ADD
             )
@@ -672,12 +675,11 @@ def tile_paralleldirectpoincaredynamics_v_kernel(
         def finish(i):
             mix = banks()
             for k, src in enumerate((x_all[:, i, :], mv_all[:, i, :], b_all[:])):
-                add_turned(mix, times_row_factor(src, kappa[:, i, k : k + 1]), k == 0, k == 2)
+                add_turned(mix, [times_row_factor(src, kappa[:, i, k : k + 1])], k == 0, k == 2)
             turned_mix = work.tile([P, N], F32, name="turned_mix")
             out_of_psum(turned_mix, mix)
             dmv = banks()
-            add_turned(dmv, turned_sums[i], True, False)
-            add_turned(dmv, turned_mix, False, True)
+            add_turned(dmv, [turned_sums[i], turned_mix], True, True)
             out_of_psum(d_rows[i // PACK][:, i % PACK, :], dmv)
 
         for i in range(TILES + 1):
@@ -697,10 +699,10 @@ def tile_paralleldirectpoincaredynamics_v_kernel(
                 inner_products(i, total)
             if 0 <= c < PASSES:
                 quantise_pass(v_halves, v_codes[:, c, :], v_scales[:, c, :], E4M3_X4)
-            if i > 0 and i % PACK == 0:
-                done = i // PACK - 1
-                d_halves = regroup_pass(d_rows[done][:], nc.vector.tensor_copy)
-                quantise_pass(d_halves, d_codes[:, done, :], d_scales[:, done, :], E5M2_X4)
+
+        for c in range(PASSES):
+            d_halves = regroup_pass(d_rows[c][:], nc.vector.tensor_copy)
+            quantise_pass(d_halves, d_codes[:, c, :], d_scales[:, c, :], E5M2_X4)
 
         for m in range(BLOCKS):
             of_block = slice(m * P, (m + 1) * P)

@@ -26,8 +26,14 @@ BANK = 512
 HALVES = N // BANK
 BLOCKS = N // P
 BLOCKS_PER_BANK = BANK // P
-B_COPIES = 32
-V_INIT_AT = 5
+B_COPIES = 2
+WORD = 2
+WORD_BLOCKS = N // (WORD * P)
+ROW_GROUP = P // (T * WORD)
+ROW_GROUPS = P // ROW_GROUP
+PAIRED = ROW_GROUP * WORD
+VECTOR_X_TILES = 2
+VECTOR_TERMS = 4
 
 EPS = 1e-7
 EPS_SQ = EPS * EPS
@@ -48,9 +54,9 @@ def tile_paralleldirectpoincaredynamics_v_kernel(
         grads = ctx.enter_context(tc.tile_pool(name="grads", bufs=3))
         unread = ctx.enter_context(tc.tile_pool(name="unread", bufs=3))
         stage = ctx.enter_context(tc.tile_pool(name="stage", bufs=2))
-        chain = ctx.enter_context(tc.tile_pool(name="chain", bufs=1))
         work = ctx.enter_context(tc.tile_pool(name="work", bufs=2))
-        psum = ctx.enter_context(tc.psum_pool(name="psum", bufs=8))
+        early = ctx.enter_context(tc.tile_pool(name="early", bufs=2))
+        psum = ctx.enter_context(tc.psum_pool(name="psum", bufs=2))
 
         x_all = keep.tile([P, TILES, N], BF16, name="x_all")
         mv_all = keep.tile([P, TILES, N], F32, name="mv_all")
@@ -78,6 +84,20 @@ def tile_paralleldirectpoincaredynamics_v_kernel(
 
         identity = keep.tile([P, P], F32, name="identity")
         masks.make_identity(nc, identity[:])
+        same_pair = keep.tile([P, PAIRED], F32, name="same_pair")
+        same_horizon = keep.tile([P, T], F32, name="same_horizon")
+        nc.vector.tensor_reduce(
+            out=same_pair[:],
+            in_=identity[:].rearrange("p (t s) -> p s t", s=PAIRED),
+            axis=mybir.AxisListType.X,
+            op=ADD,
+        )
+        nc.vector.tensor_reduce(
+            out=same_horizon[:],
+            in_=identity[:].rearrange("p (t s) -> p t s", s=PAIRED),
+            axis=mybir.AxisListType.X,
+            op=ADD,
+        )
         horizon = keep.tile([P, T], F32, name="horizon")
         for t in range(T):
             nc.vector.memset(horizon[:, t : t + 1], float(t + 1))
@@ -137,7 +157,7 @@ def tile_paralleldirectpoincaredynamics_v_kernel(
             )
 
         def square_sum(acc, a):
-            squares = unread.tile([P, N], BF16, name="squares")
+            squares = unread.tile([P, N], BF16, name="squares", bufs=2)
             nc.scalar.activation(out=squares[:], in_=a, func=ACT.Square, accum_out=acc)
 
         def regroup_pass(rows, copy):
@@ -174,14 +194,34 @@ def tile_paralleldirectpoincaredynamics_v_kernel(
                     dot(xb[:, i : i + 1], x_all[:, i, :], b_all[:], N)
                 else:
                     dot(xm[:, i : i + 1], x_all[:, i, :], mv_all[:, i, :], N)
-            elif n < 2 * TILES + TILES * T:
+            elif n < 2 * TILES + VECTOR_X_TILES * T:
                 i, t = divmod(n - 2 * TILES, T)
-                if t == 0:
-                    g_tiles[i] = grads.tile([P, T, N], BF16, name="g")
-                    nc.sync.dma_start(
-                        out=g_tiles[i][:].rearrange("p t n -> p (t n)"), in_=g_view[i // PACK, i % PACK]
-                    )
                 dot(dots[:, i, 0, t : t + 1], g_tiles[i][:, t, :], x_all[:, i, :], N)
+
+        def load_g(i):
+            g_tiles[i] = grads.tile([P, T, N], BF16, name="g")
+            nc.sync.dma_start(
+                out=g_tiles[i][:].rearrange("p t n -> p (t n)"), in_=g_view[i // PACK, i % PACK]
+            )
+
+        halves_fetched = {}
+        HALVES_AHEAD = [(i, h) for i in range(VECTOR_X_TILES, TILES) for h in range(HALVES)]
+
+        def fetch_half(s):
+            if s < len(HALVES_AHEAD):
+                i, h = HALVES_AHEAD[s]
+                halves_fetched[s] = early.tile([P, T, BANK], BF16, name="g_half")
+                nc.sync.dma_start(
+                    out=halves_fetched[s][:],
+                    in_=g_view[i // PACK, i % PACK].rearrange("p (t n) -> p t n", t=T)[
+                        :, :, h * BANK : (h + 1) * BANK
+                    ],
+                )
+
+        for s in range(2):
+            fetch_half(s)
+        for i in range(VECTOR_X_TILES):
+            load_g(i)
 
         v_codes = keep.tile([P, PASSES, K], U32, name="v_codes", align_bytes=64)
         v_scales = keep.tile([P, PASSES, K], U8, name="v_scales", align_bytes=64)
@@ -199,8 +239,8 @@ def tile_paralleldirectpoincaredynamics_v_kernel(
         b_cols = keep.tile([P, BLOCKS, B_COPIES], F32, name="b_cols")
 
 
-        def banks():
-            return [psum.tile([P, BANK], F32, name="bank") for h in range(HALVES)]
+        def banks(role):
+            return [psum.tile([P, BANK], F32, name=role) for h in range(HALVES)]
 
         def add_turned(total, terms, first, last):
             for h in range(HALVES):
@@ -220,14 +260,17 @@ def tile_paralleldirectpoincaredynamics_v_kernel(
             for h in range(HALVES):
                 nc.scalar.copy(out=dst[:, h * BANK : (h + 1) * BANK], in_=total[h][:])
 
-        def times_row_factor(src, factor):
+        def times_row_factor(src, factor, on_vector=False):
             scaled = work.tile([P, N], F32, name="scaled", bufs=4)
-            nc.scalar.activation(out=scaled[:], in_=src, func=ACT.Copy, scale=factor)
+            if on_vector:
+                scale(scaled[:], src, factor)
+            else:
+                nc.scalar.activation(out=scaled[:], in_=src, func=ACT.Copy, scale=factor)
             return scaled
 
         b_f32 = work.tile([P, N], F32, name="scaled", bufs=4)
         nc.vector.tensor_copy(out=b_f32[:], in_=b_all[:])
-        b_turned = banks()
+        b_turned = banks("total")
         add_turned(b_turned, [b_f32], True, True)
         for h in range(HALVES):
             nc.scalar.copy(
@@ -235,397 +278,473 @@ def tile_paralleldirectpoincaredynamics_v_kernel(
                 in_=b_turned[h][:].rearrange("p (q r) -> p q r", r=P)[:, :, :B_COPIES],
             )
 
-        def col(name):
-            return chain.tile([P, 1], F32, name=name)
+        def x_dots_on_tensor(i):
+            x_words = x_all[:, i, :].bitcast(F32)
+            x_turned_psum = psum.tile([P, WORD_BLOCKS, P], F32, name="turn", bufs=2)
+            for k in range(WORD_BLOCKS):
+                nc.tensor.transpose(x_turned_psum[:, k, :], x_words[:, k * P : (k + 1) * P], identity[:])
+            x_turned = work.tile([P, WORD_BLOCKS, P], F32, name="x_turned")
+            nc.scalar.copy(out=x_turned[:], in_=x_turned_psum[:])
+            x_pairs = x_turned[:].bitcast(BF16)
+            crossed = psum.tile([P, ROW_GROUPS, PAIRED], F32, name="crossed", bufs=1)
+            blocks_per_half = WORD_BLOCKS // HALVES
 
-        def row(name):
-            return chain.tile([P, TILES], F32, name=name)
+            def turn(k):
+                h, q = divmod(k, blocks_per_half)
+                s = HALVES_AHEAD.index((i, h))
+                g_words = halves_fetched[s][:].bitcast(F32)
+                g_turned = work.tile([P, ROW_GROUPS, T, ROW_GROUP], F32, name="g_turned")
+                for first in range(0, T, BLOCKS_PER_BANK):
+                    g_turned_psum = psum.tile([P, BLOCKS_PER_BANK, P], F32, name="turn", bufs=2)
+                    for t in range(BLOCKS_PER_BANK):
+                        nc.tensor.transpose(
+                            g_turned_psum[:, t, :], g_words[:, first + t, q * P : (q + 1) * P], identity[:]
+                        )
+                    nc.scalar.copy(
+                        out=g_turned[:, :, first : first + BLOCKS_PER_BANK, :],
+                        in_=g_turned_psum[:].rearrange("p t (u r) -> p u t r", r=ROW_GROUP),
+                    )
+                if q == blocks_per_half - 1:
+                    fetch_half(s + 2)
+                return g_turned[:].bitcast(BF16)
 
-        def row2(name):
-            return chain.tile([P, 2, TILES], F32, name=name)
+            g_pairs = turn(0)
+            for k in range(WORD_BLOCKS):
+                following = turn(k + 1) if k + 1 < WORD_BLOCKS else None
+                for u in range(ROW_GROUPS):
+                    nc.tensor.matmul(
+                        out=crossed[:, u, :],
+                        lhsT=g_pairs[:, u].rearrange("p t s -> p (t s)"),
+                        rhs=x_pairs[:, k, u * PAIRED : (u + 1) * PAIRED],
+                        start=(k == 0 and u == 0),
+                        stop=(k == WORD_BLOCKS - 1 and u == ROW_GROUPS - 1),
+                    )
+                g_pairs = following
+            own_row = work.tile([P, WORD, ROW_GROUPS, ROW_GROUP], F32, name="own_row")
+            nc.vector.tensor_tensor(
+                out=own_row[:],
+                in0=crossed[:].rearrange("p u (r e) -> p e u r", e=WORD),
+                in1=same_pair[:]
+                .rearrange("p (r e) -> p e r", e=WORD)
+                .unsqueeze(2)
+                .to_broadcast([P, WORD, ROW_GROUPS, ROW_GROUP]),
+                op=MUL,
+            )
+            by_row = psum.tile([P, T], F32, name="turn", bufs=2)
+            for e in range(WORD):
+                nc.tensor.matmul(
+                    out=by_row[:],
+                    lhsT=own_row[:, e].rearrange("p u r -> p (u r)"),
+                    rhs=same_horizon[:],
+                    start=(e == 0),
+                    stop=(e == WORD - 1),
+                )
+            nc.scalar.copy(out=dots[:, i, 0, :], in_=by_row[:])
 
-        def grid(name):
-            return chain.tile([P, TILES, T], F32, name=name)
+        def coefficients(chain):
+            def col(name):
+                return chain.tile([P, 1], F32, name=name)
 
-        def pair(r):
-            return r.unsqueeze(1).to_broadcast([P, 2, TILES])
+            def row(name):
+                return chain.tile([P, TILES], F32, name=name)
 
-        def over_t(r):
-            return r.unsqueeze(2).to_broadcast([P, TILES, T])
+            def row2(name):
+                return chain.tile([P, 2, TILES], F32, name=name)
 
-        def over_tiles(h):
-            return h.unsqueeze(1).to_broadcast([P, TILES, T])
+            def grid(name):
+                return chain.tile([P, TILES, T], F32, name=name)
+
+            def pair(r):
+                return r.unsqueeze(1).to_broadcast([P, 2, TILES])
+
+            def over_t(r):
+                return r.unsqueeze(2).to_broadcast([P, TILES, T])
+
+            def over_tiles(h):
+                return h.unsqueeze(1).to_broadcast([P, TILES, T])
 
 
-        clipped = row("clipped")
-        nc.vector.tensor_scalar(
-            out=clipped,
-            in0=vn_row,
-            scalar1=-CLIP,
-            scalar2=CLIP,
-            op0=mybir.AluOpType.max,
-            op1=mybir.AluOpType.min,
-        )
-        ivn = inverse(row("ivn"), vn_row)
+            clipped = row("clipped")
+            nc.vector.tensor_scalar(
+                out=clipped,
+                in0=vn_row,
+                scalar1=-CLIP,
+                scalar2=CLIP,
+                op0=mybir.AluOpType.max,
+                op1=mybir.AluOpType.min,
+            )
+            ivn = inverse(row("ivn"), vn_row)
 
-        one_minus = affine(row("one_minus"), clipped, -1.0, 1.0)
+            one_minus = affine(row("one_minus"), clipped, -1.0, 1.0)
 
-        inv_one_minus = inverse(row("inv_one_minus"), one_minus)
+            inv_one_minus = inverse(row("inv_one_minus"), one_minus)
 
-        ratio = fused(row("ratio"), clipped, 1.0, inv_one_minus, ADD, MUL)
-        ln_ratio = table(row("ln_ratio"), ratio, ACT.Ln)
+            ratio = fused(row("ratio"), clipped, 1.0, inv_one_minus, ADD, MUL)
+            ln_ratio = table(row("ln_ratio"), ratio, ACT.Ln)
 
-        bb = col("bb")
-        m2, mb, x2 = row("m2"), row("mb"), row("x2")
-        square_sum(bb, b_all[:])
-        for i in range(TILES):
-            square_sum(m2[:, i : i + 1], mv_all[:, i, :])
-            dot(mb[:, i : i + 1], mv_all[:, i, :], b_all[:], N)
-        for spare in range(2):
+            bb = col("bb")
+            m2, mb, x2 = row("m2"), row("mb"), row("x2")
+            square_sum(bb, b_all[:])
+            for i in range(TILES):
+                square_sum(m2[:, i : i + 1], mv_all[:, i, :])
+                dot(mb[:, i : i + 1], mv_all[:, i, :], b_all[:], N)
+            for spare in range(2):
+                ready_dot()
+
+            m2_c = at_least(row("m2_c"), m2, EPS_SQ)
+            bb_c = at_least(col("bb_c"), bb, EPS_SQ)
+            free_m = above(row("free_m"), m2, EPS_SQ)
+            k1 = fused(row("k1"), ln_ratio, 0.5, ivn, MUL, MUL)
+            rm = table(row("rm"), m2_c, ACT.Sqrt)
+            rb = table(col("rb"), bb_c, ACT.Sqrt)
+            ready_dot()
             ready_dot()
 
-        m2_c = at_least(row("m2_c"), m2, EPS_SQ)
-        bb_c = at_least(col("bb_c"), bb, EPS_SQ)
-        free_m = above(row("free_m"), m2, EPS_SQ)
-        k1 = fused(row("k1"), ln_ratio, 0.5, ivn, MUL, MUL)
-        rm = table(row("rm"), m2_c, ACT.Sqrt)
-        rb = table(col("rb"), bb_c, ACT.Sqrt)
-        ready_dot()
-        ready_dot()
+            k1_rm = mul(row("k1_rm"), k1, rm)
+            irm = inverse(row("irm"), rm)
+            irb = inverse(col("irb"), rb)
+            hm = table(row("hm"), k1_rm, ACT.Tanh)
+            hb = table(col("hb"), rb, ACT.Tanh)
+            half_tanh = table(col("half_tanh"), logit, ACT.Tanh, 0.5)
+            for i in range(TILES):
+                square_sum(x2[:, i : i + 1], x_all[:, i, :])
+            ready_dot()
+            ready_dot()
+            v_rows = grads.tile([P, PASSES, PACK, K], BF16, name="g")
+            nc.sync.dma_start(out=v_rows[:].rearrange("p c j k -> p c (j k)"), in_=v_view)
+            v_halves = regroup_pass(v_rows[:, 0], nc.scalar.copy)
 
-        k1_rm = mul(row("k1_rm"), k1, rm)
-        irm = inverse(row("irm"), rm)
-        irb = inverse(col("irb"), rb)
-        hm = table(row("hm"), k1_rm, ACT.Tanh)
-        hb = table(col("hb"), rb, ACT.Tanh)
-        half_tanh = table(col("half_tanh"), logit, ACT.Tanh, 0.5)
-        for i in range(TILES):
-            square_sum(x2[:, i : i + 1], x_all[:, i, :])
-        ready_dot()
-        ready_dot()
-
-        alpha = mul(row("alpha"), hm, irm)
-        beta = mul(col("beta"), hb, irb)
-        step = affine(col("step"), half_tanh, 0.5, 0.5)
-        ready_dot()
-
-        alpha_m2 = mul(row("alpha_m2"), alpha, m2)
-        alpha_mb = mul(row("alpha_mb"), alpha, mb)
-        beta2 = scale(col("beta2"), beta, 2.0)
-        beta_bb = mul(col("beta_bb"), beta, bb)
-        ct = scale(chain.tile([P, T], F32, name="ct"), horizon, step)
-        ready_dot()
-
-        res2 = mul(row("res2"), alpha_m2, alpha)
-        res_b2 = scale(row("res_b2"), alpha_mb, beta2)
-        y2 = mul(col("y2"), beta_bb, beta)
-        ct2 = mul(chain.tile([P, T], F32, name="ct2"), ct, ct)
-        ready_dot()
-
-        base = shift(row("base"), res_b2, 1.0)
-        a2 = affine(row("a2"), res2, -1.0, 1.0)
-        ct3 = mul(chain.tile([P, T], F32, name="ct3"), ct2, ct)
-        ready_dot()
-
-        den0 = fused(row("den0"), res2, y2, base, MUL, ADD)
-        a1 = shift(row("a1"), base, y2)
-        ready_dot()
-
-        den = at_least(row("den"), den0, EPS)
-        live = above(row("live"), den0, EPS)
-        ready_dot()
-
-        iden = inverse(row("iden"), den)
-        ready_dot()
-
-        p1 = mul(row("p1"), a1, iden)
-        p2 = mul(row("p2"), a2, iden)
-        ready_dot()
-
-        pa = mul(row("pa"), p1, alpha)
-        pb = scale(row("pb"), p2, beta)
-        ready_dot()
-
-        pa_m2 = mul(row("pa_m2"), pa, m2)
-        pb_mb = mul(row("pb_mb"), pb, mb)
-        pa_mb = mul(row("pa_mb"), pa, mb)
-        ready_dot()
-
-        p_mv = add(row("p_mv"), pa_m2, pb_mb)
-        p_b = fused(row("p_b"), pb, bb, pa_mb, MUL, ADD)
-        ready_dot()
-
-        pa_pmv = mul(row("pa_pmv"), pa, p_mv)
-        pb_pb = mul(row("pb_pb"), pb, p_b)
-        gap = affine(row("gap"), x2, -1.0, 1.0)
-        ready_dot()
-
-        pp = add(row("pp"), pa_pmv, pb_pb)
-        gap_c = at_least(row("gap_c"), gap, EPS)
-        ready_dot()
-
-        pp_c = at_least(row("pp_c"), pp, TINY)
-        on_p = above(row("on_p"), pp, MAX_NORM * MAX_NORM)
-        k2 = inverse(row("k2"), gap_c)
-        rp_raw = table(row("rp_raw"), pp_c, ACT.Sqrt)
-        while ready_issued[0] < 2 * TILES:
+            alpha = mul(row("alpha"), hm, irm)
+            beta = mul(col("beta"), hb, irb)
+            step = affine(col("step"), half_tanh, 0.5, 0.5)
             ready_dot()
 
-        rp = at_least(row("rp"), rp_raw, EPS)
+            alpha_m2 = mul(row("alpha_m2"), alpha, m2)
+            alpha_mb = mul(row("alpha_mb"), alpha, mb)
+            beta2 = scale(col("beta2"), beta, 2.0)
+            beta_bb = mul(col("beta_bb"), beta, bb)
+            ct = scale(chain.tile([P, T], F32, name="ct"), horizon, step)
+            ready_dot()
 
-        irp = inverse(row("irp"), rp)
+            res2 = mul(row("res2"), alpha_m2, alpha)
+            res_b2 = scale(row("res_b2"), alpha_mb, beta2)
+            y2 = mul(col("y2"), beta_bb, beta)
+            ct2 = mul(chain.tile([P, T], F32, name="ct2"), ct, ct)
+            ready_dot()
 
-        shrink = fused(row("shrink"), irp, MAX_NORM, on_p, MUL, MUL)
-        irp2 = mul(row("irp2"), irp, irp)
+            base = shift(row("base"), res_b2, 1.0)
+            a2 = affine(row("a2"), res2, -1.0, 1.0)
+            ct3 = mul(chain.tile([P, T], F32, name="ct3"), ct2, ct)
+            ready_dot()
 
-        pi = fused(row("pi"), shrink, 1.0, on_p, ADD, SUB)
-        phi = mul(row("phi"), shrink, irp2)
+            quantise_pass(v_halves, v_codes[:, 0, :], v_scales[:, 0, :], E4M3_X4)
+            v_halves = regroup_pass(v_rows[:, 1], nc.scalar.copy)
 
-        mul(mu, pi, pa)
-        mul(nu, pi, pb)
-        r0 = mul(row("r0"), pi, rp_raw)
-        pi_sq = mul(row("pi_sq"), pi, pi)
+            den0 = fused(row("den0"), res2, y2, base, MUL, ADD)
+            a1 = shift(row("a1"), base, y2)
+            ready_dot()
 
-        c_r0 = mul(grid("c_r0"), over_t(r0), over_tiles(ct))
-        vv = mul(row("vv"), pi_sq, pp)
-        mu_xm = mul(row("mu_xm"), mu, xm)
-        nu_xb = mul(row("nu_xb"), nu, xb)
+            den = at_least(row("den"), den0, EPS)
+            live = above(row("live"), den0, EPS)
+            ready_dot()
 
-        rt = at_least(grid("rt"), c_r0, EPS)
-        free_t = above(grid("free_t"), c_r0, EPS)
-        xv = add(row("xv"), mu_xm, nu_xb)
+            iden = inverse(row("iden"), den)
+            ready_dot()
 
-        k2_rt = mul(grid("k2_rt"), rt, over_t(k2))
-        irt = inverse(grid("irt"), rt)
-        ht = table(grid("ht"), k2_rt, ACT.Tanh)
-        ready_dot()
-        ready_dot()
+            p1 = mul(row("p1"), a1, iden)
+            p2 = mul(row("p2"), a2, iden)
+            ready_dot()
 
-        sigma = mul(grid("sigma"), ht, irt)
+            pa = mul(row("pa"), p1, alpha)
+            pb = scale(row("pb"), p2, beta)
+            ready_dot()
 
-        s = mul(grid("s"), sigma, over_tiles(ct))
+            quantise_pass(v_halves, v_codes[:, 1, :], v_scales[:, 1, :], E4M3_X4)
 
-        x_sec = mul(grid("x_sec"), s, over_t(xv))
-        s_vv = mul(grid("s_vv"), s, over_t(vv))
+            pa_m2 = mul(row("pa_m2"), pa, m2)
+            pb_mb = mul(row("pb_mb"), pb, mb)
+            pa_mb = mul(row("pa_mb"), pa, mb)
+            ready_dot()
 
-        base_t = affine(grid("base_t"), x_sec, 2.0, 1.0)
-        sec2 = mul(grid("sec2"), s_vv, s)
+            p_mv = add(row("p_mv"), pa_m2, pb_mb)
+            p_b = fused(row("p_b"), pb, bb, pa_mb, MUL, ADD)
+            ready_dot()
 
-        x2_sec2 = mul(grid("x2_sec2"), sec2, over_t(x2))
-        b1 = add(grid("b1"), base_t, sec2)
+            pa_pmv = mul(row("pa_pmv"), pa, p_mv)
+            pb_pb = mul(row("pb_pb"), pb, p_b)
+            gap = affine(row("gap"), x2, -1.0, 1.0)
+            ready_dot()
 
-        den0_t = add(grid("den0_t"), x2_sec2, base_t)
+            pp = add(row("pp"), pa_pmv, pb_pb)
+            gap_c = at_least(row("gap_c"), gap, EPS)
+            ready_dot()
 
-        den_t = at_least(grid("den_t"), den0_t, EPS)
-        live_t = above(grid("live_t"), den0_t, EPS)
+            pp_c = at_least(row("pp_c"), pp, TINY)
+            on_p = above(row("on_p"), pp, MAX_NORM * MAX_NORM)
+            k2 = inverse(row("k2"), gap_c)
+            rp_raw = table(row("rp_raw"), pp_c, ACT.Sqrt)
+            while ready_issued[0] < 2 * TILES:
+                ready_dot()
 
-        iden_t = inverse(grid("iden_t"), den_t)
+            rp = at_least(row("rp"), rp_raw, EPS)
 
-        q1 = mul(grid("q1"), b1, iden_t)
-        q2 = mul(grid("q2"), iden_t, over_t(gap))
+            irp = inverse(row("irp"), rp)
 
-        q2s = mul(grid("q2s"), q2, s)
-        q1_x2 = mul(grid("q1_x2"), q1, over_t(x2))
-        q2_xsec = mul(grid("q2_xsec"), q2, x_sec)
-        q1_xv = mul(grid("q1_xv"), q1, over_t(xv))
+            shrink = fused(row("shrink"), irp, MAX_NORM, on_p, MUL, MUL)
+            irp2 = mul(row("irp2"), irp, irp)
 
-        q_x = add(grid("q_x"), q1_x2, q2_xsec)
-        q2s_vv = mul(grid("q2s_vv"), q2s, over_t(vv))
+            pi = fused(row("pi"), shrink, 1.0, on_p, ADD, SUB)
+            phi = mul(row("phi"), shrink, irp2)
 
-        q_v = add(grid("q_v"), q1_xv, q2s_vv)
-        q1_qx = mul(grid("q1_qx"), q1, q_x)
+            mul(mu, pi, pa)
+            mul(nu, pi, pb)
+            r0 = mul(row("r0"), pi, rp_raw)
+            pi_sq = mul(row("pi_sq"), pi, pi)
 
-        q2s_qv = mul(grid("q2s_qv"), q2s, q_v)
+            c_r0 = mul(grid("c_r0"), over_t(r0), over_tiles(ct))
+            vv = mul(row("vv"), pi_sq, pp)
+            mu_xm = mul(row("mu_xm"), mu, xm)
+            nu_xb = mul(row("nu_xb"), nu, xb)
 
-        qq = add(grid("qq"), q1_qx, q2s_qv)
+            rt = at_least(grid("rt"), c_r0, EPS)
+            free_t = above(grid("free_t"), c_r0, EPS)
+            xv = add(row("xv"), mu_xm, nu_xb)
 
-        qq_c = at_least(grid("qq_c"), qq, EPS_SQ)
-        on_q = above(grid("on_q"), qq, MAX_NORM * MAX_NORM)
-        rq = table(grid("rq"), qq_c, ACT.Sqrt)
-        ready_dot()
-        ready_dot()
+            k2_rt = mul(grid("k2_rt"), rt, over_t(k2))
+            irt = inverse(grid("irt"), rt)
+            ht = table(grid("ht"), k2_rt, ACT.Tanh)
+            ready_dot()
+            ready_dot()
 
-        irq = inverse(grid("irq"), rq)
+            sigma = mul(grid("sigma"), ht, irt)
 
-        shrink_q = fused(grid("shrink_q"), irq, MAX_NORM, on_q, MUL, MUL)
-        irq2 = mul(grid("irq2"), irq, irq)
+            s = mul(grid("s"), sigma, over_tiles(ct))
 
-        pi_q = fused(grid("pi_q"), shrink_q, 1.0, on_q, ADD, SUB)
-        phi_q = mul(grid("phi_q"), shrink_q, irq2)
+            x_sec = mul(grid("x_sec"), s, over_t(xv))
+            s_vv = mul(grid("s_vv"), s, over_t(vv))
 
-        a_t = mul(from_dots[:, 2, 1], q2s, pi_q)
-        nc.vector.memset(from_dots[:, 2, 0], 0.0)
+            base_t = affine(grid("base_t"), x_sec, 2.0, 1.0)
+            sec2 = mul(grid("sec2"), s_vv, s)
 
-        mul(a_scaled[:], a_t, over_t(mu))
+            x2_sec2 = mul(grid("x2_sec2"), sec2, over_t(x2))
+            b1 = add(grid("b1"), base_t, sec2)
 
-        phi_qq = mul(grid("phi_qq"), phi_q, qq)
-        phi_qx = mul(grid("phi_qx"), phi_q, q_x)
-        q2_phi = mul(grid("q2_phi"), q2, phi_q)
-        iden_pi = mul(grid("iden_pi"), iden_t, pi_q)
-        ht2 = mul(grid("ht2"), ht, ht)
-        irt2 = mul(grid("irt2"), irt, irt)
-        xv_svv = add(grid("xv_svv"), s_vv, over_t(xv))
-        q2_pi = mul(grid("q2_pi"), q2, pi_q)
+            den0_t = add(grid("den0_t"), x2_sec2, base_t)
 
-        keep_q = sub(grid("keep_q"), pi_q, phi_qq)
-        lost_x = mul(grid("lost_x"), q2_phi, q1)
-        lost_v = mul(grid("lost_v"), q2_phi, q2s)
-        lost_qv = mul(grid("lost_qv"), q2_phi, q_v)
-        s_iden_pi = mul(grid("s_iden_pi"), s, iden_pi)
-        slope_t = affine(grid("slope_t"), ht2, -1.0, 1.0)
-        irt3 = mul(grid("irt3"), irt2, irt)
+            den_t = at_least(grid("den_t"), den0_t, EPS)
+            live_t = above(grid("live_t"), den0_t, EPS)
 
-        live_keep = mul(grid("live_keep"), live_t, keep_q)
-        slope_kr = mul(grid("slope_kr"), slope_t, k2_rt)
-        free_irt3 = mul(grid("free_irt3"), irt3, free_t)
-        iden_pi_sum = mul(grid("iden_pi_sum"), iden_pi, xv_svv)
-        ss_iden_pi = mul(grid("ss_iden_pi"), s, s_iden_pi)
+            iden_t = inverse(grid("iden_t"), den_t)
 
-        on_x_sum = add(grid("on_x_sum"), phi_qx, live_keep)
-        x2_live_keep = mul(grid("x2_live_keep"), live_keep, over_t(x2))
-        top_t = sub(grid("top_t"), slope_kr, ht)
-        free_c3 = mul(grid("free_c3"), free_irt3, over_tiles(ct3))
+            q1 = mul(grid("q1"), b1, iden_t)
+            q2 = mul(grid("q2"), iden_t, over_t(gap))
 
-        on_x = mul(grid("on_x"), iden_t, on_x_sum)
-        on_sec_sum = add(grid("on_sec_sum"), phi_qx, x2_live_keep)
-        coef_c3 = mul(grid("coef_c3"), top_t, free_c3)
+            q2s = mul(grid("q2s"), q2, s)
+            q1_x2 = mul(grid("q1_x2"), q1, over_t(x2))
+            q2_xsec = mul(grid("q2_xsec"), q2, x_sec)
+            q1_xv = mul(grid("q1_xv"), q1, over_t(xv))
 
-        on_sec = mul(grid("on_sec"), iden_t, on_sec_sum)
-        x_c_half = fused(grid("x_c_half"), on_x, 2.0, lost_x, MUL, ADD)
-        on_x_xv = mul(grid("on_x_xv"), on_x, over_t(xv))
-        v_b = mul(grid("v_b"), coef_c3, q2_pi)
-        coef_a = mul(grid("coef_a"), coef_c3, iden_pi_sum)
+            q_x = add(grid("q_x"), q1_x2, q2_xsec)
+            q2s_vv = mul(grid("q2s_vv"), q2s, over_t(vv))
 
-        s_on_sec = mul(grid("s_on_sec"), s, on_sec)
-        x_c = fused(grid("x_c"), x_c_half, -1.0, s, MUL, MUL)
-        v_a_half = add(grid("v_a_half"), ss_iden_pi, coef_a)
+            q_v = add(grid("q_v"), q1_xv, q2s_vv)
+            q1_qx = mul(grid("q1_qx"), q1, q_x)
 
-        v_c_first = fused(grid("v_c_first"), s_on_sec, 2.0, lost_v, MUL, ADD)
-        s_on_sec_vv = mul(grid("s_on_sec_vv"), s_on_sec, over_t(vv))
-        x_c_q1 = mul(grid("x_c_q1"), x_c, q1)
-        mul(from_dots[:, 0, 1], x_c, q2s)
+            q2s_qv = mul(grid("q2s_qv"), q2s, q_v)
 
-        s_v_c_first = mul(grid("s_v_c_first"), s, v_c_first)
-        ds_v_c_half = add(grid("ds_v_c_half"), on_x_xv, s_on_sec_vv)
-        fused(from_dots[:, 0, 0], s_iden_pi, 2.0, x_c_q1, MUL, ADD)
+            qq = add(grid("qq"), q1_qx, q2s_qv)
 
-        ds_v_c = fused(grid("ds_v_c"), ds_v_c_half, 2.0, lost_qv, MUL, ADD)
+            qq_c = at_least(grid("qq_c"), qq, EPS_SQ)
+            on_q = above(grid("on_q"), qq, MAX_NORM * MAX_NORM)
+            rq = table(grid("rq"), qq_c, ACT.Sqrt)
+            ready_dot()
+            ready_dot()
 
-        phi_pp = mul(row("phi_pp"), phi, pp)
-        iden_alpha = mul(row("iden_alpha"), iden, alpha)
-        iden_beta = scale(row("iden_beta"), iden, beta)
-        phi_pmv = mul(row("phi_pmv"), phi, p_mv)
-        phi_pb = mul(row("phi_pb"), phi, p_b)
+            irq = inverse(grid("irq"), rq)
 
-        coef_ds_v_c = mul(grid("coef_ds_v_c"), coef_c3, ds_v_c)
-        beta2_mb = scale(row("beta2_mb"), mb, beta2)
-        alpha2_m2 = scale(row("alpha2_m2"), alpha_m2, 2.0)
-        hm2 = mul(row("hm2"), hm, hm)
-        irm2 = mul(row("irm2"), irm, irm)
+            shrink_q = fused(grid("shrink_q"), irq, MAX_NORM, on_q, MUL, MUL)
+            irq2 = mul(grid("irq2"), irq, irq)
 
-        v_c = fused(grid("v_c"), s_v_c_first, -1.0, coef_ds_v_c, MUL, SUB)
-        lost = mul(row("lost"), pa, phi)
-        alpha_sq2 = fused(row("alpha_sq2"), alpha, 2.0, alpha, MUL, MUL)
-        alpha_beta2 = scale(row("alpha_beta2"), alpha, beta2)
-        imu = inverse(row("imu"), mu)
+            pi_q = fused(grid("pi_q"), shrink_q, 1.0, on_q, ADD, SUB)
+            phi_q = mul(grid("phi_q"), shrink_q, irq2)
 
-        v_c_q1 = mul(grid("v_c_q1"), v_c, q1)
-        v_c_q2s = mul(grid("v_c_q2s"), v_c, q2s)
-        keep_p = sub(row("keep_p"), pi, phi_pp)
-        a_first = mul(row("a_first"), iden_alpha, pi)
-        b_first = mul(row("b_first"), iden_beta, pi)
+            a_t = mul(from_dots[:, 2, 1], q2s, pi_q)
+            nc.vector.memset(from_dots[:, 2, 0], 0.0)
 
-        fused(from_dots[:, 1, 0], v_a_half, 2.0, v_c_q1, MUL, ADD)
-        add(from_dots[:, 1, 1], v_c_q2s, v_b)
-        alpha_phi_pmv = mul(row("alpha_phi_pmv"), alpha, phi_pmv)
-        beta_phi_pb = scale(row("beta_phi_pb"), phi_pb, beta)
-        slope_m = affine(row("slope_m"), hm2, -1.0, 1.0)
-        irm3 = mul(row("irm3"), irm2, irm)
+            mul(a_scaled[:], a_t, over_t(mu))
 
-        live_keep_p = mul(row("live_keep_p"), live, keep_p)
-        lost_pa = mul(row("lost_pa"), lost, pa)
-        lost_pb = mul(row("lost_pb"), lost, pb)
-        p1_phi_pmv = mul(row("p1_phi_pmv"), p1, phi_pmv)
-        p1_pi = mul(row("p1_pi"), p1, pi)
+            phi_qq = mul(grid("phi_qq"), phi_q, qq)
+            phi_qx = mul(grid("phi_qx"), phi_q, q_x)
+            q2_phi = mul(grid("q2_phi"), q2, phi_q)
+            iden_pi = mul(grid("iden_pi"), iden_t, pi_q)
+            ht2 = mul(grid("ht2"), ht, ht)
+            irt2 = mul(grid("irt2"), irt, irt)
+            xv_svv = add(grid("xv_svv"), s_vv, over_t(xv))
+            q2_pi = mul(grid("q2_pi"), q2, pi_q)
 
-        to_b_sum = add(row("to_b_sum"), alpha_phi_pmv, live_keep_p)
-        y2_live_keep_p = scale(row("y2_live_keep_p"), live_keep_p, y2)
-        slope_km = mul(row("slope_km"), slope_m, k1_rm)
-        free_irm3 = mul(row("free_irm3"), irm3, free_m)
-        mb_a_first = mul(row("mb_a_first"), beta2_mb, a_first)
-        m2_b_first = mul(row("m2_b_first"), alpha2_m2, b_first)
+            keep_q = sub(grid("keep_q"), pi_q, phi_qq)
+            lost_x = mul(grid("lost_x"), q2_phi, q1)
+            lost_v = mul(grid("lost_v"), q2_phi, q2s)
+            lost_qv = mul(grid("lost_qv"), q2_phi, q_v)
+            s_iden_pi = mul(grid("s_iden_pi"), s, iden_pi)
+            slope_t = affine(grid("slope_t"), ht2, -1.0, 1.0)
+            irt3 = mul(grid("irt3"), irt2, irt)
 
-        to_b_c = mul(row("to_b_c"), iden, to_b_sum)
-        to_res_sum = sub(row("to_res_sum"), y2_live_keep_p, beta_phi_pb)
-        top_m = sub(row("top_m"), slope_km, hm)
-        on_b_a = mul(row("on_b_a"), alpha_beta2, a_first)
-        sq_b_first = mul(row("sq_b_first"), alpha_sq2, b_first)
-        dres_a = add(row("dres_a"), p1_pi, mb_a_first)
+            live_keep = mul(grid("live_keep"), live_t, keep_q)
+            slope_kr = mul(grid("slope_kr"), slope_t, k2_rt)
+            free_irt3 = mul(grid("free_irt3"), irt3, free_t)
+            iden_pi_sum = mul(grid("iden_pi_sum"), iden_pi, xv_svv)
+            ss_iden_pi = mul(grid("ss_iden_pi"), s, s_iden_pi)
 
-        to_res_c = mul(row("to_res_c"), iden, to_res_sum)
-        coef_m = mul(row("coef_m"), top_m, free_irm3)
-        mb_to_b_c = mul(row("mb_to_b_c"), beta2_mb, to_b_c)
-        ab_to_b_c = mul(row("ab_to_b_c"), alpha_beta2, to_b_c)
+            on_x_sum = add(grid("on_x_sum"), phi_qx, live_keep)
+            x2_live_keep = mul(grid("x2_live_keep"), live_keep, over_t(x2))
+            top_t = sub(grid("top_t"), slope_kr, ht)
+            free_c3 = mul(grid("free_c3"), free_irt3, over_tiles(ct3))
 
-        m2_to_res_c = mul(row("m2_to_res_c"), alpha2_m2, to_res_c)
-        sq_to_res_c = mul(row("sq_to_res_c"), alpha_sq2, to_res_c)
-        dres_c_part = add(row("dres_c_part"), p1_phi_pmv, mb_to_b_c)
-        on_b_c = add(row("on_b_c"), ab_to_b_c, lost_pb)
-        on_mv_a = mul(row("on_mv_a"), coef_m, dres_a)
-        coef_dres_b = mul(row("coef_dres_b"), coef_m, m2_b_first)
+            on_x = mul(grid("on_x"), iden_t, on_x_sum)
+            on_sec_sum = add(grid("on_sec_sum"), phi_qx, x2_live_keep)
+            coef_c3 = mul(grid("coef_c3"), top_t, free_c3)
 
-        dres_c = add(row("dres_c"), dres_c_part, m2_to_res_c)
-        on_mv_c_part = add(row("on_mv_c_part"), sq_to_res_c, lost_pa)
-        on_mv_b = add(row("on_mv_b"), coef_dres_b, sq_b_first)
-        on_b_c_pa = mul(row("on_b_c_pa"), on_b_c, pa)
+            on_sec = mul(grid("on_sec"), iden_t, on_sec_sum)
+            x_c_half = fused(grid("x_c_half"), on_x, 2.0, lost_x, MUL, ADD)
+            on_x_xv = mul(grid("on_x_xv"), on_x, over_t(xv))
+            v_b = mul(grid("v_b"), coef_c3, q2_pi)
+            coef_a = mul(grid("coef_a"), coef_c3, iden_pi_sum)
 
-        coef_dres_c = mul(row("coef_dres_c"), coef_m, dres_c)
-        on_both = chain.tile([P, 2, 2, TILES], F32, name="on_both")
-        sub(on_both[:, 1, 0, :], on_b_a, on_b_c_pa)
-        fused(on_both[:, 1, 1, :], on_b_c, -1.0, pb, MUL, MUL)
-        mu_mb = mul(row("mu_mb"), mu, mb)
-        nu_bb = scale(row("nu_bb"), nu, bb)
+            s_on_sec = mul(grid("s_on_sec"), s, on_sec)
+            x_c = fused(grid("x_c"), x_c_half, -1.0, s, MUL, MUL)
+            v_a_half = add(grid("v_a_half"), ss_iden_pi, coef_a)
 
-        on_mv_c = add(row("on_mv_c"), coef_dres_c, on_mv_c_part)
-        vb = add(row("vb"), mu_mb, nu_bb)
-        nc.vector.memset(to_kappa[:], 0.0)
+            v_c_first = fused(grid("v_c_first"), s_on_sec, 2.0, lost_v, MUL, ADD)
+            s_on_sec_vv = mul(grid("s_on_sec_vv"), s_on_sec, over_t(vv))
+            x_c_q1 = mul(grid("x_c_q1"), x_c, q1)
+            mul(from_dots[:, 0, 1], x_c, q2s)
 
-        on_mv_c_pa = mul(row("on_mv_c_pa"), on_mv_c, pa)
-        on_mv_c_pb = mul(row("on_mv_c_pb"), on_mv_c, pb)
-        nc.vector.tensor_copy(out=to_kappa[:, :, 0, 0], in_=mu)
+            s_v_c_first = mul(grid("s_v_c_first"), s, v_c_first)
+            ds_v_c_half = add(grid("ds_v_c_half"), on_x_xv, s_on_sec_vv)
+            fused(from_dots[:, 0, 0], s_iden_pi, 2.0, x_c_q1, MUL, ADD)
 
-        sub(on_both[:, 0, 0, :], on_mv_a, on_mv_c_pa)
-        fused(on_both[:, 0, 1, :], on_mv_c_pb, -1.0, on_mv_b, MUL, SUB)
+            ds_v_c = fused(grid("ds_v_c"), ds_v_c_half, 2.0, lost_qv, MUL, ADD)
 
-        in_v0_b = chain.tile([P, 2, 2, TILES], F32, name="in_v0_b")
-        mul(in_v0_b[:, :, 0, :], on_both[:, :, 0, :], pair(imu))
+            phi_pp = mul(row("phi_pp"), phi, pp)
+            iden_alpha = mul(row("iden_alpha"), iden, alpha)
+            iden_beta = scale(row("iden_beta"), iden, beta)
+            phi_pmv = mul(row("phi_pmv"), phi, p_mv)
+            phi_pb = mul(row("phi_pb"), phi, p_b)
 
-        nu_first = mul(row2("nu_first"), in_v0_b[:, :, 0, :], pair(nu))
+            coef_ds_v_c = mul(grid("coef_ds_v_c"), coef_c3, ds_v_c)
+            beta2_mb = scale(row("beta2_mb"), mb, beta2)
+            alpha2_m2 = scale(row("alpha2_m2"), alpha_m2, 2.0)
+            hm2 = mul(row("hm2"), hm, hm)
+            irm2 = mul(row("irm2"), irm, irm)
 
-        sub(in_v0_b[:, :, 1, :], on_both[:, :, 1, :], nu_first)
+            v_c = fused(grid("v_c"), s_v_c_first, -1.0, coef_ds_v_c, MUL, SUB)
+            lost = mul(row("lost"), pa, phi)
+            alpha_sq2 = fused(row("alpha_sq2"), alpha, 2.0, alpha, MUL, MUL)
+            alpha_beta2 = scale(row("alpha_beta2"), alpha, beta2)
+            imu = inverse(row("imu"), mu)
 
-        weights = chain.tile([P, 2, 2, TILES], F32, name="weights")
-        mul(weights[:, 0], in_v0_b[:, 0], pair(imu))
+            v_c_q1 = mul(grid("v_c_q1"), v_c, q1)
+            v_c_q2s = mul(grid("v_c_q2s"), v_c, q2s)
+            keep_p = sub(row("keep_p"), pi, phi_pp)
+            a_first = mul(row("a_first"), iden_alpha, pi)
+            b_first = mul(row("b_first"), iden_beta, pi)
 
-        nu_on_v0 = mul(row2("nu_on_v0"), weights[:, 0], pair(nu))
+            fused(from_dots[:, 1, 0], v_a_half, 2.0, v_c_q1, MUL, ADD)
+            add(from_dots[:, 1, 1], v_c_q2s, v_b)
+            alpha_phi_pmv = mul(row("alpha_phi_pmv"), alpha, phi_pmv)
+            beta_phi_pb = scale(row("beta_phi_pb"), phi_pb, beta)
+            slope_m = affine(row("slope_m"), hm2, -1.0, 1.0)
+            irm3 = mul(row("irm3"), irm2, irm)
 
-        sub(weights[:, 1], in_v0_b[:, 1], nu_on_v0)
+            live_keep_p = mul(row("live_keep_p"), live, keep_p)
+            lost_pa = mul(row("lost_pa"), lost, pa)
+            lost_pb = mul(row("lost_pb"), lost, pb)
+            p1_phi_pmv = mul(row("p1_phi_pmv"), p1, phi_pmv)
+            p1_pi = mul(row("p1_pi"), p1, pi)
 
-        def kappa_column(m):
-            return to_kappa[:, :, 1:3, m].rearrange("p i k -> p k i")
+            to_b_sum = add(row("to_b_sum"), alpha_phi_pmv, live_keep_p)
+            y2_live_keep_p = scale(row("y2_live_keep_p"), live_keep_p, y2)
+            slope_km = mul(row("slope_km"), slope_m, k1_rm)
+            free_irm3 = mul(row("free_irm3"), irm3, free_m)
+            mb_a_first = mul(row("mb_a_first"), beta2_mb, a_first)
+            m2_b_first = mul(row("m2_b_first"), alpha2_m2, b_first)
 
-        w_v0, w_b = weights[:, :, 0, :], weights[:, :, 1, :]
-        kx_a = mul(row2("kx_a"), w_v0, pair(xv))
-        kx_b = mul(row2("kx_b"), w_b, pair(xb))
-        kv_a = mul(row2("kv_a"), w_v0, pair(vv))
-        kv_b = mul(row2("kv_b"), w_b, pair(vb))
-        nc.vector.tensor_copy(out=kappa_column(2), in_=w_v0)
-        mul(kappa_column(3), w_b, pair(imu))
+            to_b_c = mul(row("to_b_c"), iden, to_b_sum)
+            to_res_sum = sub(row("to_res_sum"), y2_live_keep_p, beta_phi_pb)
+            top_m = sub(row("top_m"), slope_km, hm)
+            on_b_a = mul(row("on_b_a"), alpha_beta2, a_first)
+            sq_b_first = mul(row("sq_b_first"), alpha_sq2, b_first)
+            dres_a = add(row("dres_a"), p1_pi, mb_a_first)
 
-        add(kappa_column(0), kx_a, kx_b)
-        add(kappa_column(1), kv_a, kv_b)
+            to_res_c = mul(row("to_res_c"), iden, to_res_sum)
+            coef_m = mul(row("coef_m"), top_m, free_irm3)
+            mb_to_b_c = mul(row("mb_to_b_c"), beta2_mb, to_b_c)
+            ab_to_b_c = mul(row("ab_to_b_c"), alpha_beta2, to_b_c)
 
-        add(to_kappa[:, :, 1, 1], to_kappa[:, :, 1, 1], mu)
+            m2_to_res_c = mul(row("m2_to_res_c"), alpha2_m2, to_res_c)
+            sq_to_res_c = mul(row("sq_to_res_c"), alpha_sq2, to_res_c)
+            dres_c_part = add(row("dres_c_part"), p1_phi_pmv, mb_to_b_c)
+            on_b_c = add(row("on_b_c"), ab_to_b_c, lost_pb)
+            on_mv_a = mul(row("on_mv_a"), coef_m, dres_a)
+            coef_dres_b = mul(row("coef_dres_b"), coef_m, m2_b_first)
+
+            dres_c = add(row("dres_c"), dres_c_part, m2_to_res_c)
+            on_mv_c_part = add(row("on_mv_c_part"), sq_to_res_c, lost_pa)
+            on_mv_b = add(row("on_mv_b"), coef_dres_b, sq_b_first)
+            on_b_c_pa = mul(row("on_b_c_pa"), on_b_c, pa)
+
+            coef_dres_c = mul(row("coef_dres_c"), coef_m, dres_c)
+            on_both = chain.tile([P, 2, 2, TILES], F32, name="on_both")
+            sub(on_both[:, 1, 0, :], on_b_a, on_b_c_pa)
+            fused(on_both[:, 1, 1, :], on_b_c, -1.0, pb, MUL, MUL)
+            mu_mb = mul(row("mu_mb"), mu, mb)
+            nu_bb = scale(row("nu_bb"), nu, bb)
+
+            on_mv_c = add(row("on_mv_c"), coef_dres_c, on_mv_c_part)
+            vb = add(row("vb"), mu_mb, nu_bb)
+            nc.vector.memset(to_kappa[:], 0.0)
+
+            on_mv_c_pa = mul(row("on_mv_c_pa"), on_mv_c, pa)
+            on_mv_c_pb = mul(row("on_mv_c_pb"), on_mv_c, pb)
+            nc.vector.tensor_copy(out=to_kappa[:, :, 0, 0], in_=mu)
+
+            sub(on_both[:, 0, 0, :], on_mv_a, on_mv_c_pa)
+            fused(on_both[:, 0, 1, :], on_mv_c_pb, -1.0, on_mv_b, MUL, SUB)
+
+            in_v0_b = chain.tile([P, 2, 2, TILES], F32, name="in_v0_b")
+            mul(in_v0_b[:, :, 0, :], on_both[:, :, 0, :], pair(imu))
+
+            nu_first = mul(row2("nu_first"), in_v0_b[:, :, 0, :], pair(nu))
+
+            sub(in_v0_b[:, :, 1, :], on_both[:, :, 1, :], nu_first)
+
+            weights = chain.tile([P, 2, 2, TILES], F32, name="weights")
+            mul(weights[:, 0], in_v0_b[:, 0], pair(imu))
+
+            nu_on_v0 = mul(row2("nu_on_v0"), weights[:, 0], pair(nu))
+
+            sub(weights[:, 1], in_v0_b[:, 1], nu_on_v0)
+
+            def kappa_column(m):
+                return to_kappa[:, :, 1:3, m].rearrange("p i k -> p k i")
+
+            w_v0, w_b = weights[:, :, 0, :], weights[:, :, 1, :]
+            kx_a = mul(row2("kx_a"), w_v0, pair(xv))
+            kx_b = mul(row2("kx_b"), w_b, pair(xb))
+            kv_a = mul(row2("kv_a"), w_v0, pair(vv))
+            kv_b = mul(row2("kv_b"), w_b, pair(vb))
+            nc.vector.tensor_copy(out=kappa_column(2), in_=w_v0)
+            mul(kappa_column(3), w_b, pair(imu))
+
+            add(kappa_column(0), kx_a, kx_b)
+            add(kappa_column(1), kv_a, kv_b)
+
+            add(to_kappa[:, :, 1, 1], to_kappa[:, :, 1, 1], mu)
+
+        with tc.tile_pool(name="chain", bufs=1) as chain:
+            coefficients(chain)
+        post = ctx.enter_context(tc.tile_pool(name="post", bufs=2))
 
         turned_sums = {}
         d_rows = {}
@@ -634,20 +753,21 @@ def tile_paralleldirectpoincaredynamics_v_kernel(
             v0 = mv_all[:, i, :]
             nc.scalar.activation(out=v0, in_=v0, func=ACT.Copy, scale=mu[:, i : i + 1])
             fused(v0, b_all[:], nu[:, i : i + 1], v0, MUL, ADD)
-            while ready_issued[0] < 2 * TILES + (i + 1) * T:
+            while ready_issued[0] < 2 * TILES + min(i + 1, VECTOR_X_TILES) * T:
                 ready_dot()
-            total = banks()
+            total = banks("total")
             for t in range(T):
-                term = times_row_factor(g_tiles[i][:, t, :], a_scaled[:, i, t : t + 1])
+                on_vector = t % 2 == 0 and t // 2 < VECTOR_TERMS
+                term = times_row_factor(g_tiles[i][:, t, :], a_scaled[:, i, t : t + 1], on_vector)
                 add_turned(total, [term], t == 0, t == T - 1)
             return total
 
         def inner_products(i, total):
             for t in range(T):
                 dot(dots[:, i, 1, t : t + 1], g_tiles[i][:, t, :], mv_all[:, i, :], N)
-            turned_sums[i] = work.tile([P, N], F32, name="turned_sum", bufs=3)
+            turned_sums[i] = post.tile([P, N], F32, name="turned_sum", bufs=3)
             out_of_psum(turned_sums[i], total)
-            s_b = psum.tile([P, BANK], F32, name="bank")
+            s_b = psum.tile([P, BANK], F32, name="s_b", bufs=1)
             for k in range(BLOCKS):
                 nc.tensor.matmul(
                     out=s_b[:, :B_COPIES],
@@ -673,32 +793,28 @@ def tile_paralleldirectpoincaredynamics_v_kernel(
             )
 
         def finish(i):
-            mix = banks()
+            mix = banks("mix")
             for k, src in enumerate((x_all[:, i, :], mv_all[:, i, :], b_all[:])):
                 add_turned(mix, [times_row_factor(src, kappa[:, i, k : k + 1])], k == 0, k == 2)
-            turned_mix = work.tile([P, N], F32, name="turned_mix")
+            turned_mix = post.tile([P, N], F32, name="turned_mix")
             out_of_psum(turned_mix, mix)
-            dmv = banks()
+            dmv = banks("mix")
             add_turned(dmv, [turned_sums[i], turned_mix], True, True)
             out_of_psum(d_rows[i // PACK][:, i % PACK, :], dmv)
 
         for i in range(TILES + 1):
+            if VECTOR_X_TILES <= i + 1 < TILES:
+                x_dots_on_tensor(i + 1)
+            if i + 2 < TILES:
+                load_g(i + 2)
             if i < TILES:
                 if i % PACK == 0:
                     d_rows[i // PACK] = stage.tile([P, PACK, N], BF16, name="rows")
                 total = weighted_sum(i)
             if i > 0:
                 finish(i - 1)
-            c = i - V_INIT_AT
-            if c == 0:
-                v_rows = grads.tile([P, PASSES, PACK, K], BF16, name="g")
-                nc.sync.dma_start(out=v_rows[:].rearrange("p c j k -> p c (j k)"), in_=v_view)
-            if 0 <= c < PASSES:
-                v_halves = regroup_pass(v_rows[:, c], nc.scalar.copy)
             if i < TILES:
                 inner_products(i, total)
-            if 0 <= c < PASSES:
-                quantise_pass(v_halves, v_codes[:, c, :], v_scales[:, c, :], E4M3_X4)
 
         for c in range(PASSES):
             d_halves = regroup_pass(d_rows[c][:], nc.vector.tensor_copy)
@@ -709,7 +825,7 @@ def tile_paralleldirectpoincaredynamics_v_kernel(
             result = work.tile([P, K], F32, name="scaled", bufs=4)
             for h in range(K // BANK):
                 half = slice(h * BANK, (h + 1) * BANK)
-                acc = psum.tile([P, BANK], F32, name="bank")
+                acc = psum.tile([P, BANK], F32, name=("total", "mix", "turn")[(m * (K // BANK) + h) % 3])
                 for c in range(PASSES):
                     nc.tensor.matmul_mx(
                         out=acc[:],

@@ -32,8 +32,9 @@ WORD_BLOCKS = N // (WORD * P)
 ROW_GROUP = P // (T * WORD)
 ROW_GROUPS = P // ROW_GROUP
 PAIRED = ROW_GROUP * WORD
-VECTOR_X_TILES = 2
-VECTOR_TERMS = 4
+TENSOR_X_TILES = 4
+VECTOR_X_TILES = TILES - TENSOR_X_TILES
+VECTOR_TERMS = 2
 
 EPS = 1e-7
 EPS_SQ = EPS * EPS
@@ -55,8 +56,6 @@ def tile_paralleldirectpoincaredynamics_v_kernel(
         unread = ctx.enter_context(tc.tile_pool(name="unread", bufs=3))
         stage = ctx.enter_context(tc.tile_pool(name="stage", bufs=2))
         work = ctx.enter_context(tc.tile_pool(name="work", bufs=2))
-        early = ctx.enter_context(tc.tile_pool(name="early", bufs=2))
-        psum = ctx.enter_context(tc.psum_pool(name="psum", bufs=2))
 
         x_all = keep.tile([P, TILES, N], BF16, name="x_all")
         mv_all = keep.tile([P, TILES, N], F32, name="mv_all")
@@ -196,13 +195,15 @@ def tile_paralleldirectpoincaredynamics_v_kernel(
                     dot(xm[:, i : i + 1], x_all[:, i, :], mv_all[:, i, :], N)
             elif n < 2 * TILES + VECTOR_X_TILES * T:
                 i, t = divmod(n - 2 * TILES, T)
+                load_g(i)
                 dot(dots[:, i, 0, t : t + 1], g_tiles[i][:, t, :], x_all[:, i, :], N)
 
         def load_g(i):
-            g_tiles[i] = grads.tile([P, T, N], BF16, name="g")
-            nc.sync.dma_start(
-                out=g_tiles[i][:].rearrange("p t n -> p (t n)"), in_=g_view[i // PACK, i % PACK]
-            )
+            if i < TILES and i not in g_tiles:
+                g_tiles[i] = grads.tile([P, T, N], BF16, name="g")
+                nc.sync.dma_start(
+                    out=g_tiles[i][:].rearrange("p t n -> p (t n)"), in_=g_view[i // PACK, i % PACK]
+                )
 
         halves_fetched = {}
         HALVES_AHEAD = [(i, h) for i in range(VECTOR_X_TILES, TILES) for h in range(HALVES)]
@@ -217,11 +218,6 @@ def tile_paralleldirectpoincaredynamics_v_kernel(
                         :, :, h * BANK : (h + 1) * BANK
                     ],
                 )
-
-        for s in range(2):
-            fetch_half(s)
-        for i in range(VECTOR_X_TILES):
-            load_g(i)
 
         v_codes = keep.tile([P, PASSES, K], U32, name="v_codes", align_bytes=64)
         v_scales = keep.tile([P, PASSES, K], U8, name="v_scales", align_bytes=64)
@@ -239,8 +235,8 @@ def tile_paralleldirectpoincaredynamics_v_kernel(
         b_cols = keep.tile([P, BLOCKS, B_COPIES], F32, name="b_cols")
 
 
-        def banks(role):
-            return [psum.tile([P, BANK], F32, name=role) for h in range(HALVES)]
+        def banks():
+            return [psum.tile([P, BANK], F32, name="bank") for h in range(HALVES)]
 
         def add_turned(total, terms, first, last):
             for h in range(HALVES):
@@ -268,25 +264,15 @@ def tile_paralleldirectpoincaredynamics_v_kernel(
                 nc.scalar.activation(out=scaled[:], in_=src, func=ACT.Copy, scale=factor)
             return scaled
 
-        b_f32 = work.tile([P, N], F32, name="scaled", bufs=4)
-        nc.vector.tensor_copy(out=b_f32[:], in_=b_all[:])
-        b_turned = banks("total")
-        add_turned(b_turned, [b_f32], True, True)
-        for h in range(HALVES):
-            nc.scalar.copy(
-                out=b_cols[:, h * BLOCKS_PER_BANK : (h + 1) * BLOCKS_PER_BANK, :],
-                in_=b_turned[h][:].rearrange("p (q r) -> p q r", r=P)[:, :, :B_COPIES],
-            )
-
         def x_dots_on_tensor(i):
             x_words = x_all[:, i, :].bitcast(F32)
-            x_turned_psum = psum.tile([P, WORD_BLOCKS, P], F32, name="turn", bufs=2)
+            x_turned_psum = ahead_psum.tile([P, WORD_BLOCKS, P], F32, name="turn")
             for k in range(WORD_BLOCKS):
                 nc.tensor.transpose(x_turned_psum[:, k, :], x_words[:, k * P : (k + 1) * P], identity[:])
             x_turned = work.tile([P, WORD_BLOCKS, P], F32, name="x_turned")
             nc.scalar.copy(out=x_turned[:], in_=x_turned_psum[:])
             x_pairs = x_turned[:].bitcast(BF16)
-            crossed = psum.tile([P, ROW_GROUPS, PAIRED], F32, name="crossed", bufs=1)
+            crossed = ahead_psum.tile([P, ROW_GROUPS, PAIRED], F32, name="crossed", bufs=2)
             blocks_per_half = WORD_BLOCKS // HALVES
 
             def turn(k):
@@ -295,7 +281,7 @@ def tile_paralleldirectpoincaredynamics_v_kernel(
                 g_words = halves_fetched[s][:].bitcast(F32)
                 g_turned = work.tile([P, ROW_GROUPS, T, ROW_GROUP], F32, name="g_turned")
                 for first in range(0, T, BLOCKS_PER_BANK):
-                    g_turned_psum = psum.tile([P, BLOCKS_PER_BANK, P], F32, name="turn", bufs=2)
+                    g_turned_psum = ahead_psum.tile([P, BLOCKS_PER_BANK, P], F32, name="turn")
                     for t in range(BLOCKS_PER_BANK):
                         nc.tensor.transpose(
                             g_turned_psum[:, t, :], g_words[:, first + t, q * P : (q + 1) * P], identity[:]
@@ -330,7 +316,7 @@ def tile_paralleldirectpoincaredynamics_v_kernel(
                 .to_broadcast([P, WORD, ROW_GROUPS, ROW_GROUP]),
                 op=MUL,
             )
-            by_row = psum.tile([P, T], F32, name="turn", bufs=2)
+            by_row = ahead_psum.tile([P, T], F32, name="turn")
             for e in range(WORD):
                 nc.tensor.matmul(
                     out=by_row[:],
@@ -742,9 +728,25 @@ def tile_paralleldirectpoincaredynamics_v_kernel(
 
             add(to_kappa[:, :, 1, 1], to_kappa[:, :, 1, 1], mu)
 
-        with tc.tile_pool(name="chain", bufs=1) as chain:
-            coefficients(chain)
+        with tc.psum_pool(name="ahead_psum", bufs=4) as ahead_psum:
+            with tc.tile_pool(name="early", bufs=2) as early:
+                for s in range(2):
+                    fetch_half(s)
+                b_f32 = work.tile([P, N], F32, name="scaled", bufs=4)
+                nc.vector.tensor_copy(out=b_f32[:], in_=b_all[:])
+                b_turned = [ahead_psum.tile([P, BANK], F32, name="turn") for h in range(HALVES)]
+                add_turned(b_turned, [b_f32], True, True)
+                for h in range(HALVES):
+                    nc.scalar.copy(
+                        out=b_cols[:, h * BLOCKS_PER_BANK : (h + 1) * BLOCKS_PER_BANK, :],
+                        in_=b_turned[h][:].rearrange("p (q r) -> p q r", r=P)[:, :, :B_COPIES],
+                    )
+                with tc.tile_pool(name="chain", bufs=1) as chain:
+                    coefficients(chain)
+                for i in range(VECTOR_X_TILES, TILES):
+                    x_dots_on_tensor(i)
         post = ctx.enter_context(tc.tile_pool(name="post", bufs=2))
+        psum = ctx.enter_context(tc.psum_pool(name="psum", bufs=8))
 
         turned_sums = {}
         d_rows = {}
@@ -755,7 +757,7 @@ def tile_paralleldirectpoincaredynamics_v_kernel(
             fused(v0, b_all[:], nu[:, i : i + 1], v0, MUL, ADD)
             while ready_issued[0] < 2 * TILES + min(i + 1, VECTOR_X_TILES) * T:
                 ready_dot()
-            total = banks("total")
+            total = banks()
             for t in range(T):
                 on_vector = t % 2 == 0 and t // 2 < VECTOR_TERMS
                 term = times_row_factor(g_tiles[i][:, t, :], a_scaled[:, i, t : t + 1], on_vector)
@@ -767,7 +769,7 @@ def tile_paralleldirectpoincaredynamics_v_kernel(
                 dot(dots[:, i, 1, t : t + 1], g_tiles[i][:, t, :], mv_all[:, i, :], N)
             turned_sums[i] = post.tile([P, N], F32, name="turned_sum", bufs=3)
             out_of_psum(turned_sums[i], total)
-            s_b = psum.tile([P, BANK], F32, name="s_b", bufs=1)
+            s_b = psum.tile([P, BANK], F32, name="bank")
             for k in range(BLOCKS):
                 nc.tensor.matmul(
                     out=s_b[:, :B_COPIES],
@@ -793,20 +795,18 @@ def tile_paralleldirectpoincaredynamics_v_kernel(
             )
 
         def finish(i):
-            mix = banks("mix")
+            mix = banks()
             for k, src in enumerate((x_all[:, i, :], mv_all[:, i, :], b_all[:])):
                 add_turned(mix, [times_row_factor(src, kappa[:, i, k : k + 1])], k == 0, k == 2)
             turned_mix = post.tile([P, N], F32, name="turned_mix")
             out_of_psum(turned_mix, mix)
-            dmv = banks("mix")
+            dmv = banks()
             add_turned(dmv, [turned_sums[i], turned_mix], True, True)
             out_of_psum(d_rows[i // PACK][:, i % PACK, :], dmv)
 
         for i in range(TILES + 1):
-            if VECTOR_X_TILES <= i + 1 < TILES:
-                x_dots_on_tensor(i + 1)
-            if i + 2 < TILES:
-                load_g(i + 2)
+            load_g(i)
+            load_g(i + 1)
             if i < TILES:
                 if i % PACK == 0:
                     d_rows[i // PACK] = stage.tile([P, PACK, N], BF16, name="rows")
@@ -825,7 +825,7 @@ def tile_paralleldirectpoincaredynamics_v_kernel(
             result = work.tile([P, K], F32, name="scaled", bufs=4)
             for h in range(K // BANK):
                 half = slice(h * BANK, (h + 1) * BANK)
-                acc = psum.tile([P, BANK], F32, name=("total", "mix", "turn")[(m * (K // BANK) + h) % 3])
+                acc = psum.tile([P, BANK], F32, name="bank")
                 for c in range(PASSES):
                     nc.tensor.matmul_mx(
                         out=acc[:],

@@ -34,7 +34,7 @@ ROW_GROUPS = P // ROW_GROUP
 PAIRED = ROW_GROUP * WORD
 TENSOR_X_TILES = 4
 VECTOR_X_TILES = TILES - TENSOR_X_TILES
-VECTOR_TERMS = 2
+VECTOR_TERMS = 4
 
 EPS = 1e-7
 EPS_SQ = EPS * EPS
@@ -749,6 +749,7 @@ def tile_paralleldirectpoincaredynamics_v_kernel(
         psum = ctx.enter_context(tc.psum_pool(name="psum", bufs=8))
 
         turned_sums = {}
+        turned_back = []
         d_rows = {}
 
         def weighted_sum(i):
@@ -769,6 +770,9 @@ def tile_paralleldirectpoincaredynamics_v_kernel(
                 dot(dots[:, i, 1, t : t + 1], g_tiles[i][:, t, :], mv_all[:, i, :], N)
             turned_sums[i] = post.tile([P, N], F32, name="turned_sum", bufs=3)
             out_of_psum(turned_sums[i], total)
+            if i == TILES - 1:
+                turned_back.extend(banks())
+                add_turned(turned_back, [turned_sums[i]], True, True)
             s_b = psum.tile([P, BANK], F32, name="bank")
             for k in range(BLOCKS):
                 nc.tensor.matmul(
@@ -811,33 +815,91 @@ def tile_paralleldirectpoincaredynamics_v_kernel(
                 if i % PACK == 0:
                     d_rows[i // PACK] = stage.tile([P, PACK, N], BF16, name="rows")
                 total = weighted_sum(i)
-            if i > 0:
+            if 0 < i < TILES:
                 finish(i - 1)
+            if i % PACK == 2 and i > PACK:
+                d_halves = regroup_pass(d_rows[i // PACK - 1][:], nc.scalar.copy)
             if i < TILES:
                 inner_products(i, total)
+            if i % PACK == 2 and i > PACK:
+                c = i // PACK - 1
+                quantise_pass(d_halves, d_codes[:, c, :], d_scales[:, c, :], E5M2_X4)
 
-        for c in range(PASSES):
-            d_halves = regroup_pass(d_rows[c][:], nc.vector.tensor_copy)
-            quantise_pass(d_halves, d_codes[:, c, :], d_scales[:, c, :], E5M2_X4)
+        groups = [(m, h) for m in range(BLOCKS) for h in range(K // BANK)]
+        WAVE = 8
+        accs = {}
+        results = {}
 
-        for m in range(BLOCKS):
+        def product(m, h, c):
             of_block = slice(m * P, (m + 1) * P)
-            result = work.tile([P, K], F32, name="scaled", bufs=4)
-            for h in range(K // BANK):
-                half = slice(h * BANK, (h + 1) * BANK)
-                acc = psum.tile([P, BANK], F32, name="bank")
-                for c in range(PASSES):
-                    nc.tensor.matmul_mx(
-                        out=acc[:],
-                        lhsT=d_codes[:, c, of_block].bitcast(E5M2_X4),
-                        lhsT_scale=d_scales[:, c, of_block],
-                        rhs=v_codes[:, c, half].bitcast(E4M3_X4),
-                        rhs_scale=v_scales[:, c, half],
-                        start=(c == 0),
-                        stop=(c == PASSES - 1),
-                    )
-                if h % 2 == 0:
-                    nc.scalar.copy(out=result[:, half], in_=acc[:])
-                else:
-                    nc.vector.tensor_copy(out=result[:, half], in_=acc[:])
-            nc.sync.dma_start(out=out[of_block, :], in_=result[:])
+            half = slice(h * BANK, (h + 1) * BANK)
+            nc.tensor.matmul_mx(
+                out=accs[(m, h)][:],
+                lhsT=d_codes[:, c, of_block].bitcast(E5M2_X4),
+                lhsT_scale=d_scales[:, c, of_block],
+                rhs=v_codes[:, c, half].bitcast(E4M3_X4),
+                rhs_scale=v_scales[:, c, half],
+                start=(c == 0),
+                stop=(c == PASSES - 1),
+            )
+
+        def all_but_the_last_pass(wave):
+            for m, h in wave:
+                accs[(m, h)] = psum.tile([P, BANK], F32, name="bank")
+                for c in range(PASSES - 1):
+                    product(m, h, c)
+
+        def last_pass(wave):
+            for m, h in wave:
+                product(m, h, PASSES - 1)
+                if h == 0:
+                    results[m] = work.tile([P, K], F32, name="scaled", bufs=4)
+                copy = nc.scalar.copy if h % 2 == 0 else nc.vector.tensor_copy
+                copy(out=results[m][:, h * BANK : (h + 1) * BANK], in_=accs[(m, h)][:])
+                if h == K // BANK - 1:
+                    nc.sync.dma_start(out=out[m * P : (m + 1) * P, :], in_=results[m][:])
+
+        all_but_the_last_pass(groups[:WAVE])
+
+        QUARTER = N // 4
+        last = TILES - 1
+        last_rows = d_rows[PASSES - 1]
+        for pair in range(0, N // QUARTER, 2):
+            both = (pair, pair + 1)
+            columns = {q: slice(q * QUARTER, (q + 1) * QUARTER) for q in both}
+            with_x, with_v, grouped = {}, {}, {}
+            for q in both:
+                with_x[q] = post.tile([P, QUARTER], F32, name="with_x")
+                in_bank = slice((q * QUARTER) % BANK, (q * QUARTER) % BANK + QUARTER)
+                fused(
+                    with_x[q][:],
+                    x_all[:, last, columns[q]],
+                    kappa[:, last, 0:1],
+                    turned_back[q * QUARTER // BANK][:, in_bank],
+                    MUL,
+                    ADD,
+                )
+            for q in both:
+                with_v[q] = post.tile([P, QUARTER], F32, name="with_v")
+                fused(with_v[q][:], mv_all[:, last, columns[q]], kappa[:, last, 1:2], with_x[q][:], MUL, ADD)
+            for q in both:
+                fused(
+                    last_rows[:, last % PACK, columns[q]], b_all[:, columns[q]], kappa[:, last, 2:3], with_v[q][:], MUL, ADD
+                )
+            for q in both:
+                grouped[q] = stage.tile([P, QUARTER, PACK], BF16, name="grouped", align_bytes=64)
+                nc.vector.tensor_copy(
+                    out=grouped[q][:].rearrange("p (c r) j -> p c j r", r=4),
+                    in_=last_rows[:, :, columns[q]].rearrange("p j (c r) -> p c j r", r=4),
+                )
+            for q in both:
+                nc.vector.quantize_mx(
+                    out=d_codes[:, PASSES - 1, columns[q]].bitcast(E5M2_X4),
+                    scales=d_scales[:, PASSES - 1, columns[q]],
+                    in_=grouped[q][:].rearrange("p n j -> p (n j)"),
+                )
+
+        for first in range(0, len(groups), WAVE):
+            if first > 0:
+                all_but_the_last_pass(groups[first : first + WAVE])
+            last_pass(groups[first : first + WAVE])

@@ -783,7 +783,7 @@ def tile_paralleldirectpoincaredynamics_v_kernel(
                     stop=(k == BLOCKS - 1),
                 )
             ready_dot()
-            nc.vector.tensor_copy(out=inputs[:, i, 3:4], in_=s_b[:, 0:1])
+            nc.scalar.copy(out=inputs[:, i, 3:4], in_=s_b[:, 0:1])
             terms = work.tile([P, 3, 2, T], F32, name="terms")
             mul(terms[:], from_dots[:, :, :, i, :], dots[:, i].unsqueeze(1).to_broadcast([P, 3, 2, T]))
             ready_dot()
@@ -800,13 +800,15 @@ def tile_paralleldirectpoincaredynamics_v_kernel(
 
         def finish(i):
             mix = banks()
-            for k, src in enumerate((x_all[:, i, :], mv_all[:, i, :], b_all[:])):
-                add_turned(mix, [times_row_factor(src, kappa[:, i, k : k + 1])], k == 0, k == 2)
+            for k, src in enumerate((x_all[:, i, :], mv_all[:, i, :])):
+                add_turned(mix, [times_row_factor(src, kappa[:, i, k : k + 1])], k == 0, k == 1)
             turned_mix = post.tile([P, N], F32, name="turned_mix")
             out_of_psum(turned_mix, mix)
             dmv = banks()
             add_turned(dmv, [turned_sums[i], turned_mix], True, True)
-            out_of_psum(d_rows[i // PACK][:, i % PACK, :], dmv)
+            for h in range(HALVES):
+                half = slice(h * BANK, (h + 1) * BANK)
+                fused(d_rows[i // PACK][:, i % PACK, half], b_all[:, half], kappa[:, i, 2:3], dmv[h][:], MUL, ADD)
 
         for i in range(TILES + 1):
             load_g(i)
@@ -855,9 +857,9 @@ def tile_paralleldirectpoincaredynamics_v_kernel(
                 if h == 0:
                     results[m] = work.tile([P, K], F32, name="scaled", bufs=4)
                 copy = nc.scalar.copy if h % 2 == 0 else nc.vector.tensor_copy
-                copy(out=results[m][:, h * BANK : (h + 1) * BANK], in_=accs[(m, h)][:])
-                if h == K // BANK - 1:
-                    nc.sync.dma_start(out=out[m * P : (m + 1) * P, :], in_=results[m][:])
+                half = slice(h * BANK, (h + 1) * BANK)
+                copy(out=results[m][:, half], in_=accs[(m, h)][:])
+                nc.sync.dma_start(out=out[m * P : (m + 1) * P, half], in_=results[m][:, half])
 
         all_but_the_last_pass(groups[:WAVE])
 
@@ -888,7 +890,8 @@ def tile_paralleldirectpoincaredynamics_v_kernel(
                 )
             for q in both:
                 grouped[q] = stage.tile([P, QUARTER, PACK], BF16, name="grouped", align_bytes=64)
-                nc.vector.tensor_copy(
+                copy = nc.vector.tensor_copy if q == pair else nc.scalar.copy
+                copy(
                     out=grouped[q][:].rearrange("p (c r) j -> p c j r", r=4),
                     in_=last_rows[:, :, columns[q]].rearrange("p j (c r) -> p c j r", r=4),
                 )

@@ -768,7 +768,10 @@ def tile_paralleldirectpoincaredynamics_v_kernel(
         def inner_products(i, total):
             for t in range(T):
                 dot(dots[:, i, 1, t : t + 1], g_tiles[i][:, t, :], mv_all[:, i, :], N)
-            turned_sums[i] = post.tile([P, N], F32, name="turned_sum", bufs=3)
+            if i < len(first_sums):
+                turned_sums[i] = first_sums[i]
+            else:
+                turned_sums[i] = post.tile([P, N], F32, name="turned_sum", bufs=3)
             out_of_psum(turned_sums[i], total)
             if i == TILES - 1:
                 turned_back.extend(banks())
@@ -809,6 +812,9 @@ def tile_paralleldirectpoincaredynamics_v_kernel(
             for h in range(HALVES):
                 half = slice(h * BANK, (h + 1) * BANK)
                 fused(d_rows[i // PACK][:, i % PACK, half], b_all[:, half], kappa[:, i, 2:3], dmv[h][:], MUL, ADD)
+
+        first_pair = stage.tile([P, 2, N], F32, name="rows")
+        first_sums = [first_pair[:, i, :] for i in range(2)]
 
         for i in range(TILES + 1):
             load_g(i)

@@ -34,7 +34,7 @@ ROW_GROUPS = P // ROW_GROUP
 PAIRED = ROW_GROUP * WORD
 TENSOR_X_TILES = 4
 VECTOR_X_TILES = TILES - TENSOR_X_TILES
-VECTOR_TERMS = 4
+VECTOR_TERMS = 2
 
 EPS = 1e-7
 EPS_SQ = EPS * EPS
@@ -229,6 +229,7 @@ def tile_paralleldirectpoincaredynamics_v_kernel(
         to_kappa = keep.tile([P, TILES, 3, 4], F32, name="to_kappa")
         mu = keep.tile([P, TILES], F32, name="mu")
         nu = keep.tile([P, TILES], F32, name="nu")
+        nu_over_mu = keep.tile([P, TILES], F32, name="nu_over_mu")
         dots = keep.tile([P, TILES, 2, T], F32, name="dots")
         inputs = keep.tile([P, TILES, 4], F32, name="inputs")
         kappa = keep.tile([P, TILES, 3], F32, name="kappa")
@@ -491,10 +492,12 @@ def tile_paralleldirectpoincaredynamics_v_kernel(
             vv = mul(row("vv"), pi_sq, pp)
             mu_xm = mul(row("mu_xm"), mu, xm)
             nu_xb = mul(row("nu_xb"), nu, xb)
+            imu = inverse(row("imu"), mu)
 
             rt = at_least(grid("rt"), c_r0, EPS)
             free_t = above(grid("free_t"), c_r0, EPS)
             xv = add(row("xv"), mu_xm, nu_xb)
+            mul(nu_over_mu, nu, imu)
 
             k2_rt = mul(grid("k2_rt"), rt, over_t(k2))
             irt = inverse(grid("irt"), rt)
@@ -628,7 +631,6 @@ def tile_paralleldirectpoincaredynamics_v_kernel(
             lost = mul(row("lost"), pa, phi)
             alpha_sq2 = fused(row("alpha_sq2"), alpha, 2.0, alpha, MUL, MUL)
             alpha_beta2 = scale(row("alpha_beta2"), alpha, beta2)
-            imu = inverse(row("imu"), mu)
 
             v_c_q1 = mul(grid("v_c_q1"), v_c, q1)
             v_c_q2s = mul(grid("v_c_q2s"), v_c, q2s)
@@ -727,6 +729,9 @@ def tile_paralleldirectpoincaredynamics_v_kernel(
             add(kappa_column(1), kv_a, kv_b)
 
             add(to_kappa[:, :, 1, 1], to_kappa[:, :, 1, 1], mu)
+            mul(from_dots[:, :, 1], from_dots[:, :, 1], mu[:].unsqueeze(1).unsqueeze(3).to_broadcast([P, 3, TILES, T]))
+
+            mul(to_kappa[:, :, 1, :], to_kappa[:, :, 1, :], mu[:].unsqueeze(2).to_broadcast([P, TILES, 4]))
 
         with tc.psum_pool(name="ahead_psum", bufs=4) as ahead_psum:
             with tc.tile_pool(name="early", bufs=2) as early:
@@ -753,9 +758,8 @@ def tile_paralleldirectpoincaredynamics_v_kernel(
         d_rows = {}
 
         def weighted_sum(i):
-            v0 = mv_all[:, i, :]
-            nc.scalar.activation(out=v0, in_=v0, func=ACT.Copy, scale=mu[:, i : i + 1])
-            fused(v0, b_all[:], nu[:, i : i + 1], v0, MUL, ADD)
+            w = mv_all[:, i, :]
+            fused(w, b_all[:], nu_over_mu[:, i : i + 1], w, MUL, ADD)
             while ready_issued[0] < 2 * TILES + min(i + 1, VECTOR_X_TILES) * T:
                 ready_dot()
             total = banks()
@@ -765,9 +769,7 @@ def tile_paralleldirectpoincaredynamics_v_kernel(
                 add_turned(total, [term], t == 0, t == T - 1)
             return total
 
-        def inner_products(i, total):
-            for t in range(T):
-                dot(dots[:, i, 1, t : t + 1], g_tiles[i][:, t, :], mv_all[:, i, :], N)
+        def sum_against_b(i, total):
             if i < len(first_sums):
                 turned_sums[i] = first_sums[i]
             else:
@@ -785,8 +787,12 @@ def tile_paralleldirectpoincaredynamics_v_kernel(
                     start=(k == 0),
                     stop=(k == BLOCKS - 1),
                 )
-            ready_dot()
             nc.scalar.copy(out=inputs[:, i, 3:4], in_=s_b[:, 0:1])
+
+        def inner_products(i):
+            for t in range(T):
+                dot(dots[:, i, 1, t : t + 1], g_tiles[i][:, t, :], mv_all[:, i, :], N)
+            ready_dot()
             terms = work.tile([P, 3, 2, T], F32, name="terms")
             mul(terms[:], from_dots[:, :, :, i, :], dots[:, i].unsqueeze(1).to_broadcast([P, 3, 2, T]))
             ready_dot()
@@ -801,10 +807,15 @@ def tile_paralleldirectpoincaredynamics_v_kernel(
                 out=kappa[:, i, :], in_=kappa_terms[:], axis=mybir.AxisListType.X, op=ADD
             )
 
-        def finish(i):
-            mix = banks()
+        mixes = {}
+
+        def begin_finish(i):
+            mixes[i] = banks()
             for k, src in enumerate((x_all[:, i, :], mv_all[:, i, :])):
-                add_turned(mix, [times_row_factor(src, kappa[:, i, k : k + 1])], k == 0, k == 1)
+                add_turned(mixes[i], [times_row_factor(src, kappa[:, i, k : k + 1])], k == 0, k == 1)
+
+        def finish(i):
+            mix = mixes.pop(i)
             turned_mix = post.tile([P, N], F32, name="turned_mix")
             out_of_psum(turned_mix, mix)
             dmv = banks()
@@ -824,11 +835,15 @@ def tile_paralleldirectpoincaredynamics_v_kernel(
                     d_rows[i // PACK] = stage.tile([P, PACK, N], BF16, name="rows")
                 total = weighted_sum(i)
             if 0 < i < TILES:
+                begin_finish(i - 1)
+            if i < TILES:
+                sum_against_b(i, total)
+            if 0 < i < TILES:
                 finish(i - 1)
             if i % PACK == 2 and i > PACK:
                 d_halves = regroup_pass(d_rows[i // PACK - 1][:], nc.scalar.copy)
             if i < TILES:
-                inner_products(i, total)
+                inner_products(i)
             if i % PACK == 2 and i > PACK:
                 c = i // PACK - 1
                 quantise_pass(d_halves, d_codes[:, c, :], d_scales[:, c, :], E5M2_X4)

@@ -769,25 +769,29 @@ def tile_paralleldirectpoincaredynamics_v_kernel(
                 add_turned(total, [term], t == 0, t == T - 1)
             return total
 
+        sums_b = {}
+
         def sum_against_b(i, total):
             if i < len(first_sums):
                 turned_sums[i] = first_sums[i]
             else:
                 turned_sums[i] = post.tile([P, N], F32, name="turned_sum", bufs=3)
             out_of_psum(turned_sums[i], total)
-            if i == TILES - 1:
-                turned_back.extend(banks())
-                add_turned(turned_back, [turned_sums[i]], True, True)
-            s_b = psum.tile([P, BANK], F32, name="bank")
+            sums_b[i] = psum.tile([P, BANK], F32, name="bank")
             for k in range(BLOCKS):
                 nc.tensor.matmul(
-                    out=s_b[:, :B_COPIES],
+                    out=sums_b[i][:, :B_COPIES],
                     lhsT=turned_sums[i][:, k * P : (k + 1) * P],
                     rhs=b_cols[:, k, :],
                     start=(k == 0),
                     stop=(k == BLOCKS - 1),
                 )
-            nc.scalar.copy(out=inputs[:, i, 3:4], in_=s_b[:, 0:1])
+            if i == TILES - 1:
+                turned_back.extend(banks())
+                add_turned(turned_back, [turned_sums[i]], True, True)
+
+        def sum_against_b_out(i):
+            nc.scalar.copy(out=inputs[:, i, 3:4], in_=sums_b[i][:, 0:1])
 
         def inner_products(i):
             for t in range(T):
@@ -814,12 +818,15 @@ def tile_paralleldirectpoincaredynamics_v_kernel(
             for k, src in enumerate((x_all[:, i, :], mv_all[:, i, :])):
                 add_turned(mixes[i], [times_row_factor(src, kappa[:, i, k : k + 1])], k == 0, k == 1)
 
+        turned_mixes = {}
+
+        def mix_out(i):
+            turned_mixes[i] = post.tile([P, N], F32, name="turned_mix")
+            out_of_psum(turned_mixes[i], mixes.pop(i))
+
         def finish(i):
-            mix = mixes.pop(i)
-            turned_mix = post.tile([P, N], F32, name="turned_mix")
-            out_of_psum(turned_mix, mix)
             dmv = banks()
-            add_turned(dmv, [turned_sums[i], turned_mix], True, True)
+            add_turned(dmv, [turned_sums[i], turned_mixes.pop(i)], True, True)
             for h in range(HALVES):
                 half = slice(h * BANK, (h + 1) * BANK)
                 fused(d_rows[i // PACK][:, i % PACK, half], b_all[:, half], kappa[:, i, 2:3], dmv[h][:], MUL, ADD)
@@ -838,6 +845,10 @@ def tile_paralleldirectpoincaredynamics_v_kernel(
                 begin_finish(i - 1)
             if i < TILES:
                 sum_against_b(i, total)
+            if 0 < i < TILES:
+                mix_out(i - 1)
+            if i < TILES:
+                sum_against_b_out(i)
             if 0 < i < TILES:
                 finish(i - 1)
             if i % PACK == 2 and i > PACK:

from contextlib import ExitStack

import concourse.masks as masks
import concourse.mybir as mybir

F32 = mybir.dt.float32
BF16 = mybir.dt.bfloat16
U32 = mybir.dt.uint32
U8 = mybir.dt.uint8
E4M3_X4 = mybir.dt.float8_e4m3fn_x4
E5M2_X4 = mybir.dt.float8_e5m2_x4
ACT = mybir.ActivationFunctionType
MUL = mybir.AluOpType.mult
ADD = mybir.AluOpType.add
SUB = mybir.AluOpType.subtract

P = 128
ROWS = 1024
N = 1024
K = 1024
T = 8
PACK = 4
PASSES = ROWS // (P * PACK)
TILES = PASSES * PACK
BANK = 512
HALVES = N // BANK
BLOCKS = N // P
BLOCKS_PER_BANK = BANK // P
B_COPIES = 2
WORD = 2
WORD_BLOCKS = N // (WORD * P)
ROW_GROUP = P // (T * WORD)
ROW_GROUPS = P // ROW_GROUP
PAIRED = ROW_GROUP * WORD
TENSOR_X_TILES = 4
VECTOR_X_TILES = TILES - TENSOR_X_TILES
VECTOR_TERMS = 2

EPS = 1e-7
EPS_SQ = EPS * EPS
TINY = 1e-30
MAX_NORM = 1.0 - 1e-5
CLIP = 1.0 - 1e-5

FLOPS = 2 * ROWS * N * K
BYTES = 2 * (2 * ROWS * N + ROWS * T * N + N + 1) + 4 * (ROWS * N + ROWS) + 4 * N * K


def tile_paralleldirectpoincaredynamics_v_kernel(
    tc, z_0, v_init, W, b, step_sizes, mv, vn, grad_out, out
):
    nc = tc.nc
    with ExitStack() as ctx:
        keep = ctx.enter_context(tc.tile_pool(name="keep", bufs=1))
        grads = ctx.enter_context(tc.tile_pool(name="grads", bufs=3))
        unread = ctx.enter_context(tc.tile_pool(name="unread", bufs=3))
        stage = ctx.enter_context(tc.tile_pool(name="stage", bufs=2))
        work = ctx.enter_context(tc.tile_pool(name="work", bufs=2))

        x_all = keep.tile([P, TILES, N], BF16, name="x_all")
        mv_all = keep.tile([P, TILES, N], F32, name="mv_all")
        b_all = keep.tile([P, N], BF16, name="b_all")
        vn_row = keep.tile([P, TILES], F32, name="vn_row")
        logit = keep.tile([P, 1], BF16, name="logit")
        z_view = z_0.rearrange("(c p j) n -> c p (j n)", c=PASSES, p=P, j=PACK)
        mv_view = mv.rearrange("(c p j) n -> c p (j n)", c=PASSES, p=P, j=PACK)
        v_view = v_init.rearrange("(c p j) k -> p c (j k)", c=PASSES, p=P, j=PACK)
        g_view = grad_out.rearrange("(c p j) t n -> c j p (t n)", c=PASSES, p=P, j=PACK)

        with nc.allow_non_contiguous_dma(reason="one float32 a row: runs of 4 values"):
            nc.scalar.dma_start(
                out=vn_row[:].rearrange("p (c j) -> p c j", c=PASSES),
                in_=vn.rearrange("(c p j) o -> p c (j o)", c=PASSES, p=P, j=PACK),
            )
            nc.scalar.dma_start(out=logit[:], in_=step_sizes.partition_broadcast(P))
        nc.scalar.dma_start(out=b_all[:], in_=b.partition_broadcast(P))
        for j in range(PACK):
            nc.sync.dma_start(out=mv_all[:, j, :], in_=mv_view[0][:, j * N : (j + 1) * N])
        for whole, view, c in ((mv_all, mv_view, 1), (x_all, z_view, 0), (x_all, z_view, 1)):
            nc.sync.dma_start(
                out=whole[:, c * PACK : (c + 1) * PACK, :].rearrange("p j n -> p (j n)"), in_=view[c]
            )

        identity = keep.tile([P, P], F32, name="identity")
        masks.make_identity(nc, identity[:])
        same_pair = keep.tile([P, PAIRED], F32, name="same_pair")
        same_horizon = keep.tile([P, T], F32, name="same_horizon")
        nc.vector.tensor_reduce(
            out=same_pair[:],
            in_=identity[:].rearrange("p (t s) -> p s t", s=PAIRED),
            axis=mybir.AxisListType.X,
            op=ADD,
        )
        nc.vector.tensor_reduce(
            out=same_horizon[:],
            in_=identity[:].rearrange("p (t s) -> p t s", s=PAIRED),
            axis=mybir.AxisListType.X,
            op=ADD,
        )
        horizon = keep.tile([P, T], F32, name="horizon")
        for t in range(T):
            nc.vector.memset(horizon[:, t : t + 1], float(t + 1))

        def mul(dst, a, b_):
            nc.vector.tensor_tensor(out=dst, in0=a, in1=b_, op=MUL)
            return dst

        def add(dst, a, b_):
            nc.vector.tensor_tensor(out=dst, in0=a, in1=b_, op=ADD)
            return dst

        def sub(dst, a, b_):
            nc.vector.tensor_tensor(out=dst, in0=a, in1=b_, op=SUB)
            return dst

        def fused(dst, a, scalar, b_, op0, op1):
            nc.vector.scalar_tensor_tensor(out=dst, in0=a, scalar=scalar, in1=b_, op0=op0, op1=op1)
            return dst

        def scale(dst, a, s):
            nc.vector.tensor_scalar(out=dst, in0=a, scalar1=s, scalar2=None, op0=MUL)
            return dst

        def shift(dst, a, s):
            nc.vector.tensor_scalar(out=dst, in0=a, scalar1=s, scalar2=None, op0=ADD)
            return dst

        def affine(dst, a, s, offset):
            nc.vector.tensor_scalar(out=dst, in0=a, scalar1=s, scalar2=offset, op0=MUL, op1=ADD)
            return dst

        def at_least(dst, a, low):
            nc.vector.tensor_scalar(
                out=dst, in0=a, scalar1=low, scalar2=None, op0=mybir.AluOpType.max
            )
            return dst

        def above(dst, a, bound):
            nc.vector.tensor_scalar(
                out=dst, in0=a, scalar1=bound, scalar2=None, op0=mybir.AluOpType.is_gt
            )
            return dst

        def inverse(dst, a):
            nc.vector.reciprocal(out=dst, in_=a)
            return dst

        def table(dst, a, func, s=1.0):
            nc.scalar.activation(out=dst, in_=a, func=func, scale=s)
            return dst

        def dot(acc, a, b_, width):
            products = unread.tile([P, N], F32, name="products")
            nc.vector.scalar_tensor_tensor(
                out=products[:, :width], in0=a, scalar=1.0, in1=b_, op0=MUL, op1=MUL, accum_out=acc
            )

        def square_sum(acc, a):
            squares = unread.tile([P, N], BF16, name="squares", bufs=2)
            nc.scalar.activation(out=squares[:], in_=a, func=ACT.Square, accum_out=acc)

        def regroup_pass(rows, copy):
            halves = []
            for h in range(HALVES):
                grouped = stage.tile([P, BANK, PACK], BF16, name="grouped", align_bytes=64)
                copy(
                    out=grouped[:].rearrange("p (c r) j -> p c j r", r=4),
                    in_=rows[:, :, h * BANK : (h + 1) * BANK].rearrange("p j (c r) -> p c j r", r=4),
                )
                halves.append(grouped)
            return halves

        def quantise_pass(halves, codes, scales, packed_dtype):
            for h in range(HALVES):
                half = slice(h * BANK, (h + 1) * BANK)
                nc.vector.quantize_mx(
                    out=codes[:, half].bitcast(packed_dtype),
                    scales=scales[:, half],
                    in_=halves[h][:].rearrange("p n j -> p (n j)"),
                )

        g_tiles = {}
        xb = keep.tile([P, TILES], F32, name="xb")
        xm = keep.tile([P, TILES], F32, name="xm")
        ready_issued = [0]

        def ready_dot():
            n = ready_issued[0]
            ready_issued[0] += 1
            if n < 2 * TILES:
                i = n // 2
                if n % 2 == 0:
                    dot(xb[:, i : i + 1], x_all[:, i, :], b_all[:], N)
                else:
                    dot(xm[:, i : i + 1], x_all[:, i, :], mv_all[:, i, :], N)
            elif n < 2 * TILES + VECTOR_X_TILES * T:
                i, t = divmod(n - 2 * TILES, T)
                load_g(i)
                dot(dots[:, i, 0, t : t + 1], g_tiles[i][:, t, :], x_all[:, i, :], N)

        def load_g(i):
            if i < TILES and i not in g_tiles:
                g_tiles[i] = grads.tile([P, T, N], BF16, name="g")
                nc.sync.dma_start(
                    out=g_tiles[i][:].rearrange("p t n -> p (t n)"), in_=g_view[i // PACK, i % PACK]
                )

        halves_fetched = {}
        HALVES_AHEAD = [(i, h) for i in range(VECTOR_X_TILES, TILES) for h in range(HALVES)]

        def fetch_half(s):
            if s < len(HALVES_AHEAD):
                i, h = HALVES_AHEAD[s]
                halves_fetched[s] = early.tile([P, T, BANK], BF16, name="g_half")
                nc.sync.dma_start(
                    out=halves_fetched[s][:],
                    in_=g_view[i // PACK, i % PACK].rearrange("p (t n) -> p t n", t=T)[
                        :, :, h * BANK : (h + 1) * BANK
                    ],
                )

        v_codes = keep.tile([P, PASSES, K], U32, name="v_codes", align_bytes=64)
        v_scales = keep.tile([P, PASSES, K], U8, name="v_scales", align_bytes=64)
        d_codes = keep.tile([P, PASSES, N], U32, name="d_codes", align_bytes=64)
        d_scales = keep.tile([P, PASSES, N], U8, name="d_scales", align_bytes=64)

        a_scaled = keep.tile([P, TILES, T], F32, name="a_scaled")
        from_dots = keep.tile([P, 3, 2, TILES, T], F32, name="from_dots")
        to_kappa = keep.tile([P, TILES, 3, 4], F32, name="to_kappa")
        mu = keep.tile([P, TILES], F32, name="mu")
        nu = keep.tile([P, TILES], F32, name="nu")
        nu_over_mu = keep.tile([P, TILES], F32, name="nu_over_mu")
        dots = keep.tile([P, TILES, 2, T], F32, name="dots")
        inputs = keep.tile([P, TILES, 4], F32, name="inputs")
        kappa = keep.tile([P, TILES, 3], F32, name="kappa")
        b_cols = keep.tile([P, BLOCKS, B_COPIES], F32, name="b_cols")


        def banks():
            return [psum.tile([P, BANK], F32, name="bank") for h in range(HALVES)]

        def add_turned(total, terms, first, last):
            for h in range(HALVES):
                for m, term in enumerate(terms):
                    for q in range(BLOCKS_PER_BANK):
                        k = h * BLOCKS_PER_BANK + q
                        nc.tensor.matmul(
                            out=total[h][:, q * P : (q + 1) * P],
                            lhsT=term[:, k * P : (k + 1) * P],
                            rhs=identity[:],
                            is_transpose=True,
                            start=(first and m == 0 and q == 0),
                            stop=(last and m == len(terms) - 1 and q == BLOCKS_PER_BANK - 1),
                        )

        def out_of_psum(dst, total):
            for h in range(HALVES):
                nc.scalar.copy(out=dst[:, h * BANK : (h + 1) * BANK], in_=total[h][:])

        def times_row_factor(src, factor, on_vector=False):
            scaled = work.tile([P, N], F32, name="scaled", bufs=4)
            if on_vector:
                scale(scaled[:], src, factor)
            else:
                nc.scalar.activation(out=scaled[:], in_=src, func=ACT.Copy, scale=factor)
            return scaled

        def x_dots_on_tensor(i):
            x_words = x_all[:, i, :].bitcast(F32)
            x_turned_psum = ahead_psum.tile([P, WORD_BLOCKS, P], F32, name="turn")
            for k in range(WORD_BLOCKS):
                nc.tensor.transpose(x_turned_psum[:, k, :], x_words[:, k * P : (k + 1) * P], identity[:])
            x_turned = work.tile([P, WORD_BLOCKS, P], F32, name="x_turned")
            nc.scalar.copy(out=x_turned[:], in_=x_turned_psum[:])
            x_pairs = x_turned[:].bitcast(BF16)
            crossed = ahead_psum.tile([P, ROW_GROUPS, PAIRED], F32, name="crossed", bufs=2)
            blocks_per_half = WORD_BLOCKS // HALVES

            def turn(k):
                h, q = divmod(k, blocks_per_half)
                s = HALVES_AHEAD.index((i, h))
                g_words = halves_fetched[s][:].bitcast(F32)
                g_turned = work.tile([P, ROW_GROUPS, T, ROW_GROUP], F32, name="g_turned")
                for first in range(0, T, BLOCKS_PER_BANK):
                    g_turned_psum = ahead_psum.tile([P, BLOCKS_PER_BANK, P], F32, name="turn")
                    for t in range(BLOCKS_PER_BANK):
                        nc.tensor.transpose(
                            g_turned_psum[:, t, :], g_words[:, first + t, q * P : (q + 1) * P], identity[:]
                        )
                    nc.scalar.copy(
                        out=g_turned[:, :, first : first + BLOCKS_PER_BANK, :],
                        in_=g_turned_psum[:].rearrange("p t (u r) -> p u t r", r=ROW_GROUP),
                    )
                if q == blocks_per_half - 1:
                    fetch_half(s + 2)
                return g_turned[:].bitcast(BF16)

            g_pairs = turn(0)
            for k in range(WORD_BLOCKS):
                following = turn(k + 1) if k + 1 < WORD_BLOCKS else None
                for u in range(ROW_GROUPS):
                    nc.tensor.matmul(
                        out=crossed[:, u, :],
                        lhsT=g_pairs[:, u].rearrange("p t s -> p (t s)"),
                        rhs=x_pairs[:, k, u * PAIRED : (u + 1) * PAIRED],
                        start=(k == 0 and u == 0),
                        stop=(k == WORD_BLOCKS - 1 and u == ROW_GROUPS - 1),
                    )
                g_pairs = following
            own_row = work.tile([P, WORD, ROW_GROUPS, ROW_GROUP], F32, name="own_row")
            nc.vector.tensor_tensor(
                out=own_row[:],
                in0=crossed[:].rearrange("p u (r e) -> p e u r", e=WORD),
                in1=same_pair[:]
                .rearrange("p (r e) -> p e r", e=WORD)
                .unsqueeze(2)
                .to_broadcast([P, WORD, ROW_GROUPS, ROW_GROUP]),
                op=MUL,
            )
            by_row = ahead_psum.tile([P, T], F32, name="turn")
            for e in range(WORD):
                nc.tensor.matmul(
                    out=by_row[:],
                    lhsT=own_row[:, e].rearrange("p u r -> p (u r)"),
                    rhs=same_horizon[:],
                    start=(e == 0),
                    stop=(e == WORD - 1),
                )
            nc.scalar.copy(out=dots[:, i, 0, :], in_=by_row[:])

        def coefficients(chain):
            def col(name):
                return chain.tile([P, 1], F32, name=name)

            def row(name):
                return chain.tile([P, TILES], F32, name=name)

            def row2(name):
                return chain.tile([P, 2, TILES], F32, name=name)

            def grid(name):
                return chain.tile([P, TILES, T], F32, name=name)

            def pair(r):
                return r.unsqueeze(1).to_broadcast([P, 2, TILES])

            def over_t(r):
                return r.unsqueeze(2).to_broadcast([P, TILES, T])

            def over_tiles(h):
                return h.unsqueeze(1).to_broadcast([P, TILES, T])


            clipped = row("clipped")
            nc.vector.tensor_scalar(
                out=clipped,
                in0=vn_row,
                scalar1=-CLIP,
                scalar2=CLIP,
                op0=mybir.AluOpType.max,
                op1=mybir.AluOpType.min,
            )
            ivn = inverse(row("ivn"), vn_row)

            one_minus = affine(row("one_minus"), clipped, -1.0, 1.0)

            inv_one_minus = inverse(row("inv_one_minus"), one_minus)

            ratio = fused(row("ratio"), clipped, 1.0, inv_one_minus, ADD, MUL)
            ln_ratio = table(row("ln_ratio"), ratio, ACT.Ln)

            bb = col("bb")
            m2, mb, x2 = row("m2"), row("mb"), row("x2")
            square_sum(bb, b_all[:])
            for i in range(TILES):
                square_sum(m2[:, i : i + 1], mv_all[:, i, :])
                dot(mb[:, i : i + 1], mv_all[:, i, :], b_all[:], N)
            for spare in range(2):
                ready_dot()

            m2_c = at_least(row("m2_c"), m2, EPS_SQ)
            bb_c = at_least(col("bb_c"), bb, EPS_SQ)
            free_m = above(row("free_m"), m2, EPS_SQ)
            k1 = fused(row("k1"), ln_ratio, 0.5, ivn, MUL, MUL)
            rm = table(row("rm"), m2_c, ACT.Sqrt)
            rb = table(col("rb"), bb_c, ACT.Sqrt)
            ready_dot()
            ready_dot()

            k1_rm = mul(row("k1_rm"), k1, rm)
            irm = inverse(row("irm"), rm)
            irb = inverse(col("irb"), rb)
            hm = table(row("hm"), k1_rm, ACT.Tanh)
            hb = table(col("hb"), rb, ACT.Tanh)
            half_tanh = table(col("half_tanh"), logit, ACT.Tanh, 0.5)
            for i in range(TILES):
                square_sum(x2[:, i : i + 1], x_all[:, i, :])
            ready_dot()
            ready_dot()
            v_rows = grads.tile([P, PASSES, PACK, K], BF16, name="g")
            nc.sync.dma_start(out=v_rows[:].rearrange("p c j k -> p c (j k)"), in_=v_view)
            v_halves = regroup_pass(v_rows[:, 0], nc.scalar.copy)

            alpha = mul(row("alpha"), hm, irm)
            beta = mul(col("beta"), hb, irb)
            step = affine(col("step"), half_tanh, 0.5, 0.5)
            ready_dot()

            alpha_m2 = mul(row("alpha_m2"), alpha, m2)
            alpha_mb = mul(row("alpha_mb"), alpha, mb)
            beta2 = scale(col("beta2"), beta, 2.0)
            beta_bb = mul(col("beta_bb"), beta, bb)
            ct = scale(chain.tile([P, T], F32, name="ct"), horizon, step)
            ready_dot()

            res2 = mul(row("res2"), alpha_m2, alpha)
            res_b2 = scale(row("res_b2"), alpha_mb, beta2)
            y2 = mul(col("y2"), beta_bb, beta)
            ct2 = mul(chain.tile([P, T], F32, name="ct2"), ct, ct)
            ready_dot()

            base = shift(row("base"), res_b2, 1.0)
            a2 = affine(row("a2"), res2, -1.0, 1.0)
            ct3 = mul(chain.tile([P, T], F32, name="ct3"), ct2, ct)
            ready_dot()

            quantise_pass(v_halves, v_codes[:, 0, :], v_scales[:, 0, :], E4M3_X4)
            v_halves = regroup_pass(v_rows[:, 1], nc.scalar.copy)

            den0 = fused(row("den0"), res2, y2, base, MUL, ADD)
            a1 = shift(row("a1"), base, y2)
            ready_dot()

            den = at_least(row("den"), den0, EPS)
            live = above(row("live"), den0, EPS)
            ready_dot()

            iden = inverse(row("iden"), den)
            ready_dot()

            p1 = mul(row("p1"), a1, iden)
            p2 = mul(row("p2"), a2, iden)
            ready_dot()

            pa = mul(row("pa"), p1, alpha)
            pb = scale(row("pb"), p2, beta)
            ready_dot()

            quantise_pass(v_halves, v_codes[:, 1, :], v_scales[:, 1, :], E4M3_X4)

            pa_m2 = mul(row("pa_m2"), pa, m2)
            pb_mb = mul(row("pb_mb"), pb, mb)
            pa_mb = mul(row("pa_mb"), pa, mb)
            ready_dot()

            p_mv = add(row("p_mv"), pa_m2, pb_mb)
            p_b = fused(row("p_b"), pb, bb, pa_mb, MUL, ADD)
            ready_dot()

            pa_pmv = mul(row("pa_pmv"), pa, p_mv)
            pb_pb = mul(row("pb_pb"), pb, p_b)
            gap = affine(row("gap"), x2, -1.0, 1.0)
            ready_dot()

            pp = add(row("pp"), pa_pmv, pb_pb)
            gap_c = at_least(row("gap_c"), gap, EPS)
            ready_dot()

            pp_c = at_least(row("pp_c"), pp, TINY)
            on_p = above(row("on_p"), pp, MAX_NORM * MAX_NORM)
            k2 = inverse(row("k2"), gap_c)
            rp_raw = table(row("rp_raw"), pp_c, ACT.Sqrt)
            while ready_issued[0] < 2 * TILES:
                ready_dot()

            rp = at_least(row("rp"), rp_raw, EPS)

            irp = inverse(row("irp"), rp)

            shrink = fused(row("shrink"), irp, MAX_NORM, on_p, MUL, MUL)
            irp2 = mul(row("irp2"), irp, irp)

            pi = fused(row("pi"), shrink, 1.0, on_p, ADD, SUB)
            phi = mul(row("phi"), shrink, irp2)

            mul(mu, pi, pa)
            mul(nu, pi, pb)
            r0 = mul(row("r0"), pi, rp_raw)
            pi_sq = mul(row("pi_sq"), pi, pi)

            c_r0 = mul(grid("c_r0"), over_t(r0), over_tiles(ct))
            vv = mul(row("vv"), pi_sq, pp)
            mu_xm = mul(row("mu_xm"), mu, xm)
            nu_xb = mul(row("nu_xb"), nu, xb)
            imu = inverse(row("imu"), mu)

            rt = at_least(grid("rt"), c_r0, EPS)
            free_t = above(grid("free_t"), c_r0, EPS)
            xv = add(row("xv"), mu_xm, nu_xb)
            mul(nu_over_mu, nu, imu)

            k2_rt = mul(grid("k2_rt"), rt, over_t(k2))
            irt = inverse(grid("irt"), rt)
            ht = table(grid("ht"), k2_rt, ACT.Tanh)
            ready_dot()
            ready_dot()

            sigma = mul(grid("sigma"), ht, irt)

            s = mul(grid("s"), sigma, over_tiles(ct))

            x_sec = mul(grid("x_sec"), s, over_t(xv))
            s_vv = mul(grid("s_vv"), s, over_t(vv))

            base_t = affine(grid("base_t"), x_sec, 2.0, 1.0)
            sec2 = mul(grid("sec2"), s_vv, s)

            x2_sec2 = mul(grid("x2_sec2"), sec2, over_t(x2))
            b1 = add(grid("b1"), base_t, sec2)

            den0_t = add(grid("den0_t"), x2_sec2, base_t)

            den_t = at_least(grid("den_t"), den0_t, EPS)
            live_t = above(grid("live_t"), den0_t, EPS)

            iden_t = inverse(grid("iden_t"), den_t)

            q1 = mul(grid("q1"), b1, iden_t)
            q2 = mul(grid("q2"), iden_t, over_t(gap))

            q2s = mul(grid("q2s"), q2, s)
            q1_x2 = mul(grid("q1_x2"), q1, over_t(x2))
            q2_xsec = mul(grid("q2_xsec"), q2, x_sec)
            q1_xv = mul(grid("q1_xv"), q1, over_t(xv))

            q_x = add(grid("q_x"), q1_x2, q2_xsec)
            q2s_vv = mul(grid("q2s_vv"), q2s, over_t(vv))

            q_v = add(grid("q_v"), q1_xv, q2s_vv)
            q1_qx = mul(grid("q1_qx"), q1, q_x)

            q2s_qv = mul(grid("q2s_qv"), q2s, q_v)

            qq = add(grid("qq"), q1_qx, q2s_qv)

            qq_c = at_least(grid("qq_c"), qq, EPS_SQ)
            on_q = above(grid("on_q"), qq, MAX_NORM * MAX_NORM)
            rq = table(grid("rq"), qq_c, ACT.Sqrt)
            ready_dot()
            ready_dot()

            irq = inverse(grid("irq"), rq)

            shrink_q = fused(grid("shrink_q"), irq, MAX_NORM, on_q, MUL, MUL)
            irq2 = mul(grid("irq2"), irq, irq)

            pi_q = fused(grid("pi_q"), shrink_q, 1.0, on_q, ADD, SUB)
            phi_q = mul(grid("phi_q"), shrink_q, irq2)

            a_t = mul(from_dots[:, 2, 1], q2s, pi_q)
            nc.vector.memset(from_dots[:, 2, 0], 0.0)

            mul(a_scaled[:], a_t, over_t(mu))

            phi_qq = mul(grid("phi_qq"), phi_q, qq)
            phi_qx = mul(grid("phi_qx"), phi_q, q_x)
            q2_phi = mul(grid("q2_phi"), q2, phi_q)
            iden_pi = mul(grid("iden_pi"), iden_t, pi_q)
            ht2 = mul(grid("ht2"), ht, ht)
            irt2 = mul(grid("irt2"), irt, irt)
            xv_svv = add(grid("xv_svv"), s_vv, over_t(xv))
            q2_pi = mul(grid("q2_pi"), q2, pi_q)

            keep_q = sub(grid("keep_q"), pi_q, phi_qq)
            lost_x = mul(grid("lost_x"), q2_phi, q1)
            lost_v = mul(grid("lost_v"), q2_phi, q2s)
            lost_qv = mul(grid("lost_qv"), q2_phi, q_v)
            s_iden_pi = mul(grid("s_iden_pi"), s, iden_pi)
            slope_t = affine(grid("slope_t"), ht2, -1.0, 1.0)
            irt3 = mul(grid("irt3"), irt2, irt)

            live_keep = mul(grid("live_keep"), live_t, keep_q)
            slope_kr = mul(grid("slope_kr"), slope_t, k2_rt)
            free_irt3 = mul(grid("free_irt3"), irt3, free_t)
            iden_pi_sum = mul(grid("iden_pi_sum"), iden_pi, xv_svv)
            ss_iden_pi = mul(grid("ss_iden_pi"), s, s_iden_pi)

            on_x_sum = add(grid("on_x_sum"), phi_qx, live_keep)
            x2_live_keep = mul(grid("x2_live_keep"), live_keep, over_t(x2))
            top_t = sub(grid("top_t"), slope_kr, ht)
            free_c3 = mul(grid("free_c3"), free_irt3, over_tiles(ct3))

            on_x = mul(grid("on_x"), iden_t, on_x_sum)
            on_sec_sum = add(grid("on_sec_sum"), phi_qx, x2_live_keep)
            coef_c3 = mul(grid("coef_c3"), top_t, free_c3)

            on_sec = mul(grid("on_sec"), iden_t, on_sec_sum)
            x_c_half = fused(grid("x_c_half"), on_x, 2.0, lost_x, MUL, ADD)
            on_x_xv = mul(grid("on_x_xv"), on_x, over_t(xv))
            v_b = mul(grid("v_b"), coef_c3, q2_pi)
            coef_a = mul(grid("coef_a"), coef_c3, iden_pi_sum)

            s_on_sec = mul(grid("s_on_sec"), s, on_sec)
            x_c = fused(grid("x_c"), x_c_half, -1.0, s, MUL, MUL)
            v_a_half = add(grid("v_a_half"), ss_iden_pi, coef_a)

            v_c_first = fused(grid("v_c_first"), s_on_sec, 2.0, lost_v, MUL, ADD)
            s_on_sec_vv = mul(grid("s_on_sec_vv"), s_on_sec, over_t(vv))
            x_c_q1 = mul(grid("x_c_q1"), x_c, q1)
            mul(from_dots[:, 0, 1], x_c, q2s)

            s_v_c_first = mul(grid("s_v_c_first"), s, v_c_first)
            ds_v_c_half = add(grid("ds_v_c_half"), on_x_xv, s_on_sec_vv)
            fused(from_dots[:, 0, 0], s_iden_pi, 2.0, x_c_q1, MUL, ADD)

            ds_v_c = fused(grid("ds_v_c"), ds_v_c_half, 2.0, lost_qv, MUL, ADD)

            phi_pp = mul(row("phi_pp"), phi, pp)
            iden_alpha = mul(row("iden_alpha"), iden, alpha)
            iden_beta = scale(row("iden_beta"), iden, beta)
            phi_pmv = mul(row("phi_pmv"), phi, p_mv)
            phi_pb = mul(row("phi_pb"), phi, p_b)

            coef_ds_v_c = mul(grid("coef_ds_v_c"), coef_c3, ds_v_c)
            beta2_mb = scale(row("beta2_mb"), mb, beta2)
            alpha2_m2 = scale(row("alpha2_m2"), alpha_m2, 2.0)
            hm2 = mul(row("hm2"), hm, hm)
            irm2 = mul(row("irm2"), irm, irm)

            v_c = fused(grid("v_c"), s_v_c_first, -1.0, coef_ds_v_c, MUL, SUB)
            lost = mul(row("lost"), pa, phi)
            alpha_sq2 = fused(row("alpha_sq2"), alpha, 2.0, alpha, MUL, MUL)
            alpha_beta2 = scale(row("alpha_beta2"), alpha, beta2)

            v_c_q1 = mul(grid("v_c_q1"), v_c, q1)
            v_c_q2s = mul(grid("v_c_q2s"), v_c, q2s)
            keep_p = sub(row("keep_p"), pi, phi_pp)
            a_first = mul(row("a_first"), iden_alpha, pi)
            b_first = mul(row("b_first"), iden_beta, pi)

            fused(from_dots[:, 1, 0], v_a_half, 2.0, v_c_q1, MUL, ADD)
            add(from_dots[:, 1, 1], v_c_q2s, v_b)
            alpha_phi_pmv = mul(row("alpha_phi_pmv"), alpha, phi_pmv)
            beta_phi_pb = scale(row("beta_phi_pb"), phi_pb, beta)
            slope_m = affine(row("slope_m"), hm2, -1.0, 1.0)
            irm3 = mul(row("irm3"), irm2, irm)

            live_keep_p = mul(row("live_keep_p"), live, keep_p)
            lost_pa = mul(row("lost_pa"), lost, pa)
            lost_pb = mul(row("lost_pb"), lost, pb)
            p1_phi_pmv = mul(row("p1_phi_pmv"), p1, phi_pmv)
            p1_pi = mul(row("p1_pi"), p1, pi)

            to_b_sum = add(row("to_b_sum"), alpha_phi_pmv, live_keep_p)
            y2_live_keep_p = scale(row("y2_live_keep_p"), live_keep_p, y2)
            slope_km = mul(row("slope_km"), slope_m, k1_rm)
            free_irm3 = mul(row("free_irm3"), irm3, free_m)
            mb_a_first = mul(row("mb_a_first"), beta2_mb, a_first)
            m2_b_first = mul(row("m2_b_first"), alpha2_m2, b_first)

            to_b_c = mul(row("to_b_c"), iden, to_b_sum)
            to_res_sum = sub(row("to_res_sum"), y2_live_keep_p, beta_phi_pb)
            top_m = sub(row("top_m"), slope_km, hm)
            on_b_a = mul(row("on_b_a"), alpha_beta2, a_first)
            sq_b_first = mul(row("sq_b_first"), alpha_sq2, b_first)
            dres_a = add(row("dres_a"), p1_pi, mb_a_first)

            to_res_c = mul(row("to_res_c"), iden, to_res_sum)
            coef_m = mul(row("coef_m"), top_m, free_irm3)
            mb_to_b_c = mul(row("mb_to_b_c"), beta2_mb, to_b_c)
            ab_to_b_c = mul(row("ab_to_b_c"), alpha_beta2, to_b_c)

            m2_to_res_c = mul(row("m2_to_res_c"), alpha2_m2, to_res_c)
            sq_to_res_c = mul(row("sq_to_res_c"), alpha_sq2, to_res_c)
            dres_c_part = add(row("dres_c_part"), p1_phi_pmv, mb_to_b_c)
            on_b_c = add(row("on_b_c"), ab_to_b_c, lost_pb)
            on_mv_a = mul(row("on_mv_a"), coef_m, dres_a)
            coef_dres_b = mul(row("coef_dres_b"), coef_m, m2_b_first)

            dres_c = add(row("dres_c"), dres_c_part, m2_to_res_c)
            on_mv_c_part = add(row("on_mv_c_part"), sq_to_res_c, lost_pa)
            on_mv_b = add(row("on_mv_b"), coef_dres_b, sq_b_first)
            on_b_c_pa = mul(row("on_b_c_pa"), on_b_c, pa)

            coef_dres_c = mul(row("coef_dres_c"), coef_m, dres_c)
            on_both = chain.tile([P, 2, 2, TILES], F32, name="on_both")
            sub(on_both[:, 1, 0, :], on_b_a, on_b_c_pa)
            fused(on_both[:, 1, 1, :], on_b_c, -1.0, pb, MUL, MUL)
            mu_mb = mul(row("mu_mb"), mu, mb)
            nu_bb = scale(row("nu_bb"), nu, bb)

            on_mv_c = add(row("on_mv_c"), coef_dres_c, on_mv_c_part)
            vb = add(row("vb"), mu_mb, nu_bb)
            nc.vector.memset(to_kappa[:], 0.0)

            on_mv_c_pa = mul(row("on_mv_c_pa"), on_mv_c, pa)
            on_mv_c_pb = mul(row("on_mv_c_pb"), on_mv_c, pb)
            nc.vector.tensor_copy(out=to_kappa[:, :, 0, 0], in_=mu)

            sub(on_both[:, 0, 0, :], on_mv_a, on_mv_c_pa)
            fused(on_both[:, 0, 1, :], on_mv_c_pb, -1.0, on_mv_b, MUL, SUB)

            in_v0_b = chain.tile([P, 2, 2, TILES], F32, name="in_v0_b")
            mul(in_v0_b[:, :, 0, :], on_both[:, :, 0, :], pair(imu))

            nu_first = mul(row2("nu_first"), in_v0_b[:, :, 0, :], pair(nu))

            sub(in_v0_b[:, :, 1, :], on_both[:, :, 1, :], nu_first)

            weights = chain.tile([P, 2, 2, TILES], F32, name="weights")
            mul(weights[:, 0], in_v0_b[:, 0], pair(imu))

            nu_on_v0 = mul(row2("nu_on_v0"), weights[:, 0], pair(nu))

            sub(weights[:, 1], in_v0_b[:, 1], nu_on_v0)

            def kappa_column(m):
                return to_kappa[:, :, 1:3, m].rearrange("p i k -> p k i")

            w_v0, w_b = weights[:, :, 0, :], weights[:, :, 1, :]
            kx_a = mul(row2("kx_a"), w_v0, pair(xv))
            kx_b = mul(row2("kx_b"), w_b, pair(xb))
            kv_a = mul(row2("kv_a"), w_v0, pair(vv))
            kv_b = mul(row2("kv_b"), w_b, pair(vb))
            nc.vector.tensor_copy(out=kappa_column(2), in_=w_v0)
            mul(kappa_column(3), w_b, pair(imu))

            add(kappa_column(0), kx_a, kx_b)
            add(kappa_column(1), kv_a, kv_b)

            add(to_kappa[:, :, 1, 1], to_kappa[:, :, 1, 1], mu)
            mul(from_dots[:, :, 1], from_dots[:, :, 1], mu[:].unsqueeze(1).unsqueeze(3).to_broadcast([P, 3, TILES, T]))

            mul(to_kappa[:, :, 1, :], to_kappa[:, :, 1, :], mu[:].unsqueeze(2).to_broadcast([P, TILES, 4]))

        with tc.psum_pool(name="ahead_psum", bufs=4) as ahead_psum:
            with tc.tile_pool(name="early", bufs=2) as early:
                for s in range(2):
                    fetch_half(s)
                b_f32 = work.tile([P, N], F32, name="scaled", bufs=4)
                nc.vector.tensor_copy(out=b_f32[:], in_=b_all[:])
                b_turned = [ahead_psum.tile([P, BANK], F32, name="turn") for h in range(HALVES)]
                add_turned(b_turned, [b_f32], True, True)
                for h in range(HALVES):
                    nc.scalar.copy(
                        out=b_cols[:, h * BLOCKS_PER_BANK : (h + 1) * BLOCKS_PER_BANK, :],
                        in_=b_turned[h][:].rearrange("p (q r) -> p q r", r=P)[:, :, :B_COPIES],
                    )
                with tc.tile_pool(name="chain", bufs=1) as chain:
                    coefficients(chain)
                for i in range(VECTOR_X_TILES, TILES):
                    x_dots_on_tensor(i)
        post = ctx.enter_context(tc.tile_pool(name="post", bufs=2))
        psum = ctx.enter_context(tc.psum_pool(name="psum", bufs=8))

        turned_sums = {}
        turned_back = []
        d_rows = {}

        def weighted_sum(i):
            w = mv_all[:, i, :]
            fused(w, b_all[:], nu_over_mu[:, i : i + 1], w, MUL, ADD)
            while ready_issued[0] < 2 * TILES + min(i + 1, VECTOR_X_TILES) * T:
                ready_dot()
            total = banks()
            for t in range(T):
                on_vector = t % 2 == 0 and t // 2 < VECTOR_TERMS
                term = times_row_factor(g_tiles[i][:, t, :], a_scaled[:, i, t : t + 1], on_vector)
                add_turned(total, [term], t == 0, t == T - 1)
            return total

        sums_b = {}

        def sum_against_b(i, total):
            if i < len(first_sums):
                turned_sums[i] = first_sums[i]
            else:
                turned_sums[i] = post.tile([P, N], F32, name="turned_sum", bufs=3)
            out_of_psum(turned_sums[i], total)
            sums_b[i] = psum.tile([P, BANK], F32, name="bank")
            for k in range(BLOCKS):
                nc.tensor.matmul(
                    out=sums_b[i][:, :B_COPIES],
                    lhsT=turned_sums[i][:, k * P : (k + 1) * P],
                    rhs=b_cols[:, k, :],
                    start=(k == 0),
                    stop=(k == BLOCKS - 1),
                )
            if i == TILES - 1:
                turned_back.extend(banks())
                add_turned(turned_back, [turned_sums[i]], True, True)

        def sum_against_b_out(i):
            nc.scalar.copy(out=inputs[:, i, 3:4], in_=sums_b[i][:, 0:1])

        def inner_products(i):
            for t in range(T):
                dot(dots[:, i, 1, t : t + 1], g_tiles[i][:, t, :], mv_all[:, i, :], N)
            ready_dot()
            terms = work.tile([P, 3, 2, T], F32, name="terms")
            mul(terms[:], from_dots[:, :, :, i, :], dots[:, i].unsqueeze(1).to_broadcast([P, 3, 2, T]))
            ready_dot()
            nc.vector.tensor_reduce(
                out=inputs[:, i, 0:3], in_=terms[:], axis=mybir.AxisListType.XY, op=ADD
            )
            ready_dot()
            kappa_terms = work.tile([P, 3, 4], F32, name="kappa_terms")
            mul(kappa_terms[:], to_kappa[:, i], inputs[:, i].unsqueeze(1).to_broadcast([P, 3, 4]))
            ready_dot()
            nc.vector.tensor_reduce(
                out=kappa[:, i, :], in_=kappa_terms[:], axis=mybir.AxisListType.X, op=ADD
            )

        mixes = {}

        def begin_finish(i):
            mixes[i] = banks()
            for k, src in enumerate((x_all[:, i, :], mv_all[:, i, :])):
                add_turned(mixes[i], [times_row_factor(src, kappa[:, i, k : k + 1])], k == 0, k == 1)

        turned_mixes = {}

        def mix_out(i):
            turned_mixes[i] = post.tile([P, N], F32, name="turned_mix")
            out_of_psum(turned_mixes[i], mixes.pop(i))

        def finish(i):
            dmv = banks()
            add_turned(dmv, [turned_sums[i], turned_mixes.pop(i)], True, True)
            for h in range(HALVES):
                half = slice(h * BANK, (h + 1) * BANK)
                fused(d_rows[i // PACK][:, i % PACK, half], b_all[:, half], kappa[:, i, 2:3], dmv[h][:], MUL, ADD)

        first_pair = stage.tile([P, 2, N], F32, name="rows")
        first_sums = [first_pair[:, i, :] for i in range(2)]

        for i in range(TILES + 1):
            load_g(i)
            load_g(i + 1)
            if i < TILES:
                if i % PACK == 0:
                    d_rows[i // PACK] = stage.tile([P, PACK, N], BF16, name="rows")
                total = weighted_sum(i)
            if 0 < i < TILES:
                begin_finish(i - 1)
            if i < TILES:
                sum_against_b(i, total)
            if 0 < i < TILES:
                mix_out(i - 1)
            if i < TILES:
                sum_against_b_out(i)
            if 0 < i < TILES:
                finish(i - 1)
            if i % PACK == 2 and i > PACK:
                d_halves = regroup_pass(d_rows[i // PACK - 1][:], nc.scalar.copy)
            if i < TILES:
                inner_products(i)
            if i % PACK == 2 and i > PACK:
                c = i // PACK - 1
                quantise_pass(d_halves, d_codes[:, c, :], d_scales[:, c, :], E5M2_X4)

        groups = [(m, h) for m in range(BLOCKS) for h in range(K // BANK)]
        WAVE = 8
        accs = {}
        results = {}

        def product(m, h, c):
            of_block = slice(m * P, (m + 1) * P)
            half = slice(h * BANK, (h + 1) * BANK)
            nc.tensor.matmul_mx(
                out=accs[(m, h)][:],
                lhsT=d_codes[:, c, of_block].bitcast(E5M2_X4),
                lhsT_scale=d_scales[:, c, of_block],
                rhs=v_codes[:, c, half].bitcast(E4M3_X4),
                rhs_scale=v_scales[:, c, half],
                start=(c == 0),
                stop=(c == PASSES - 1),
            )

        def all_but_the_last_pass(wave):
            for m, h in wave:
                accs[(m, h)] = psum.tile([P, BANK], F32, name="bank")
                for c in range(PASSES - 1):
                    product(m, h, c)

        def last_pass(wave):
            for m, h in wave:
                product(m, h, PASSES - 1)
                if h == 0:
                    results[m] = work.tile([P, K], F32, name="scaled", bufs=4)
                copy = nc.scalar.copy if h % 2 == 0 else nc.vector.tensor_copy
                half = slice(h * BANK, (h + 1) * BANK)
                copy(out=results[m][:, half], in_=accs[(m, h)][:])
                nc.sync.dma_start(out=out[m * P : (m + 1) * P, half], in_=results[m][:, half])

        all_but_the_last_pass(groups[:WAVE])

        QUARTER = N // 4
        last = TILES - 1
        last_rows = d_rows[PASSES - 1]
        for pair in range(0, N // QUARTER, 2):
            both = (pair, pair + 1)
            columns = {q: slice(q * QUARTER, (q + 1) * QUARTER) for q in both}
            with_x, with_v, grouped = {}, {}, {}
            for q in both:
                with_x[q] = post.tile([P, QUARTER], F32, name="with_x")
                in_bank = slice((q * QUARTER) % BANK, (q * QUARTER) % BANK + QUARTER)
                fused(
                    with_x[q][:],
                    x_all[:, last, columns[q]],
                    kappa[:, last, 0:1],
                    turned_back[q * QUARTER // BANK][:, in_bank],
                    MUL,
                    ADD,
                )
            for q in both:
                with_v[q] = post.tile([P, QUARTER], F32, name="with_v")
                fused(with_v[q][:], mv_all[:, last, columns[q]], kappa[:, last, 1:2], with_x[q][:], MUL, ADD)
            for q in both:
                fused(
                    last_rows[:, last % PACK, columns[q]], b_all[:, columns[q]], kappa[:, last, 2:3], with_v[q][:], MUL, ADD
                )
            for q in both:
                grouped[q] = stage.tile([P, QUARTER, PACK], BF16, name="grouped", align_bytes=64)
                copy = nc.vector.tensor_copy if q == pair else nc.scalar.copy
                copy(
                    out=grouped[q][:].rearrange("p (c r) j -> p c j r", r=4),
                    in_=last_rows[:, :, columns[q]].rearrange("p j (c r) -> p c j r", r=4),
                )
            for q in both:
                nc.vector.quantize_mx(
                    out=d_codes[:, PASSES - 1, columns[q]].bitcast(E5M2_X4),
                    scales=d_scales[:, PASSES - 1, columns[q]],
                    in_=grouped[q][:].rearrange("p n j -> p (n j)"),
                )

        for first in range(0, len(groups), WAVE):
            if first > 0:
                all_but_the_last_pass(groups[first : first + WAVE])
            last_pass(groups[first : first + WAVE])
